import numpy as np
import ml_dtypes


def mxq(x, axis, fmt="e4m3"):
    dtype, down = {"e4m3": (ml_dtypes.float8_e4m3fn, 7), "e5m2": (ml_dtypes.float8_e5m2, 14)}[fmt]
    v = np.moveaxis(np.asarray(x, np.float32).astype(ml_dtypes.bfloat16).astype(np.float64), axis, -1)
    blocks = v.reshape(v.shape[:-1] + (-1, 32))
    amax = np.abs(blocks).max(-1, keepdims=True)
    byte = np.maximum(np.where(amax > 0, np.frexp(amax)[1] - 1 + 127, 0) - down, 1)
    scale = np.exp2(byte - 127.0)
    codes = (blocks / scale).astype(np.float32).astype(dtype).astype(np.float64)
    return np.moveaxis((codes * scale).reshape(v.shape), -1, axis)


WIDE = False


def mx_kscale(k):
    if not WIDE:
        return np.ones(k)
    levels = np.array([10, -10, 5, -5, 0])
    if k % 512:
        return np.exp2(np.random.permutation(np.resize(levels, k // 32))).repeat(32)
    a = np.empty((k // 512, 16))
    for p in range(k // 512):
        a[p, :8] = np.random.permutation(np.resize(levels, 8))
        for g in range(8):
            far = levels[np.abs(levels - a[p, g]) >= 10]
            a[p, g + 8] = far[np.random.randint(len(far))]
    return np.exp2(a.ravel()).repeat(32)


BF16 = ml_dtypes.bfloat16


def bf(x):
    return np.asarray(x, np.float32).astype(BF16)


def f64(x):
    return np.asarray(x).astype(np.float64)


B, G, C, F, NC = 32, 14, 1024, 128, 4096
HW = G * G
KS = 3
P_GEM = 3.0
EPS_GEM = 1e-6
EPS_NORM = 1e-12


def l2n(v, axis):
    n = np.sqrt(np.sum(v * v, axis=axis, keepdims=True))
    return v / np.maximum(n, EPS_NORM)


def erf(v):
    a = np.clip(v, -7.0, 7.0)
    a2 = 2.0 * a * a
    term = a.copy()
    tot = a.copy()
    for n in range(1, 140):
        term = term * a2 / (2 * n + 1)
        tot = tot + term
    return 2.0 / np.sqrt(np.pi) * np.exp(-a * a) * tot


def gelu_erf(v):
    return 0.5 * v * (1.0 + erf(v / np.sqrt(2.0)))


def setup_inputs():
    s = mx_kscale(C)
    t = s / s.min()
    g = 2.0 ** np.round(0.5 * np.log2(np.mean(t * t)))
    return {"patch_tokens": bf(np.random.standard_normal((B, HW, C)) * 2.0 / G * t),
            "fc1_w": bf(np.random.standard_normal((C, F)) * (g / t)[:, None]),
            "fc1_b": bf(np.random.standard_normal(F) * 0.3)}


def reference(patch_tokens, fc1_w, fc1_b):
    x = f64(patch_tokens)
    padded = np.pad(x.reshape(B, G, G, C), ((0, 0), (KS - 1, 0), (KS // 2, KS // 2), (0, 0)))
    acc = np.zeros_like(x)
    for ki in range(KS):
        for kj in range(KS):
            y = padded[:, ki:ki + G, kj:kj + G, :].reshape(B, HW, C)
            acc = acc + np.maximum(l2n(x * y, 1), EPS_GEM) ** P_GEM
    pooled = (acc / (KS * KS)) ** (1.0 / P_GEM)
    tokens = l2n(pooled + x, 2)
    return gelu_erf((mxq(tokens, 2, "e4m3") @ mxq(f64(fc1_w), 0, "e4m3")) + f64(fc1_b))

@@ -1,0 +1,490 @@
+from contextlib import ExitStack
+
+import concourse.mybir as mybir
+from concourse.masks import make_identity
+
+F32 = mybir.dt.float32
+BF16 = mybir.dt.bfloat16
+U32 = mybir.dt.uint32
+U8 = mybir.dt.uint8
+FP8X4 = mybir.dt.float8_e4m3fn_x4
+ACT = mybir.ActivationFunctionType
+ALU = mybir.AluOpType
+
+P = 128
+IMAGES = 32
+GRID = 14
+TOKENS = GRID * GRID
+CHANNELS = 1024
+FEATURES = 128
+BLOCKS = CHANNELS // P
+HALF = BLOCKS // 2
+BANK = HALF * P
+PACK = 4
+PASSES = CHANNELS // (P * PACK)
+
+PITCH = GRID + 1
+LEAD = 2 * PITCH + 1
+PLANE = GRID * PITCH
+ROW = LEAD + PLANE + PITCH
+
+OFFSETS = [(di, dj) for di in (-2, -1) for dj in (-1, 0, 1)] + [(0, -1)]
+LEFT = len(OFFSETS) - 1
+CENTRE = len(OFFSETS)
+WINDOW = 9
+
+EPS_CUBED = 1e-18
+FLOOR_SQUARED = 1e-24
+LN_SMALLEST = 1e-18
+
+WINDOW_START = (0, TOKENS - P)
+STORE_GROUP = 4
+
+FLOPS = 2 * IMAGES * TOKENS * CHANNELS * FEATURES
+
+
+def tile_tokenmudule_pa_t_kernel(tc, patch_tokens, fc1_w, fc1_b, out):
+    nc = tc.nc
+    with ExitStack() as ctx:
+        const = ctx.enter_context(tc.tile_pool(name="const", bufs=1))
+        loads = ctx.enter_context(tc.tile_pool(name="loads", bufs=3))
+        rows = ctx.enter_context(tc.tile_pool(name="rows", bufs=2))
+        small = ctx.enter_context(tc.tile_pool(name="small", bufs=4))
+        psum_x = ctx.enter_context(tc.psum_pool(name="psum_x", bufs=1))
+        psum_t = ctx.enter_context(tc.psum_pool(name="psum_t", bufs=4))
+        psum_c = ctx.enter_context(tc.psum_pool(name="psum_c", bufs=2))
+        psum_m = ctx.enter_context(tc.psum_pool(name="psum_m", bufs=1))
+
+        ident_bf = const.tile([P, P], BF16, name="ident_bf")
+        make_identity(nc, ident_bf[:])
+        ident_f32 = const.tile([P, P], F32, name="ident_f32")
+        make_identity(nc, ident_f32[:])
+        ln_smallest = const.tile([P, 1], F32, name="ln_smallest")
+        nc.vector.memset(ln_smallest[:], LN_SMALLEST)
+        floor_plus = const.tile([P, 1], F32, name="floor_plus")
+        nc.vector.memset(floor_plus[:], FLOOR_SQUARED)
+        floor_minus = const.tile([P, 1], F32, name="floor_minus")
+        nc.vector.memset(floor_minus[:], -FLOOR_SQUARED)
+
+        bias_bf = const.tile([P, FEATURES], BF16, name="bias_bf")
+        nc.sync.dma_start(out=bias_bf[:], in_=fc1_b.partition_broadcast(P))
+        bias = const.tile([P, FEATURES], F32, name="bias")
+        nc.vector.tensor_copy(out=bias[:], in_=bias_bf[:])
+
+        w_raw = const.tile([P, PASSES, PACK, FEATURES], BF16, name="w_raw")
+        nc.sync.dma_start(out=w_raw[:], in_=fc1_w.rearrange("(g p t) n -> p g t n", p=P, t=PACK))
+        w_grouped = const.tile([P, PASSES, FEATURES, PACK], BF16, name="w_grouped", align_bytes=64)
+        for g in range(PASSES):
+            nc.vector.tensor_copy(
+                out=w_grouped[:, g, :, :], in_=w_raw[:, g, :, :].rearrange("p t n -> p n t")
+            )
+        w_codes = const.tile([P, PASSES * FEATURES], U32, name="w_codes", align_bytes=64)
+        w_scales = const.tile([P, PASSES * FEATURES], U8, name="w_scales", align_bytes=64)
+        nc.vector.quantize_mx(
+            out=w_codes[:].bitcast(FP8X4),
+            scales=w_scales[:],
+            in_=w_grouped[:].rearrange("p g n t -> p (g n t)"),
+        )
+
+        X_RING = 2
+        x_ring = [const.tile([P, BLOCKS, ROW], BF16, name="x_pad%d" % n) for n in range(X_RING)]
+        for x_pad in x_ring:
+            nc.vector.memset(x_pad[:], 0.0)
+        CUBE_RING = 2
+        cube_ring = [const.tile([P, BLOCKS, ROW], F32, name="cube%d" % n) for n in range(CUBE_RING)]
+        for cube in cube_ring:
+            nc.vector.memset(cube[:], 0.0)
+        term = [
+            const.tile([P, BLOCKS, TOKENS + (GRID if o == LEFT else 0)], F32, name="term%d" % o)
+            for o in range(len(OFFSETS))
+        ]
+        for o, (di, dj) in enumerate(OFFSETS):
+            if di < 0:
+                nc.vector.memset(term[o][:, :, 0 : -di * GRID], EPS_CUBED)
+        term_centre = const.tile([P, BLOCKS, TOKENS], F32, name="term_centre")
+        JUNK = 4
+        junk_row = const.tile([P, JUNK, PLANE], BF16, name="junk_row")
+        junk_wide = const.tile([P, 2, CHANNELS], BF16, name="junk_wide")
+
+        tiles = {}
+
+        def lines_of_rows(padded, first_line, n_lines, shift):
+            start = LEAD + PITCH * first_line + shift
+            view = padded[:, :, start : start + PITCH * n_lines]
+            return view.rearrange("p k (i j) -> p k i j", j=PITCH)[:, :, :, 0:GRID]
+
+        def lines_of_row(padded, k, first_line, n_lines, shift):
+            start = LEAD + PITCH * first_line + shift
+            view = padded[:, k, start : start + PITCH * n_lines]
+            return view.rearrange("p (i j) -> p i j", j=PITCH)[:, :, 0:GRID]
+
+        def load_windows(x_tile, b):
+            for w in range(2):
+                nc.sync.dma_start(
+                    out=x_tile[:, w, :], in_=patch_tokens[b, WINDOW_START[w] : WINDOW_START[w] + P, :]
+                )
+
+        def load(b):
+            tiles["x_in", b] = loads.tile([P, 2, CHANNELS], BF16, name="x_in")
+            load_windows(tiles["x_in", b], b)
+
+        def load_again(b):
+            tiles["x_again", b] = loads.tile([P, 2, CHANNELS], BF16, name="x_again", bufs=2)
+            load_windows(tiles["x_again", b], b)
+
+        def transpose_in(b):
+            x_in = tiles["x_in", b]
+            x_pad = x_ring[b % X_RING]
+            square = rows.tile([P, BLOCKS, PLANE], F32, name="square")
+            sum_sq = small.tile([P, BLOCKS], F32, name="sum_sq")
+            norm_sq = small.tile([P, BLOCKS, CENTRE + 1], F32, name="norm_sq")
+            for h in range(2):
+                x_t = psum_x.tile([P, HALF, TOKENS], BF16, name="x_t")
+                for kk in range(HALF):
+                    cols = slice((HALF * h + kk) * P, (HALF * h + kk + 1) * P)
+                    for w in range(2):
+                        nc.tensor.transpose(
+                            x_t[:, kk, WINDOW_START[w] : WINDOW_START[w] + P], x_in[:, w, cols], ident_bf[:]
+                        )
+                nc.scalar.copy(
+                    out=lines_of_rows(x_pad[:, HALF * h : HALF * (h + 1), :], 0, GRID, 0),
+                    in_=x_t[:].rearrange("p k (i j) -> p k i j", j=GRID),
+                )
+                for k in range(HALF * h, HALF * (h + 1)):
+                    nc.scalar.activation(
+                        out=square[:, k, :],
+                        in_=x_pad[:, k, LEAD : LEAD + PLANE],
+                        func=ACT.Square,
+                        accum_out=sum_sq[:, k : k + 1],
+                    )
+                for k in range(HALF * h, HALF * (h + 1)):
+                    nc.scalar.activation(
+                        out=junk_row[:, k % JUNK, :],
+                        in_=square[:, k, :],
+                        func=ACT.Square,
+                        accum_out=norm_sq[:, k, CENTRE : CENTRE + 1],
+                    )
+            tiles["square", b] = square
+            tiles["sum_sq", b] = sum_sq
+            tiles["norm_sq", b] = norm_sq
+
+        def mean_square(b):
+            mean_sq = small.tile([P, BLOCKS], F32, name="mean_sq")
+            nc.vector.tensor_scalar(
+                out=mean_sq[:],
+                in0=tiles["sum_sq", b][:],
+                scalar1=1.0 / TOKENS,
+                scalar2=1e-20,
+                op0=ALU.mult,
+                op1=ALU.max,
+            )
+            tiles["mean_sq", b] = mean_sq
+
+        def row_scale(b):
+            c = small.tile([P, BLOCKS], F32, name="c")
+            nc.vector.reciprocal(out=c[:], in_=tiles["mean_sq", b][:])
+            tiles["c", b] = c
+
+        def c_for_offsets(b):
+            return tiles["c", b][:].unsqueeze(2).to_broadcast([P, BLOCKS, CENTRE + 1])
+
+        def cubes(b):
+            x_pad = x_ring[b % X_RING]
+            cube = cube_ring[b % CUBE_RING]
+            for k in range(BLOCKS):
+                nc.vector.scalar_tensor_tensor(
+                    out=cube[:, k, LEAD : LEAD + PLANE],
+                    in0=x_pad[:, k, LEAD : LEAD + PLANE],
+                    scalar=tiles["c", b][:, k : k + 1],
+                    in1=tiles["square", b][:, k, :],
+                    op0=ALU.mult,
+                    op1=ALU.mult,
+                )
+
+        def window_norms(b):
+            x_pad = x_ring[b % X_RING]
+            norm_sq = tiles["norm_sq", b]
+            for o, (di, dj) in enumerate(OFFSETS):
+                n_lines = GRID + di
+                length = GRID * n_lines
+                z = rows.tile([P, BLOCKS, TOKENS], F32, name="z", bufs=4)
+                nc.vector.tensor_tensor(
+                    out=z[:, :, 0:length].rearrange("p k (i j) -> p k i j", j=GRID),
+                    in0=lines_of_rows(x_pad, -di, n_lines, 0),
+                    in1=lines_of_rows(x_pad, -di, n_lines, PITCH * di + dj),
+                    op=ALU.mult,
+                )
+                for k in range(BLOCKS):
+                    nc.scalar.activation(
+                        out=z[:, k, 0:length],
+                        in_=z[:, k, 0:length],
+                        func=ACT.Square,
+                        accum_out=norm_sq[:, k, o : o + 1],
+                    )
+
+        def scaled_norms_first(b):
+            scaled = small.tile([P, BLOCKS, CENTRE + 1], F32, name="scaled")
+            nc.vector.scalar_tensor_tensor(
+                out=scaled[:],
+                in0=tiles["norm_sq", b][:],
+                scalar=FLOOR_SQUARED,
+                in1=c_for_offsets(b),
+                op0=ALU.max,
+                op1=ALU.mult,
+            )
+            tiles["scaled", b] = scaled
+
+        def scaled_norms_second(b):
+            scaled = tiles["scaled", b]
+            nc.vector.tensor_tensor(out=scaled[:], in0=scaled[:], in1=c_for_offsets(b), op=ALU.mult)
+
+        def weights_ln(b):
+            scaled = tiles["scaled", b]
+            nc.scalar.activation(out=scaled[:], in_=scaled[:], func=ACT.Ln, bias=ln_smallest[:])
+
+        def weights_exp(b):
+            ln_scaled = tiles["scaled", b]
+            power = small.tile([P, BLOCKS, CENTRE + 1], F32, name="power")
+            nc.scalar.activation(out=power[:], in_=ln_scaled[:], func=ACT.Exp, scale=-1.5)
+            centre_scale = small.tile([P, BLOCKS], F32, name="centre_scale")
+            nc.scalar.activation(out=centre_scale[:], in_=ln_scaled[:, :, CENTRE], func=ACT.Exp, scale=-0.75)
+            tiles["power", b] = power
+            tiles["centre_scale", b] = centre_scale
+
+        def weights(b):
+            weight = small.tile([P, BLOCKS, CENTRE + 1], F32, name="weight")
+            nc.vector.tensor_tensor(out=weight[:], in0=tiles["power", b][:], in1=c_for_offsets(b), op=ALU.mult)
+            tiles["weight", b] = weight
+
+        def centre_square(b):
+            centre = rows.tile([P, BLOCKS, TOKENS], F32, name="centre", bufs=1)
+            for k in range(BLOCKS):
+                nc.scalar.activation(
+                    out=centre[:, k, :].rearrange("p (i j) -> p i j", j=GRID),
+                    in_=lines_of_row(cube_ring[b % CUBE_RING], k, 0, GRID, 0),
+                    func=ACT.Square,
+                    scale=tiles["centre_scale", b][:, k : k + 1],
+                )
+            tiles["centre", b] = centre
+
+        def centre_term(b):
+            for k in range(BLOCKS):
+                nc.vector.tensor_scalar(
+                    out=term_centre[:, k, :],
+                    in0=tiles["centre", b][:, k, :],
+                    scalar1=tiles["c", b][:, k : k + 1],
+                    scalar2=EPS_CUBED,
+                    op0=ALU.mult,
+                    op1=ALU.max,
+                )
+
+        def shifted_terms(b, h):
+            cube = cube_ring[b % CUBE_RING]
+            weight = tiles["weight", b]
+
+            def lines_written(o):
+                di, dj = OFFSETS[o]
+                return GRID + 1 if o == LEFT else GRID + di
+
+            def products(o):
+                di, dj = OFFSETS[o]
+                n_lines = lines_written(o)
+                for k in range(HALF * h, HALF * (h + 1)):
+                    nc.vector.scalar_tensor_tensor(
+                        out=term[o][:, k, -di * GRID : (n_lines - di) * GRID].rearrange("p (i j) -> p i j", j=GRID),
+                        in0=lines_of_row(cube, k, -di, n_lines, PITCH * di + dj),
+                        scalar=weight[:, k, o : o + 1],
+                        in1=lines_of_row(cube, k, -di, n_lines, 0),
+                        op0=ALU.mult,
+                        op1=ALU.mult,
+                    )
+
+            def floor_at_eps(o):
+                di, dj = OFFSETS[o]
+                written = term[o][:, HALF * h : HALF * (h + 1), -di * GRID : (lines_written(o) - di) * GRID]
+                nc.vector.tensor_scalar(
+                    out=written, in0=written, scalar1=EPS_CUBED, scalar2=None, op0=ALU.max
+                )
+
+            for o in range(len(OFFSETS)):
+                products(o)
+                if o > 0:
+                    floor_at_eps(o - 1)
+            floor_at_eps(len(OFFSETS) - 1)
+
+            for w in range(2):
+                first = WINDOW_START[w]
+                total_t = psum_t.tile([P, HALF, P], F32, name="total_t")
+                for kk in range(HALF):
+                    k = HALF * h + kk
+                    nine = [term[o][:, k, first : first + P] for o in range(len(OFFSETS))]
+                    nine.append(term[LEFT][:, k, first + 1 : first + 1 + P])
+                    nine.append(term_centre[:, k, first : first + P])
+                    for n, one in enumerate(nine):
+                        nc.tensor.matmul(
+                            out=total_t[:, kk, :],
+                            lhsT=one,
+                            rhs=ident_f32[:],
+                            is_transpose=True,
+                            start=(n == 0),
+                            stop=(n == WINDOW - 1),
+                        )
+                tiles["total_t", b, w, h] = total_t
+
+        def root_ln(b):
+            r_t = rows.tile([P, 2, CHANNELS], F32, name="r_t", bufs=3)
+            for w in range(2):
+                for h in range(2):
+                    nc.scalar.activation(
+                        out=r_t[:, w, BANK * h : BANK * (h + 1)],
+                        in_=tiles["total_t", b, w, h][:].rearrange("p k c -> p (k c)"),
+                        func=ACT.Ln,
+                        scale=1.0 / WINDOW,
+                    )
+            tiles["r_t", b] = r_t
+
+        def root_exp(b):
+            flat = tiles["r_t", b][:].rearrange("p w c -> p (w c)")
+            nc.scalar.activation(out=flat, in_=flat, func=ACT.Exp, scale=1.0 / 3.0)
+
+        def residual(b):
+            r_t = tiles["r_t", b]
+            nc.vector.tensor_tensor(out=r_t[:], in0=r_t[:], in1=tiles["x_again", b][:], op=ALU.add)
+
+        def token_norms(b):
+            length_sq = small.tile([P, 2], F32, name="length_sq")
+            for w in range(2):
+                nc.scalar.activation(
+                    out=junk_wide[:, w, :],
+                    in_=tiles["r_t", b][:, w, :],
+                    func=ACT.Square,
+                    accum_out=length_sq[:, w : w + 1],
+                )
+            tiles["length_sq", b] = length_sq
+
+        def length_floor(b):
+            length_sq = tiles["length_sq", b]
+            nc.scalar.activation(out=length_sq[:], in_=length_sq[:], func=ACT.Relu, bias=floor_minus[:])
+
+        def length_ln(b):
+            length_sq = tiles["length_sq", b]
+            nc.scalar.activation(out=length_sq[:], in_=length_sq[:], func=ACT.Ln, bias=floor_plus[:])
+
+        def length_exp(b):
+            inverse = small.tile([P, 2], F32, name="inverse")
+            nc.scalar.activation(out=inverse[:], in_=tiles["length_sq", b][:], func=ACT.Exp, scale=-0.5)
+            tiles["inverse", b] = inverse
+
+        def normalise(b):
+            tok_t = rows.tile([P, 2, CHANNELS], BF16, name="tok_t")
+            for w in range(2):
+                nc.vector.tensor_scalar(
+                    out=tok_t[:, w, :],
+                    in0=tiles["r_t", b][:, w, :],
+                    scalar1=tiles["inverse", b][:, w : w + 1],
+                    scalar2=None,
+                    op0=ALU.mult,
+                )
+            for g in range(PASSES):
+                tok_c = psum_c.tile([P, PACK, 2 * P], BF16, name="tok_c")
+                for t in range(PACK):
+                    cols = slice(PACK * P * g + t, PACK * P * (g + 1), PACK)
+                    for w in range(2):
+                        nc.tensor.transpose(tok_c[:, t, w * P : (w + 1) * P], tok_t[:, w, cols], ident_bf[:])
+                tiles["tok_c", b, g] = tok_c
+
+        def regroup(b):
+            grouped = rows.tile([P, PASSES, 2 * P, PACK], BF16, name="grouped", align_bytes=64)
+            for g in range(PASSES):
+                nc.scalar.copy(out=grouped[:, g, :, :], in_=tiles["tok_c", b, g][:].rearrange("p t n -> p n t"))
+            tiles["grouped", b] = grouped
+
+        def project(b):
+            codes = small.tile([P, PASSES * 2 * P], U32, name="codes", bufs=2, align_bytes=64)
+            scales = small.tile([P, PASSES * 2 * P], U8, name="scales", bufs=2, align_bytes=64)
+            nc.vector.quantize_mx(
+                out=codes[:].bitcast(FP8X4),
+                scales=scales[:],
+                in_=tiles["grouped", b][:].rearrange("p g n t -> p (g n t)"),
+            )
+            product = psum_m.tile([P, 2, FEATURES], F32, name="product")
+            for w in range(2):
+                for g in range(PASSES):
+                    token_cols = slice((2 * g + w) * P, (2 * g + w + 1) * P)
+                    w_cols = slice(g * FEATURES, (g + 1) * FEATURES)
+                    nc.tensor.matmul_mx(
+                        out=product[:, w, :],
+                        lhsT=codes[:, token_cols].bitcast(FP8X4),
+                        lhsT_scale=scales[:, token_cols],
+                        rhs=w_codes[:, w_cols].bitcast(FP8X4),
+                        rhs_scale=w_scales[:, w_cols],
+                        start=(g == 0),
+                        stop=(g == PASSES - 1),
+                    )
+            tiles["product", b] = product
+
+        def finish(b):
+            n = b % STORE_GROUP
+            if n == 0:
+                tiles["result"] = rows.tile([P, STORE_GROUP, 2, FEATURES], F32, name="result")
+            result = tiles["result"]
+            nc.vector.tensor_tensor(
+                out=result[:, n, :, :],
+                in0=tiles["product", b][:],
+                in1=bias[:].unsqueeze(1).to_broadcast([P, 2, FEATURES]),
+                op=ALU.add,
+            )
+            if n == STORE_GROUP - 1:
+                flat = result[:].rearrange("p n w f -> p (n w f)")
+                nc.scalar.activation(out=flat, in_=flat, func=ACT.Gelu)
+                nc.sync.dma_start(
+                    out=out[b - n : b + 1, 0:P, :].rearrange("n t f -> t n f"), in_=result[:, :, 0, :]
+                )
+                nc.sync.dma_start(
+                    out=out[b - n : b + 1, P:TOKENS, :].rearrange("n t f -> t n f"),
+                    in_=result[P - WINDOW_START[1] : P, :, 1, :],
+                )
+
+        def when_valid(stage, b, *more):
+            if 0 <= b < IMAGES:
+                stage(b, *more)
+
+        def step(i):
+            when_valid(regroup, i - 7)
+            when_valid(finish, i - 8)
+            when_valid(centre_square, i - 3)
+            when_valid(load, i + 2)
+            when_valid(load_again, i - 4)
+            when_valid(mean_square, i - 1)
+            when_valid(window_norms, i - 1)
+            when_valid(transpose_in, i)
+            when_valid(residual, i - 5)
+            when_valid(token_norms, i - 5)
+            when_valid(root_ln, i - 4)
+            when_valid(length_floor, i - 5)
+            when_valid(weights_ln, i - 2)
+            when_valid(length_ln, i - 5)
+            when_valid(weights_exp, i - 2)
+            when_valid(length_exp, i - 5)
+            when_valid(root_exp, i - 4)
+            when_valid(project, i - 7)
+            when_valid(row_scale, i - 1)
+            when_valid(weights, i - 3)
+            when_valid(normalise, i - 6)
+            when_valid(centre_term, i - 3)
+            when_valid(shifted_terms, i - 3, 0)
+            when_valid(shifted_terms, i - 3, 1)
+            when_valid(scaled_norms_first, i - 1)
+            when_valid(cubes, i - 1)
+            when_valid(scaled_norms_second, i - 1)
+
+        LAST_STAGE = 8
+        load(0)
+        load(1)
+        for i in range(LAST_STAGE):
+            step(i)
+        with tc.manual_schedule():
+            for i in range(LAST_STAGE, IMAGES):
+                step(i)
+        for i in range(IMAGES, IMAGES + LAST_STAGE):
+            step(i)

@@ -32,6 +32,7 @@ OFFSETS = [(di, dj) for di in (-2, -1) for dj in (-1, 0, 1)] + [(0, -1)]
 LEFT = len(OFFSETS) - 1
 CENTRE = len(OFFSETS)
 WINDOW = 9
+FOLD = P // BLOCKS
 
 EPS_CUBED = 1e-18
 FLOOR_SQUARED = 1e-24
@@ -50,9 +51,10 @@ def tile_tokenmudule_pa_t_kernel(tc, patch_tokens, fc1_w, fc1_b, out):
         loads = ctx.enter_context(tc.tile_pool(name="loads", bufs=3))
         rows = ctx.enter_context(tc.tile_pool(name="rows", bufs=2))
         small = ctx.enter_context(tc.tile_pool(name="small", bufs=4))
-        psum_x = ctx.enter_context(tc.psum_pool(name="psum_x", bufs=1))
-        psum_t = ctx.enter_context(tc.psum_pool(name="psum_t", bufs=4))
-        psum_c = ctx.enter_context(tc.psum_pool(name="psum_c", bufs=2))
+        work_partial = ctx.enter_context(tc.tile_pool(name="work_partial", bufs=1))
+        psum_io = ctx.enter_context(tc.psum_pool(name="psum_io", bufs=2))
+        psum_t = ctx.enter_context(tc.psum_pool(name="psum_t", bufs=3))
+        psum_n = ctx.enter_context(tc.psum_pool(name="psum_n", bufs=2))
         psum_m = ctx.enter_context(tc.psum_pool(name="psum_m", bufs=1))
 
         ident_bf = const.tile([P, P], BF16, name="ident_bf")
@@ -65,6 +67,14 @@ def tile_tokenmudule_pa_t_kernel(tc, patch_tokens, fc1_w, fc1_b, out):
         nc.vector.memset(floor_plus[:], FLOOR_SQUARED)
         floor_minus = const.tile([P, 1], F32, name="floor_minus")
         nc.vector.memset(floor_minus[:], -FLOOR_SQUARED)
+        eps_minus = const.tile([P, 1], F32, name="eps_minus")
+        nc.vector.memset(eps_minus[:], -EPS_CUBED)
+        eps_in_mean = const.tile([P, 1], F32, name="eps_in_mean")
+        nc.vector.memset(eps_in_mean[:], EPS_CUBED * (WINDOW - 1) / WINDOW)
+        member = const.tile([P, BLOCKS], F32, name="member")
+        nc.vector.reduce_sum(
+            out=member[:], in_=ident_f32[:].rearrange("p (k i) -> p k i", k=BLOCKS), axis=mybir.AxisListType.X
+        )
 
         bias_bf = const.tile([P, FEATURES], BF16, name="bias_bf")
         nc.sync.dma_start(out=bias_bf[:], in_=fc1_b.partition_broadcast(P))
@@ -87,9 +97,16 @@ def tile_tokenmudule_pa_t_kernel(tc, patch_tokens, fc1_w, fc1_b, out):
         )
 
         X_RING = 2
-        x_ring = [const.tile([P, BLOCKS, ROW], BF16, name="x_pad%d" % n) for n in range(X_RING)]
+        x_ring = [const.tile([P, BLOCKS, PLANE], BF16, name="x_pad%d" % n) for n in range(X_RING)]
         for x_pad in x_ring:
             nc.vector.memset(x_pad[:], 0.0)
+        s_ring = [const.tile([P, BLOCKS, ROW], F32, name="square%d" % n) for n in range(X_RING)]
+        for square in s_ring:
+            nc.vector.memset(square[:], 0.0)
+        spacing = [-(-GRID * (GRID + di) // FOLD) for di, dj in OFFSETS]
+        products_sq = [const.tile([P, BLOCKS, FOLD * spacing[o]], F32, name="products_sq%d" % o) for o in range(len(OFFSETS))]
+        for tile in products_sq:
+            nc.vector.memset(tile[:], 0.0)
         CUBE_RING = 2
         cube_ring = [const.tile([P, BLOCKS, ROW], F32, name="cube%d" % n) for n in range(CUBE_RING)]
         for cube in cube_ring:
@@ -100,7 +117,7 @@ def tile_tokenmudule_pa_t_kernel(tc, patch_tokens, fc1_w, fc1_b, out):
         ]
         for o, (di, dj) in enumerate(OFFSETS):
             if di < 0:
-                nc.vector.memset(term[o][:, :, 0 : -di * GRID], EPS_CUBED)
+                nc.vector.memset(term[o][:, :, 0 : -di * GRID], 0.0)
         term_centre = const.tile([P, BLOCKS, TOKENS], F32, name="term_centre")
         JUNK = 4
         junk_row = const.tile([P, JUNK, PLANE], BF16, name="junk_row")
@@ -134,39 +151,43 @@ def tile_tokenmudule_pa_t_kernel(tc, patch_tokens, fc1_w, fc1_b, out):
 
         def transpose_in(b):
             x_in = tiles["x_in", b]
-            x_pad = x_ring[b % X_RING]
-            square = rows.tile([P, BLOCKS, PLANE], F32, name="square")
-            sum_sq = small.tile([P, BLOCKS], F32, name="sum_sq")
-            norm_sq = small.tile([P, BLOCKS, CENTRE + 1], F32, name="norm_sq")
             for h in range(2):
-                x_t = psum_x.tile([P, HALF, TOKENS], BF16, name="x_t")
+                x_t = psum_io.tile([P, HALF, TOKENS], BF16, name="x_t", tag="io")
                 for kk in range(HALF):
                     cols = slice((HALF * h + kk) * P, (HALF * h + kk + 1) * P)
                     for w in range(2):
                         nc.tensor.transpose(
                             x_t[:, kk, WINDOW_START[w] : WINDOW_START[w] + P], x_in[:, w, cols], ident_bf[:]
                         )
+                tiles["x_t", b, h] = x_t
+
+        def squares(b):
+            x_pad = x_ring[b % X_RING]
+            square = s_ring[b % X_RING]
+            sum_sq = small.tile([P, BLOCKS], F32, name="sum_sq")
+            norm_sq_centre = small.tile([P, BLOCKS], F32, name="norm_sq_centre")
+            for h in range(2):
+                x_t = tiles["x_t", b, h]
                 nc.scalar.copy(
-                    out=lines_of_rows(x_pad[:, HALF * h : HALF * (h + 1), :], 0, GRID, 0),
+                    out=x_pad[:, HALF * h : HALF * (h + 1), :].rearrange("p k (i j) -> p k i j", j=PITCH)[:, :, :, 0:GRID],
                     in_=x_t[:].rearrange("p k (i j) -> p k i j", j=GRID),
                 )
                 for k in range(HALF * h, HALF * (h + 1)):
                     nc.scalar.activation(
-                        out=square[:, k, :],
-                        in_=x_pad[:, k, LEAD : LEAD + PLANE],
+                        out=square[:, k, LEAD : LEAD + PLANE],
+                        in_=x_pad[:, k, :],
                         func=ACT.Square,
                         accum_out=sum_sq[:, k : k + 1],
                     )
                 for k in range(HALF * h, HALF * (h + 1)):
                     nc.scalar.activation(
                         out=junk_row[:, k % JUNK, :],
-                        in_=square[:, k, :],
+                        in_=square[:, k, LEAD : LEAD + PLANE],
                         func=ACT.Square,
-                        accum_out=norm_sq[:, k, CENTRE : CENTRE + 1],
+                        accum_out=norm_sq_centre[:, k : k + 1],
                     )
-            tiles["square", b] = square
             tiles["sum_sq", b] = sum_sq
-            tiles["norm_sq", b] = norm_sq
+            tiles["norm_sq_centre", b] = norm_sq_centre
 
         def mean_square(b):
             mean_sq = small.tile([P, BLOCKS], F32, name="mean_sq")
@@ -186,7 +207,7 @@ def tile_tokenmudule_pa_t_kernel(tc, patch_tokens, fc1_w, fc1_b, out):
             tiles["c", b] = c
 
         def c_for_offsets(b):
-            return tiles["c", b][:].unsqueeze(2).to_broadcast([P, BLOCKS, CENTRE + 1])
+            return tiles["c", b][:].unsqueeze(1).to_broadcast([P, CENTRE + 1, BLOCKS])
 
         def cubes(b):
             x_pad = x_ring[b % X_RING]
@@ -194,41 +215,70 @@ def tile_tokenmudule_pa_t_kernel(tc, patch_tokens, fc1_w, fc1_b, out):
             for k in range(BLOCKS):
                 nc.vector.scalar_tensor_tensor(
                     out=cube[:, k, LEAD : LEAD + PLANE],
-                    in0=x_pad[:, k, LEAD : LEAD + PLANE],
+                    in0=x_pad[:, k, :],
                     scalar=tiles["c", b][:, k : k + 1],
-                    in1=tiles["square", b][:, k, :],
+                    in1=s_ring[b % X_RING][:, k, LEAD : LEAD + PLANE],
                     op0=ALU.mult,
                     op1=ALU.mult,
                 )
 
-        def window_norms(b):
-            x_pad = x_ring[b % X_RING]
-            norm_sq = tiles["norm_sq", b]
+        def window_products(b):
+            square = s_ring[b % X_RING]
             for o, (di, dj) in enumerate(OFFSETS):
                 n_lines = GRID + di
-                length = GRID * n_lines
-                z = rows.tile([P, BLOCKS, TOKENS], F32, name="z", bufs=4)
                 nc.vector.tensor_tensor(
-                    out=z[:, :, 0:length].rearrange("p k (i j) -> p k i j", j=GRID),
-                    in0=lines_of_rows(x_pad, -di, n_lines, 0),
-                    in1=lines_of_rows(x_pad, -di, n_lines, PITCH * di + dj),
+                    out=products_sq[o][:, :, 0 : GRID * n_lines].rearrange("p k (i j) -> p k i j", j=GRID),
+                    in0=lines_of_rows(square, -di, n_lines, 0),
+                    in1=lines_of_rows(square, -di, n_lines, PITCH * di + dj),
                     op=ALU.mult,
                 )
-                for k in range(BLOCKS):
-                    nc.scalar.activation(
-                        out=z[:, k, 0:length],
-                        in_=z[:, k, 0:length],
-                        func=ACT.Square,
-                        accum_out=norm_sq[:, k, o : o + 1],
-                    )
+
+        def fold(b):
+            for first in (0, HALF):
+                folded = psum_n.tile([P, HALF, P], F32, name="folded")
+                for o in range(first, min(first + HALF, len(OFFSETS))):
+                    flat = products_sq[o][:].rearrange("p k e -> p (k e)")
+                    for r in range(spacing[o]):
+                        nc.tensor.matmul(
+                            out=folded[:, o - first, :],
+                            lhsT=flat[:, r : P * spacing[o] : spacing[o]],
+                            rhs=ident_f32[:],
+                            is_transpose=True,
+                            start=(r == 0),
+                            stop=(r == spacing[o] - 1),
+                        )
+                tiles["folded", b, first] = folded
+
+        def fold_out(b):
+            partial = work_partial.tile([P, len(OFFSETS), P], F32, name="partial")
+            for first in (0, HALF):
+                last = min(first + HALF, len(OFFSETS))
+                nc.scalar.copy(out=partial[:, first:last, :], in_=tiles["folded", b, first][:, 0 : last - first, :])
+            tiles["partial", b] = partial
+
+        def fold_sum(b):
+            partial = tiles["partial", b]
+            norms = tiles["folded", b, HALF][:, HALF - 1, 0 : len(OFFSETS) * BLOCKS].rearrange("p (o k) -> p o k", k=BLOCKS)
+            for o in range(len(OFFSETS)):
+                nc.tensor.matmul(out=norms[:, o, :], lhsT=partial[:, o, :], rhs=member[:], start=True, stop=True)
+            tiles["norms", b] = norms
 
         def scaled_norms_first(b):
-            scaled = small.tile([P, BLOCKS, CENTRE + 1], F32, name="scaled")
+            scaled = small.tile([P, CENTRE + 1, BLOCKS], F32, name="scaled")
+            c = tiles["c", b]
             nc.vector.scalar_tensor_tensor(
-                out=scaled[:],
-                in0=tiles["norm_sq", b][:],
+                out=scaled[:, 0:CENTRE, :],
+                in0=tiles["norms", b],
                 scalar=FLOOR_SQUARED,
-                in1=c_for_offsets(b),
+                in1=c[:].unsqueeze(1).to_broadcast([P, CENTRE, BLOCKS]),
+                op0=ALU.max,
+                op1=ALU.mult,
+            )
+            nc.vector.scalar_tensor_tensor(
+                out=scaled[:, CENTRE, :],
+                in0=tiles["norm_sq_centre", b][:],
+                scalar=FLOOR_SQUARED,
+                in1=c[:],
                 op0=ALU.max,
                 op1=ALU.mult,
             )
@@ -244,74 +294,66 @@ def tile_tokenmudule_pa_t_kernel(tc, patch_tokens, fc1_w, fc1_b, out):
 
         def weights_exp(b):
             ln_scaled = tiles["scaled", b]
-            power = small.tile([P, BLOCKS, CENTRE + 1], F32, name="power")
+            power = small.tile([P, CENTRE + 1, BLOCKS], F32, name="power")
             nc.scalar.activation(out=power[:], in_=ln_scaled[:], func=ACT.Exp, scale=-1.5)
             centre_scale = small.tile([P, BLOCKS], F32, name="centre_scale")
-            nc.scalar.activation(out=centre_scale[:], in_=ln_scaled[:, :, CENTRE], func=ACT.Exp, scale=-0.75)
+            nc.scalar.activation(out=centre_scale[:], in_=ln_scaled[:, CENTRE, :], func=ACT.Exp, scale=-0.75)
             tiles["power", b] = power
             tiles["centre_scale", b] = centre_scale
 
         def weights(b):
-            weight = small.tile([P, BLOCKS, CENTRE + 1], F32, name="weight")
+            weight = small.tile([P, CENTRE + 1, BLOCKS], F32, name="weight")
             nc.vector.tensor_tensor(out=weight[:], in0=tiles["power", b][:], in1=c_for_offsets(b), op=ALU.mult)
             tiles["weight", b] = weight
 
         def centre_square(b):
-            centre = rows.tile([P, BLOCKS, TOKENS], F32, name="centre", bufs=1)
             for k in range(BLOCKS):
                 nc.scalar.activation(
-                    out=centre[:, k, :].rearrange("p (i j) -> p i j", j=GRID),
+                    out=term_centre[:, k, :].rearrange("p (i j) -> p i j", j=GRID),
                     in_=lines_of_row(cube_ring[b % CUBE_RING], k, 0, GRID, 0),
                     func=ACT.Square,
                     scale=tiles["centre_scale", b][:, k : k + 1],
                 )
-            tiles["centre", b] = centre
 
         def centre_term(b):
             for k in range(BLOCKS):
                 nc.vector.tensor_scalar(
                     out=term_centre[:, k, :],
-                    in0=tiles["centre", b][:, k, :],
+                    in0=term_centre[:, k, :],
                     scalar1=tiles["c", b][:, k : k + 1],
                     scalar2=EPS_CUBED,
                     op0=ALU.mult,
                     op1=ALU.max,
                 )
 
-        def shifted_terms(b, h):
-            cube = cube_ring[b % CUBE_RING]
-            weight = tiles["weight", b]
+        def written_lines(o):
+            di, dj = OFFSETS[o]
+            return -di, GRID + 1 if o == LEFT else GRID + di
 
-            def lines_written(o):
-                di, dj = OFFSETS[o]
-                return GRID + 1 if o == LEFT else GRID + di
-
-            def products(o):
-                di, dj = OFFSETS[o]
-                n_lines = lines_written(o)
-                for k in range(HALF * h, HALF * (h + 1)):
-                    nc.vector.scalar_tensor_tensor(
-                        out=term[o][:, k, -di * GRID : (n_lines - di) * GRID].rearrange("p (i j) -> p i j", j=GRID),
-                        in0=lines_of_row(cube, k, -di, n_lines, PITCH * di + dj),
-                        scalar=weight[:, k, o : o + 1],
-                        in1=lines_of_row(cube, k, -di, n_lines, 0),
-                        op0=ALU.mult,
-                        op1=ALU.mult,
-                    )
-
-            def floor_at_eps(o):
-                di, dj = OFFSETS[o]
-                written = term[o][:, HALF * h : HALF * (h + 1), -di * GRID : (lines_written(o) - di) * GRID]
-                nc.vector.tensor_scalar(
-                    out=written, in0=written, scalar1=EPS_CUBED, scalar2=None, op0=ALU.max
+        def shifted_products(b, h):
+            cube = cube_ring[b % CUBE_RING][:, HALF * h : HALF * (h + 1), :]
+            for o, (di, dj) in enumerate(OFFSETS):
+                first, n_lines = written_lines(o)
+                nc.vector.tensor_tensor(
+                    out=term[o][:, HALF * h : HALF * (h + 1), first * GRID : (first + n_lines) * GRID].rearrange(
+                        "p k (i j) -> p k i j", j=GRID
+                    ),
+                    in0=lines_of_rows(cube, first, n_lines, PITCH * di + dj),
+                    in1=lines_of_rows(cube, first, n_lines, 0),
+                    op=ALU.mult,
                 )
 
+        def shifted_terms(b, h):
+            weight = tiles["weight", b]
             for o in range(len(OFFSETS)):
-                products(o)
-                if o > 0:
-                    floor_at_eps(o - 1)
-            floor_at_eps(len(OFFSETS) - 1)
+                first, n_lines = written_lines(o)
+                for k in range(HALF * h, HALF * (h + 1)):
+                    written = term[o][:, k, first * GRID : (first + n_lines) * GRID]
+                    nc.scalar.activation(
+                        out=written, in_=written, func=ACT.Relu, scale=weight[:, o, k : k + 1], bias=eps_minus[:]
+                    )
 
+        def sum_terms(b, h):
             for w in range(2):
                 first = WINDOW_START[w]
                 total_t = psum_t.tile([P, HALF, P], F32, name="total_t")
@@ -331,17 +373,17 @@ def tile_tokenmudule_pa_t_kernel(tc, patch_tokens, fc1_w, fc1_b, out):
                         )
                 tiles["total_t", b, w, h] = total_t
 
-        def root_ln(b):
-            r_t = rows.tile([P, 2, CHANNELS], F32, name="r_t", bufs=3)
+        def root_ln(b, h):
+            if h == 0:
+                tiles["r_t", b] = rows.tile([P, 2, CHANNELS], F32, name="r_t", bufs=3)
             for w in range(2):
-                for h in range(2):
-                    nc.scalar.activation(
-                        out=r_t[:, w, BANK * h : BANK * (h + 1)],
-                        in_=tiles["total_t", b, w, h][:].rearrange("p k c -> p (k c)"),
-                        func=ACT.Ln,
-                        scale=1.0 / WINDOW,
-                    )
-            tiles["r_t", b] = r_t
+                nc.scalar.activation(
+                    out=tiles["r_t", b][:, w, BANK * h : BANK * (h + 1)],
+                    in_=tiles["total_t", b, w, h][:].rearrange("p k c -> p (k c)"),
+                    func=ACT.Ln,
+                    scale=1.0 / WINDOW,
+                    bias=eps_in_mean[:],
+                )
 
         def root_exp(b):
             flat = tiles["r_t", b][:].rearrange("p w c -> p (w c)")
@@ -385,21 +427,30 @@ def tile_tokenmudule_pa_t_kernel(tc, patch_tokens, fc1_w, fc1_b, out):
                     scalar2=None,
                     op0=ALU.mult,
                 )
+            tiles["tok_t", b] = tok_t
+
+        def transpose_back(b):
+            words = tiles["tok_t", b][:].bitcast(F32)
             for g in range(PASSES):
-                tok_c = psum_c.tile([P, PACK, 2 * P], BF16, name="tok_c")
-                for t in range(PACK):
-                    cols = slice(PACK * P * g + t, PACK * P * (g + 1), PACK)
+                tok_c = psum_io.tile([P, 2, 2 * P], F32, name="tok_c", tag="io")
+                for u in range(2):
                     for w in range(2):
-                        nc.tensor.transpose(tok_c[:, t, w * P : (w + 1) * P], tok_t[:, w, cols], ident_bf[:])
+                        nc.tensor.transpose(
+                            tok_c[:, u, w * P : (w + 1) * P],
+                            words[:, w, 2 * P * g + u : 2 * P * (g + 1) : 2],
+                            ident_f32[:],
+                        )
                 tiles["tok_c", b, g] = tok_c
 
         def regroup(b):
             grouped = rows.tile([P, PASSES, 2 * P, PACK], BF16, name="grouped", align_bytes=64)
             for g in range(PASSES):
-                nc.scalar.copy(out=grouped[:, g, :, :], in_=tiles["tok_c", b, g][:].rearrange("p t n -> p n t"))
+                nc.scalar.copy(
+                    out=grouped[:, g, :, :].bitcast(F32), in_=tiles["tok_c", b, g][:].rearrange("p u n -> p n u")
+                )
             tiles["grouped", b] = grouped
 
-        def project(b):
+        def quantise(b):
             codes = small.tile([P, PASSES * 2 * P], U32, name="codes", bufs=2, align_bytes=64)
             scales = small.tile([P, PASSES * 2 * P], U8, name="scales", bufs=2, align_bytes=64)
             nc.vector.quantize_mx(
@@ -407,6 +458,12 @@ def tile_tokenmudule_pa_t_kernel(tc, patch_tokens, fc1_w, fc1_b, out):
                 scales=scales[:],
                 in_=tiles["grouped", b][:].rearrange("p g n t -> p (g n t)"),
             )
+            tiles["codes", b] = codes
+            tiles["scales", b] = scales
+
+        def project(b):
+            codes = tiles["codes", b]
+            scales = tiles["scales", b]
             product = psum_m.tile([P, 2, FEATURES], F32, name="product")
             for w in range(2):
                 for g in range(PASSES):
@@ -450,37 +507,50 @@ def tile_tokenmudule_pa_t_kernel(tc, patch_tokens, fc1_w, fc1_b, out):
                 stage(b, *more)
 
         def step(i):
-            when_valid(regroup, i - 7)
-            when_valid(finish, i - 8)
+            when_valid(load, i + 3)
+            when_valid(load_again, i - 3)
+            when_valid(shifted_products, i - 3, 0)
+            when_valid(fold, i - 2)
             when_valid(centre_square, i - 3)
-            when_valid(load, i + 2)
-            when_valid(load_again, i - 4)
-            when_valid(mean_square, i - 1)
-            when_valid(window_norms, i - 1)
-            when_valid(transpose_in, i)
-            when_valid(residual, i - 5)
-            when_valid(token_norms, i - 5)
-            when_valid(root_ln, i - 4)
-            when_valid(length_floor, i - 5)
-            when_valid(weights_ln, i - 2)
-            when_valid(length_ln, i - 5)
-            when_valid(weights_exp, i - 2)
-            when_valid(length_exp, i - 5)
-            when_valid(root_exp, i - 4)
-            when_valid(project, i - 7)
-            when_valid(row_scale, i - 1)
+            when_valid(squares, i)
+            when_valid(project, i - 6)
+            when_valid(shifted_products, i - 3, 1)
             when_valid(weights, i - 3)
-            when_valid(normalise, i - 6)
             when_valid(centre_term, i - 3)
+            when_valid(residual, i - 4)
+            when_valid(fold_out, i - 2)
+            when_valid(fold_sum, i - 2)
             when_valid(shifted_terms, i - 3, 0)
             when_valid(shifted_terms, i - 3, 1)
-            when_valid(scaled_norms_first, i - 1)
+            when_valid(normalise, i - 5)
+            when_valid(sum_terms, i - 3, 0)
+            when_valid(transpose_back, i - 5)
+            when_valid(mean_square, i - 1)
+            when_valid(row_scale, i - 1)
+            when_valid(window_products, i - 1)
+            when_valid(regroup, i - 5)
+            when_valid(token_norms, i - 4)
+            when_valid(scaled_norms_first, i - 2)
             when_valid(cubes, i - 1)
-            when_valid(scaled_norms_second, i - 1)
+            when_valid(finish, i - 6)
+            when_valid(scaled_norms_second, i - 2)
+            when_valid(weights_ln, i - 2)
+            when_valid(length_floor, i - 4)
+            when_valid(root_ln, i - 3, 0)
+            when_valid(length_ln, i - 4)
+            when_valid(sum_terms, i - 3, 1)
+            when_valid(transpose_in, i + 1)
+            when_valid(quantise, i - 5)
+            when_valid(root_ln, i - 3, 1)
+            when_valid(weights_exp, i - 2)
+            when_valid(root_exp, i - 3)
+            when_valid(length_exp, i - 4)
 
-        LAST_STAGE = 8
+        LAST_STAGE = 6
         load(0)
         load(1)
+        load(2)
+        transpose_in(0)
         for i in range(LAST_STAGE):
             step(i)
         with tc.manual_schedule():

@@ -13,6 +13,7 @@ ALU = mybir.AluOpType
 
 P = 128
 IMAGES = 32
+PAIRS = IMAGES // 2
 GRID = 14
 TOKENS = GRID * GRID
 CHANNELS = 1024
@@ -23,42 +24,45 @@ BANK = HALF * P
 PACK = 4
 PASSES = CHANNELS // (P * PACK)
 
-PITCH = GRID + 1
+PITCH = 16
 LEAD = 2 * PITCH + 1
 PLANE = GRID * PITCH
 ROW = LEAD + PLANE + PITCH
 
 OFFSETS = [(di, dj) for di in (-2, -1) for dj in (-1, 0, 1)] + [(0, -1)]
-LEFT = len(OFFSETS) - 1
-CENTRE = len(OFFSETS)
+SHIFTS = len(OFFSETS)
+LEFT = SHIFTS - 1
+CENTRE = SHIFTS
 WINDOW = 9
-FOLD = P // BLOCKS
+FOLDED = 3
+RELUED = 5
 
 EPS_CUBED = 1e-18
 FLOOR_SQUARED = 1e-24
 LN_SMALLEST = 1e-18
 
 WINDOW_START = (0, TOKENS - P)
-STORE_GROUP = 4
+PAIR = 2 * TOKENS
+WHOLE = PAIR // P
+REST = PAIR - WHOLE * P
+GROUP = 2
 
 FLOPS = 2 * IMAGES * TOKENS * CHANNELS * FEATURES
 
 
 def tile_tokenmudule_pa_t_kernel(tc, patch_tokens, fc1_w, fc1_b, out):
     nc = tc.nc
+    flat_x = patch_tokens.rearrange("b t c -> (b t) c")
+    flat_out = out.rearrange("b t f -> (b t) f")
     with ExitStack() as ctx:
         const = ctx.enter_context(tc.tile_pool(name="const", bufs=1))
-        loads = ctx.enter_context(tc.tile_pool(name="loads", bufs=3))
-        rows = ctx.enter_context(tc.tile_pool(name="rows", bufs=2))
+        loads = ctx.enter_context(tc.tile_pool(name="loads", bufs=2))
+        work = ctx.enter_context(tc.tile_pool(name="work", bufs=2))
         small = ctx.enter_context(tc.tile_pool(name="small", bufs=4))
-        work_partial = ctx.enter_context(tc.tile_pool(name="work_partial", bufs=1))
         psum_io = ctx.enter_context(tc.psum_pool(name="psum_io", bufs=2))
         psum_t = ctx.enter_context(tc.psum_pool(name="psum_t", bufs=3))
-        psum_n = ctx.enter_context(tc.psum_pool(name="psum_n", bufs=2))
-        psum_m = ctx.enter_context(tc.psum_pool(name="psum_m", bufs=1))
+        psum_1 = ctx.enter_context(tc.psum_pool(name="psum_1", bufs=1))
 
-        ident_bf = const.tile([P, P], BF16, name="ident_bf")
-        make_identity(nc, ident_bf[:])
         ident_f32 = const.tile([P, P], F32, name="ident_f32")
         make_identity(nc, ident_f32[:])
         ln_smallest = const.tile([P, 1], F32, name="ln_smallest")
@@ -69,8 +73,9 @@ def tile_tokenmudule_pa_t_kernel(tc, patch_tokens, fc1_w, fc1_b, out):
         nc.vector.memset(floor_minus[:], -FLOOR_SQUARED)
         eps_minus = const.tile([P, 1], F32, name="eps_minus")
         nc.vector.memset(eps_minus[:], -EPS_CUBED)
+        relued_terms = RELUED + (1 if RELUED > LEFT else 0)
         eps_in_mean = const.tile([P, 1], F32, name="eps_in_mean")
-        nc.vector.memset(eps_in_mean[:], EPS_CUBED * (WINDOW - 1) / WINDOW)
+        nc.vector.memset(eps_in_mean[:], EPS_CUBED * relued_terms / WINDOW)
         member = const.tile([P, BLOCKS], F32, name="member")
         nc.vector.reduce_sum(
             out=member[:], in_=ident_f32[:].rearrange("p (k i) -> p k i", k=BLOCKS), axis=mybir.AxisListType.X
@@ -81,13 +86,11 @@ def tile_tokenmudule_pa_t_kernel(tc, patch_tokens, fc1_w, fc1_b, out):
         bias = const.tile([P, FEATURES], F32, name="bias")
         nc.vector.tensor_copy(out=bias[:], in_=bias_bf[:])
 
-        w_raw = const.tile([P, PASSES, PACK, FEATURES], BF16, name="w_raw")
+        w_raw = work.tile([P, PASSES, PACK, FEATURES], BF16, name="w_raw", tag="tok")
         nc.sync.dma_start(out=w_raw[:], in_=fc1_w.rearrange("(g p t) n -> p g t n", p=P, t=PACK))
-        w_grouped = const.tile([P, PASSES, FEATURES, PACK], BF16, name="w_grouped", align_bytes=64)
+        w_grouped = work.tile([P, PASSES, FEATURES, PACK], BF16, name="w_grouped", tag="grouped", align_bytes=64)
         for g in range(PASSES):
-            nc.vector.tensor_copy(
-                out=w_grouped[:, g, :, :], in_=w_raw[:, g, :, :].rearrange("p t n -> p n t")
-            )
+            nc.vector.tensor_copy(out=w_grouped[:, g, :, :], in_=w_raw[:, g, :, :].rearrange("p t n -> p n t"))
         w_codes = const.tile([P, PASSES * FEATURES], U32, name="w_codes", align_bytes=64)
         w_scales = const.tile([P, PASSES * FEATURES], U8, name="w_scales", align_bytes=64)
         nc.vector.quantize_mx(
@@ -96,98 +99,80 @@ def tile_tokenmudule_pa_t_kernel(tc, patch_tokens, fc1_w, fc1_b, out):
             in_=w_grouped[:].rearrange("p g n t -> p (g n t)"),
         )
 
-        X_RING = 2
-        x_ring = [const.tile([P, BLOCKS, PLANE], BF16, name="x_pad%d" % n) for n in range(X_RING)]
-        for x_pad in x_ring:
-            nc.vector.memset(x_pad[:], 0.0)
-        s_ring = [const.tile([P, BLOCKS, ROW], F32, name="square%d" % n) for n in range(X_RING)]
-        for square in s_ring:
-            nc.vector.memset(square[:], 0.0)
-        spacing = [-(-GRID * (GRID + di) // FOLD) for di, dj in OFFSETS]
-        products_sq = [const.tile([P, BLOCKS, FOLD * spacing[o]], F32, name="products_sq%d" % o) for o in range(len(OFFSETS))]
-        for tile in products_sq:
-            nc.vector.memset(tile[:], 0.0)
-        CUBE_RING = 2
-        cube_ring = [const.tile([P, BLOCKS, ROW], F32, name="cube%d" % n) for n in range(CUBE_RING)]
-        for cube in cube_ring:
-            nc.vector.memset(cube[:], 0.0)
-        term = [
-            const.tile([P, BLOCKS, TOKENS + (GRID if o == LEFT else 0)], F32, name="term%d" % o)
-            for o in range(len(OFFSETS))
-        ]
+        square = const.tile([P, BLOCKS, ROW], F32, name="square")
+        CUBES = 3
+        cube_ring = [const.tile([P, BLOCKS, ROW], F32, name="cube%d" % n) for n in range(CUBES)]
+        for padded in [square] + cube_ring:
+            nc.vector.memset(padded[:], 0.0)
+        term = const.tile([P, CENTRE + 1, BLOCKS, PAIR + 1], F32, name="term")
         for o, (di, dj) in enumerate(OFFSETS):
-            if di < 0:
-                nc.vector.memset(term[o][:, :, 0 : -di * GRID], 0.0)
-        term_centre = const.tile([P, BLOCKS, TOKENS], F32, name="term_centre")
+            for first in (0, TOKENS):
+                if di < 0:
+                    nc.vector.memset(term[:, o, :, first : first - di * GRID], 0.0 if o < RELUED else EPS_CUBED)
+        nc.vector.memset(term[:, LEFT, :, PAIR : PAIR + 1], 0.0 if LEFT < RELUED else EPS_CUBED)
+        rest = const.tile([P, BLOCKS, P], F32, name="rest")
         JUNK = 4
-        junk_row = const.tile([P, JUNK, PLANE], BF16, name="junk_row")
-        junk_wide = const.tile([P, 2, CHANNELS], BF16, name="junk_wide")
+        junk_row = const.tile([P, JUNK, TOKENS], BF16, name="junk_row")
+        junk_wide = const.tile([P, CHANNELS], BF16, name="junk_wide")
 
         tiles = {}
 
-        def lines_of_rows(padded, first_line, n_lines, shift):
+        def lines(padded, rows, first_line, n_lines, shift, width):
             start = LEAD + PITCH * first_line + shift
-            view = padded[:, :, start : start + PITCH * n_lines]
-            return view.rearrange("p k (i j) -> p k i j", j=PITCH)[:, :, :, 0:GRID]
+            view = padded[:, rows, start : start + PITCH * n_lines]
+            return view.rearrange("p k (i j) -> p k i j", j=PITCH)[:, :, :, 0:width]
 
-        def lines_of_row(padded, k, first_line, n_lines, shift):
+        def line(padded, k, first_line, n_lines, shift):
             start = LEAD + PITCH * first_line + shift
             view = padded[:, k, start : start + PITCH * n_lines]
             return view.rearrange("p (i j) -> p i j", j=PITCH)[:, :, 0:GRID]
 
-        def load_windows(x_tile, b):
-            for w in range(2):
-                nc.sync.dma_start(
-                    out=x_tile[:, w, :], in_=patch_tokens[b, WINDOW_START[w] : WINDOW_START[w] + P, :]
-                )
+        def windows(p):
+            return range(WHOLE + (1 if p == PAIRS - 1 else 0))
 
         def load(b):
-            tiles["x_in", b] = loads.tile([P, 2, CHANNELS], BF16, name="x_in")
-            load_windows(tiles["x_in", b], b)
-
-        def load_again(b):
-            tiles["x_again", b] = loads.tile([P, 2, CHANNELS], BF16, name="x_again", bufs=2)
-            load_windows(tiles["x_again", b], b)
+            x_in = loads.tile([P, 2, CHANNELS], BF16, name="x_in")
+            for w in range(2):
+                nc.sync.dma_start(out=x_in[:, w, :], in_=patch_tokens[b, WINDOW_START[w] : WINDOW_START[w] + P, :])
+            tiles["x_in", b] = x_in
 
         def transpose_in(b):
-            x_in = tiles["x_in", b]
+            words = tiles["x_in", b][:].bitcast(F32)
             for h in range(2):
-                x_t = psum_io.tile([P, HALF, TOKENS], BF16, name="x_t", tag="io")
-                for kk in range(HALF):
-                    cols = slice((HALF * h + kk) * P, (HALF * h + kk + 1) * P)
+                x_t = psum_io.tile([P, 2, TOKENS], F32, name="x_t")
+                for uu in range(2):
+                    cols = slice((2 * h + uu) * P, (2 * h + uu + 1) * P)
                     for w in range(2):
                         nc.tensor.transpose(
-                            x_t[:, kk, WINDOW_START[w] : WINDOW_START[w] + P], x_in[:, w, cols], ident_bf[:]
+                            x_t[:, uu, WINDOW_START[w] : WINDOW_START[w] + P], words[:, w, cols], ident_f32[:]
                         )
-                tiles["x_t", b, h] = x_t
+                tiles["x_t", b, h] = x_t[:].rearrange("p u n -> p (u n)").bitcast(BF16).rearrange(
+                    "p (u i j e) -> p u e i j", u=2, e=2, j=GRID
+                )
+
+        def x_row(b, k):
+            return tiles["x_t", b, k // HALF][:, (k % HALF) // 2, k % 2, :, :]
 
         def squares(b):
-            x_pad = x_ring[b % X_RING]
-            square = s_ring[b % X_RING]
             sum_sq = small.tile([P, BLOCKS], F32, name="sum_sq")
-            norm_sq_centre = small.tile([P, BLOCKS], F32, name="norm_sq_centre")
+            norm_sq = small.tile([P, CENTRE + 1, BLOCKS], F32, name="norm_sq")
             for h in range(2):
-                x_t = tiles["x_t", b, h]
-                nc.scalar.copy(
-                    out=x_pad[:, HALF * h : HALF * (h + 1), :].rearrange("p k (i j) -> p k i j", j=PITCH)[:, :, :, 0:GRID],
-                    in_=x_t[:].rearrange("p k (i j) -> p k i j", j=GRID),
-                )
                 for k in range(HALF * h, HALF * (h + 1)):
                     nc.scalar.activation(
-                        out=square[:, k, LEAD : LEAD + PLANE],
-                        in_=x_pad[:, k, :],
+                        out=line(square, k, 0, GRID, 0),
+                        in_=x_row(b, k),
                         func=ACT.Square,
                         accum_out=sum_sq[:, k : k + 1],
                     )
                 for k in range(HALF * h, HALF * (h + 1)):
                     nc.scalar.activation(
-                        out=junk_row[:, k % JUNK, :],
-                        in_=square[:, k, LEAD : LEAD + PLANE],
+                        out=junk_row[:, k % JUNK, :].rearrange("p (i j) -> p i j", j=GRID),
+                        in_=line(square, k, 0, GRID, 0),
                         func=ACT.Square,
-                        accum_out=norm_sq_centre[:, k : k + 1],
+                        accum_out=norm_sq[:, CENTRE, k : k + 1],
                     )
             tiles["sum_sq", b] = sum_sq
-            tiles["norm_sq_centre", b] = norm_sq_centre
+            tiles["norm_sq", b] = norm_sq
 
         def mean_square(b):
             mean_sq = small.tile([P, BLOCKS], F32, name="mean_sq")
@@ -195,366 +180,528 @@ def tile_tokenmudule_pa_t_kernel(tc, patch_tokens, fc1_w, fc1_b, out):
                 out=mean_sq[:],
                 in0=tiles["sum_sq", b][:],
                 scalar1=1.0 / TOKENS,
-                scalar2=1e-20,
+                scalar2=1e-19,
                 op0=ALU.mult,
                 op1=ALU.max,
             )
             tiles["mean_sq", b] = mean_sq
 
         def row_scale(b):
-            c = small.tile([P, BLOCKS], F32, name="c")
-            nc.vector.reciprocal(out=c[:], in_=tiles["mean_sq", b][:])
-            tiles["c", b] = c
-
-        def c_for_offsets(b):
-            return tiles["c", b][:].unsqueeze(1).to_broadcast([P, CENTRE + 1, BLOCKS])
+            scaled = small.tile([P, CENTRE + 2, BLOCKS], F32, name="scaled")
+            nc.vector.reciprocal(out=scaled[:, CENTRE + 1, :], in_=tiles["mean_sq", b][:])
+            tiles["scaled", b] = scaled
 
         def cubes(b):
-            x_pad = x_ring[b % X_RING]
-            cube = cube_ring[b % CUBE_RING]
+            c = tiles["scaled", b][:, CENTRE + 1, :]
             for k in range(BLOCKS):
                 nc.vector.scalar_tensor_tensor(
-                    out=cube[:, k, LEAD : LEAD + PLANE],
-                    in0=x_pad[:, k, :],
-                    scalar=tiles["c", b][:, k : k + 1],
-                    in1=s_ring[b % X_RING][:, k, LEAD : LEAD + PLANE],
+                    out=line(cube_ring[b % CUBES], k, 0, GRID, 0),
+                    in0=x_row(b, k),
+                    scalar=c[:, k : k + 1],
+                    in1=line(square, k, 0, GRID, 0),
                     op0=ALU.mult,
                     op1=ALU.mult,
                 )
 
-        def window_products(b):
-            square = s_ring[b % X_RING]
-            for o, (di, dj) in enumerate(OFFSETS):
-                n_lines = GRID + di
+        def window_products(b, o):
+            di, dj = OFFSETS[o]
+            n_lines = GRID + di
+            shift = PITCH * di + dj
+            every = slice(0, BLOCKS)
+            if o < FOLDED:
+                product = work.tile([P, GRID, BLOCKS, PITCH], F32, name="product_fold", bufs=FOLDED)
                 nc.vector.tensor_tensor(
-                    out=products_sq[o][:, :, 0 : GRID * n_lines].rearrange("p k (i j) -> p k i j", j=GRID),
-                    in0=lines_of_rows(square, -di, n_lines, 0),
-                    in1=lines_of_rows(square, -di, n_lines, PITCH * di + dj),
+                    out=product[:, 0:n_lines, :, :].rearrange("p i k j -> p k i j"),
+                    in0=lines(square, every, -di, n_lines, 0, PITCH),
+                    in1=lines(square, every, -di, n_lines, shift, PITCH),
                     op=ALU.mult,
+                )
+            else:
+                product = work.tile([P, BLOCKS, TOKENS], F32, name="product_sum")
+                nc.vector.tensor_tensor(
+                    out=product[:, :, 0 : GRID * n_lines].rearrange("p k (i j) -> p k i j", j=GRID),
+                    in0=lines(square, every, -di, n_lines, 0, GRID),
+                    in1=lines(square, every, -di, n_lines, shift, GRID),
+                    op=ALU.mult,
+                )
+            tiles["products", b, o] = product
+
+        def sum_products(b, o):
+            length = GRID * (GRID + OFFSETS[o][0])
+            product = tiles["products", b, o]
+            for k in range(BLOCKS):
+                nc.scalar.activation(
+                    out=junk_row[:, k % JUNK, 0:length],
+                    in_=product[:, k, 0:length],
+                    func=ACT.Copy,
+                    accum_out=tiles["norm_sq", b][:, o, k : k + 1],
                 )
 
         def fold(b):
-            for first in (0, HALF):
-                folded = psum_n.tile([P, HALF, P], F32, name="folded")
-                for o in range(first, min(first + HALF, len(OFFSETS))):
-                    flat = products_sq[o][:].rearrange("p k e -> p (k e)")
-                    for r in range(spacing[o]):
-                        nc.tensor.matmul(
-                            out=folded[:, o - first, :],
-                            lhsT=flat[:, r : P * spacing[o] : spacing[o]],
-                            rhs=ident_f32[:],
-                            is_transpose=True,
-                            start=(r == 0),
-                            stop=(r == spacing[o] - 1),
-                        )
-                tiles["folded", b, first] = folded
+            folded = psum_1.tile([P, HALF, P], F32, name="folded")
+            for o in range(FOLDED):
+                n_lines = GRID + OFFSETS[o][0]
+                for i in range(n_lines):
+                    nc.tensor.matmul(
+                        out=folded[:, o, :],
+                        lhsT=tiles["products", b, o][:, i, :, :].rearrange("p k j -> p (k j)"),
+                        rhs=ident_f32[:],
+                        is_transpose=True,
+                        start=(i == 0),
+                        stop=(i == n_lines - 1),
+                    )
+            tiles["folded", b] = folded
 
         def fold_out(b):
-            partial = work_partial.tile([P, len(OFFSETS), P], F32, name="partial")
-            for first in (0, HALF):
-                last = min(first + HALF, len(OFFSETS))
-                nc.scalar.copy(out=partial[:, first:last, :], in_=tiles["folded", b, first][:, 0 : last - first, :])
+            partial = work.tile([P, FOLDED, P], F32, name="partial", bufs=1)
+            nc.scalar.copy(out=partial[:], in_=tiles["folded", b][:, 0:FOLDED, :])
             tiles["partial", b] = partial
 
         def fold_sum(b):
             partial = tiles["partial", b]
-            norms = tiles["folded", b, HALF][:, HALF - 1, 0 : len(OFFSETS) * BLOCKS].rearrange("p (o k) -> p o k", k=BLOCKS)
-            for o in range(len(OFFSETS)):
+            norms = tiles["folded", b][:, HALF - 1, 0 : FOLDED * BLOCKS].rearrange("p (o k) -> p o k", k=BLOCKS)
+            for o in range(FOLDED):
                 nc.tensor.matmul(out=norms[:, o, :], lhsT=partial[:, o, :], rhs=member[:], start=True, stop=True)
             tiles["norms", b] = norms
 
-        def scaled_norms_first(b):
-            scaled = small.tile([P, CENTRE + 1, BLOCKS], F32, name="scaled")
-            c = tiles["c", b]
+        def scale_norms(b, norms, first, last):
+            scaled = tiles["scaled", b]
             nc.vector.scalar_tensor_tensor(
-                out=scaled[:, 0:CENTRE, :],
-                in0=tiles["norms", b],
+                out=scaled[:, first:last, :],
+                in0=norms,
                 scalar=FLOOR_SQUARED,
-                in1=c[:].unsqueeze(1).to_broadcast([P, CENTRE, BLOCKS]),
+                in1=scaled[:, CENTRE + 1, :].unsqueeze(1).to_broadcast([P, last - first, BLOCKS]),
                 op0=ALU.max,
                 op1=ALU.mult,
             )
-            nc.vector.scalar_tensor_tensor(
-                out=scaled[:, CENTRE, :],
-                in0=tiles["norm_sq_centre", b][:],
-                scalar=FLOOR_SQUARED,
-                in1=c[:],
-                op0=ALU.max,
-                op1=ALU.mult,
-            )
-            tiles["scaled", b] = scaled
+
+        def scaled_folds(b):
+            scale_norms(b, tiles["norms", b], 0, FOLDED)
+
+        def scaled_sums(b):
+            scale_norms(b, tiles["norm_sq", b][:, FOLDED : CENTRE + 1, :], FOLDED, CENTRE + 1)
 
         def scaled_norms_second(b):
             scaled = tiles["scaled", b]
-            nc.vector.tensor_tensor(out=scaled[:], in0=scaled[:], in1=c_for_offsets(b), op=ALU.mult)
+            norms = scaled[:, 0 : CENTRE + 1, :]
+            c = scaled[:, CENTRE + 1, :]
+            nc.vector.tensor_tensor(
+                out=norms, in0=norms, in1=c.unsqueeze(1).to_broadcast([P, CENTRE + 1, BLOCKS]), op=ALU.mult
+            )
 
         def weights_ln(b):
             scaled = tiles["scaled", b]
             nc.scalar.activation(out=scaled[:], in_=scaled[:], func=ACT.Ln, bias=ln_smallest[:])
 
+        def weights_sum(b):
+            scaled = tiles["scaled", b]
+            ln_weight = small.tile([P, CENTRE + 1, BLOCKS], F32, name="ln_weight")
+            nc.vector.scalar_tensor_tensor(
+                out=ln_weight[:],
+                in0=scaled[:, 0 : CENTRE + 1, :],
+                scalar=-1.5,
+                in1=scaled[:, CENTRE + 1, :].unsqueeze(1).to_broadcast([P, CENTRE + 1, BLOCKS]),
+                op0=ALU.mult,
+                op1=ALU.add,
+            )
+            tiles["ln_weight", b] = ln_weight
+
         def weights_exp(b):
-            ln_scaled = tiles["scaled", b]
-            power = small.tile([P, CENTRE + 1, BLOCKS], F32, name="power")
-            nc.scalar.activation(out=power[:], in_=ln_scaled[:], func=ACT.Exp, scale=-1.5)
+            ln_weight = tiles["ln_weight", b]
+            weight = small.tile([P, CENTRE, BLOCKS], F32, name="weight")
+            nc.scalar.activation(out=weight[:], in_=ln_weight[:, 0:CENTRE, :], func=ACT.Exp)
             centre_scale = small.tile([P, BLOCKS], F32, name="centre_scale")
-            nc.scalar.activation(out=centre_scale[:], in_=ln_scaled[:, CENTRE, :], func=ACT.Exp, scale=-0.75)
-            tiles["power", b] = power
+            nc.scalar.activation(out=centre_scale[:], in_=ln_weight[:, CENTRE, :], func=ACT.Exp, scale=0.5)
+            tiles["weight", b] = weight
             tiles["centre_scale", b] = centre_scale
 
-        def weights(b):
-            weight = small.tile([P, CENTRE + 1, BLOCKS], F32, name="weight")
-            nc.vector.tensor_tensor(out=weight[:], in0=tiles["power", b][:], in1=c_for_offsets(b), op=ALU.mult)
-            tiles["weight", b] = weight
+        def terms_of(b, o, k, first_line, n_lines):
+            first = TOKENS * (b % 2) + GRID * first_line
+            return term[:, o, k, first : first + GRID * n_lines]
 
         def centre_square(b):
             for k in range(BLOCKS):
                 nc.scalar.activation(
-                    out=term_centre[:, k, :].rearrange("p (i j) -> p i j", j=GRID),
-                    in_=lines_of_row(cube_ring[b % CUBE_RING], k, 0, GRID, 0),
+                    out=terms_of(b, CENTRE, k, 0, GRID).rearrange("p (i j) -> p i j", j=GRID),
+                    in_=line(cube_ring[b % CUBES], k, 0, GRID, 0),
                     func=ACT.Square,
                     scale=tiles["centre_scale", b][:, k : k + 1],
                 )
 
-        def centre_term(b):
-            for k in range(BLOCKS):
-                nc.vector.tensor_scalar(
-                    out=term_centre[:, k, :],
-                    in0=term_centre[:, k, :],
-                    scalar1=tiles["c", b][:, k : k + 1],
-                    scalar2=EPS_CUBED,
-                    op0=ALU.mult,
-                    op1=ALU.max,
-                )
+        def floor_terms(b, o, rows):
+            first_line = max(0, -OFFSETS[o][0]) if o < CENTRE else 0
+            written = terms_of(b, o, rows, first_line, GRID - first_line)
+            nc.vector.tensor_scalar(out=written, in0=written, scalar1=EPS_CUBED, scalar2=None, op0=ALU.max)
 
-        def written_lines(o):
-            di, dj = OFFSETS[o]
-            return -di, GRID + 1 if o == LEFT else GRID + di
+        def centre_floor(b):
+            floor_terms(b, CENTRE, slice(0, BLOCKS))
 
         def shifted_products(b, h):
-            cube = cube_ring[b % CUBE_RING][:, HALF * h : HALF * (h + 1), :]
-            for o, (di, dj) in enumerate(OFFSETS):
-                first, n_lines = written_lines(o)
+            rows = slice(HALF * h, HALF * (h + 1))
+            cube = cube_ring[b % CUBES]
+            for o, (di, dj) in enumerate(OFFSETS[:RELUED]):
+                n_lines = GRID + di
                 nc.vector.tensor_tensor(
-                    out=term[o][:, HALF * h : HALF * (h + 1), first * GRID : (first + n_lines) * GRID].rearrange(
-                        "p k (i j) -> p k i j", j=GRID
-                    ),
-                    in0=lines_of_rows(cube, first, n_lines, PITCH * di + dj),
-                    in1=lines_of_rows(cube, first, n_lines, 0),
+                    out=terms_of(b, o, rows, -di, n_lines).rearrange("p k (i j) -> p k i j", j=GRID),
+                    in0=lines(cube, rows, -di, n_lines, PITCH * di + dj, GRID),
+                    in1=lines(cube, rows, -di, n_lines, 0, GRID),
                     op=ALU.mult,
                 )
 
-        def shifted_terms(b, h):
+        def relu_terms(b, h):
             weight = tiles["weight", b]
-            for o in range(len(OFFSETS)):
-                first, n_lines = written_lines(o)
+            for o, (di, dj) in enumerate(OFFSETS[:RELUED]):
                 for k in range(HALF * h, HALF * (h + 1)):
-                    written = term[o][:, k, first * GRID : (first + n_lines) * GRID]
+                    written = terms_of(b, o, k, -di, GRID + di)
                     nc.scalar.activation(
                         out=written, in_=written, func=ACT.Relu, scale=weight[:, o, k : k + 1], bias=eps_minus[:]
                     )
 
-        def sum_terms(b, h):
-            for w in range(2):
-                first = WINDOW_START[w]
-                total_t = psum_t.tile([P, HALF, P], F32, name="total_t")
-                for kk in range(HALF):
-                    k = HALF * h + kk
-                    nine = [term[o][:, k, first : first + P] for o in range(len(OFFSETS))]
-                    nine.append(term[LEFT][:, k, first + 1 : first + 1 + P])
-                    nine.append(term_centre[:, k, first : first + P])
-                    for n, one in enumerate(nine):
-                        nc.tensor.matmul(
-                            out=total_t[:, kk, :],
-                            lhsT=one,
-                            rhs=ident_f32[:],
-                            is_transpose=True,
-                            start=(n == 0),
-                            stop=(n == WINDOW - 1),
-                        )
-                tiles["total_t", b, w, h] = total_t
+        def vector_terms(b, h):
+            weight = tiles["weight", b]
+            cube = cube_ring[b % CUBES]
+            for o in range(RELUED, SHIFTS):
+                di, dj = OFFSETS[o]
+                for k in range(HALF * h, HALF * (h + 1)):
+                    nc.vector.scalar_tensor_tensor(
+                        out=terms_of(b, o, k, -di, GRID + di).rearrange("p (i j) -> p i j", j=GRID),
+                        in0=line(cube, k, -di, GRID + di, PITCH * di + dj),
+                        scalar=weight[:, o, k : k + 1],
+                        in1=line(cube, k, -di, GRID + di, 0),
+                        op0=ALU.mult,
+                        op1=ALU.mult,
+                    )
+                if o > RELUED:
+                    floor_terms(b, o - 1, slice(HALF * h, HALF * (h + 1)))
+            if RELUED < SHIFTS:
+                floor_terms(b, LEFT, slice(HALF * h, HALF * (h + 1)))
 
-        def root_ln(b, h):
+        def rest_first(p):
+            nc.vector.reduce_sum(
+                out=rest[:, :, REST * p : REST * (p + 1)],
+                in_=term[:, :, :, WHOLE * P : PAIR].rearrange("p o k n -> p k n o"),
+                axis=mybir.AxisListType.X,
+            )
+
+        def rest_second(p):
+            total = rest[:, :, REST * p : REST * (p + 1)]
+            nc.vector.tensor_tensor(
+                out=total, in0=total, in1=term[:, LEFT, :, WHOLE * P + 1 : PAIR + 1], op=ALU.add
+            )
+
+        def sum_terms(p, w, h):
+            total_t = psum_t.tile([P, HALF, P], F32, name="total_t")
+            first = P * w
+            for kk in range(HALF):
+                k = HALF * h + kk
+                if w == WHOLE:
+                    addends = [rest[:, k, :]]
+                else:
+                    addends = [term[:, o, k, first : first + P] for o in range(CENTRE + 1)]
+                    addends.append(term[:, LEFT, k, first + 1 : first + 1 + P])
+                for n, one in enumerate(addends):
+                    nc.tensor.matmul(
+                        out=total_t[:, kk, :],
+                        lhsT=one,
+                        rhs=ident_f32[:],
+                        is_transpose=True,
+                        start=(n == 0),
+                        stop=(n == len(addends) - 1),
+                    )
+            tiles["total_t", p, w, h] = total_t
+
+        def root_ln(p, w, h):
             if h == 0:
-                tiles["r_t", b] = rows.tile([P, 2, CHANNELS], F32, name="r_t", bufs=3)
-            for w in range(2):
-                nc.scalar.activation(
-                    out=tiles["r_t", b][:, w, BANK * h : BANK * (h + 1)],
-                    in_=tiles["total_t", b, w, h][:].rearrange("p k c -> p (k c)"),
-                    func=ACT.Ln,
-                    scale=1.0 / WINDOW,
-                    bias=eps_in_mean[:],
-                )
+                tiles["r_t", p, w] = work.tile([P, CHANNELS], F32, name="r_t", bufs=6)
+            nc.scalar.activation(
+                out=tiles["r_t", p, w][:, BANK * h : BANK * (h + 1)].rearrange("p (u c e) -> p u c e", u=2, e=2),
+                in_=tiles["total_t", p, w, h][:].rearrange("p (u e) c -> p u c e", e=2),
+                func=ACT.Ln,
+                scale=1.0 / WINDOW,
+                bias=eps_in_mean[:],
+            )
 
-        def root_exp(b):
-            flat = tiles["r_t", b][:].rearrange("p w c -> p (w c)")
-            nc.scalar.activation(out=flat, in_=flat, func=ACT.Exp, scale=1.0 / 3.0)
+        def load_again(p, w):
+            x_again = loads.tile([P, CHANNELS], BF16, name="x_again", bufs=3)
+            if w < WHOLE:
+                nc.sync.dma_start(out=x_again[:], in_=flat_x[PAIR * p + P * w : PAIR * p + P * (w + 1), :])
+            else:
+                for q in range(PAIRS):
+                    nc.sync.dma_start(
+                        out=x_again[REST * q : REST * (q + 1), :],
+                        in_=flat_x[PAIR * q + WHOLE * P : PAIR * (q + 1), :],
+                    )
+            tiles["x_again", p, w] = x_again
 
-        def residual(b):
-            r_t = tiles["r_t", b]
-            nc.vector.tensor_tensor(out=r_t[:], in0=r_t[:], in1=tiles["x_again", b][:], op=ALU.add)
+        def root_exp(p, w):
+            r_t = tiles["r_t", p, w]
+            nc.scalar.activation(out=r_t[:], in_=r_t[:], func=ACT.Exp, scale=1.0 / 3.0)
 
-        def token_norms(b):
-            length_sq = small.tile([P, 2], F32, name="length_sq")
-            for w in range(2):
-                nc.scalar.activation(
-                    out=junk_wide[:, w, :],
-                    in_=tiles["r_t", b][:, w, :],
-                    func=ACT.Square,
-                    accum_out=length_sq[:, w : w + 1],
-                )
-            tiles["length_sq", b] = length_sq
+        def residual(p, w):
+            r_t = tiles["r_t", p, w]
+            nc.vector.tensor_tensor(out=r_t[:], in0=r_t[:], in1=tiles["x_again", p, w][:], op=ALU.add)
 
-        def length_floor(b):
-            length_sq = tiles["length_sq", b]
-            nc.scalar.activation(out=length_sq[:], in_=length_sq[:], func=ACT.Relu, bias=floor_minus[:])
+        def token_norms(p, w):
+            if w == 0:
+                tiles["length_sq", p] = small.tile([P, WHOLE + 1], F32, name="length_sq")
+            nc.scalar.activation(
+                out=junk_wide[:],
+                in_=tiles["r_t", p, w][:],
+                func=ACT.Square,
+                accum_out=tiles["length_sq", p][:, w : w + 1],
+            )
 
-        def length_ln(b):
-            length_sq = tiles["length_sq", b]
-            nc.scalar.activation(out=length_sq[:], in_=length_sq[:], func=ACT.Ln, bias=floor_plus[:])
+        def lengths(p):
+            return tiles["length_sq", p][:, 0 : len(windows(p))]
 
-        def length_exp(b):
-            inverse = small.tile([P, 2], F32, name="inverse")
-            nc.scalar.activation(out=inverse[:], in_=tiles["length_sq", b][:], func=ACT.Exp, scale=-0.5)
-            tiles["inverse", b] = inverse
+        def length_floor(p):
+            nc.scalar.activation(out=lengths(p), in_=lengths(p), func=ACT.Relu, bias=floor_minus[:])
 
-        def normalise(b):
-            tok_t = rows.tile([P, 2, CHANNELS], BF16, name="tok_t")
-            for w in range(2):
-                nc.vector.tensor_scalar(
-                    out=tok_t[:, w, :],
-                    in0=tiles["r_t", b][:, w, :],
-                    scalar1=tiles["inverse", b][:, w : w + 1],
-                    scalar2=None,
-                    op0=ALU.mult,
-                )
-            tiles["tok_t", b] = tok_t
+        def length_ln(p):
+            nc.scalar.activation(out=lengths(p), in_=lengths(p), func=ACT.Ln, bias=floor_plus[:])
 
-        def transpose_back(b):
-            words = tiles["tok_t", b][:].bitcast(F32)
+        def length_exp(p):
+            inverse = small.tile([P, WHOLE + 1], F32, name="inverse")
+            nc.scalar.activation(out=inverse[:, 0 : len(windows(p))], in_=lengths(p), func=ACT.Exp, scale=-0.5)
+            tiles["inverse", p] = inverse
+
+        def normalise(p, w):
+            tok_t = work.tile([P, CHANNELS], BF16, name="tok_t", tag="tok")
+            nc.vector.tensor_scalar(
+                out=tok_t[:],
+                in0=tiles["r_t", p, w][:],
+                scalar1=tiles["inverse", p][:, w : w + 1],
+                scalar2=None,
+                op0=ALU.mult,
+            )
+            tiles["tok_t", p, w] = tok_t
+
+        def transpose_back(p, w):
+            words = tiles["tok_t", p, w][:].bitcast(F32)
+            tok_c = psum_1.tile([P, PASSES, 2, P], F32, name="tok_c")
             for g in range(PASSES):
-                tok_c = psum_io.tile([P, 2, 2 * P], F32, name="tok_c", tag="io")
                 for u in range(2):
-                    for w in range(2):
-                        nc.tensor.transpose(
-                            tok_c[:, u, w * P : (w + 1) * P],
-                            words[:, w, 2 * P * g + u : 2 * P * (g + 1) : 2],
-                            ident_f32[:],
-                        )
-                tiles["tok_c", b, g] = tok_c
+                    nc.tensor.transpose(
+                        tok_c[:, g, u, :], words[:, 2 * P * g + u : 2 * P * (g + 1) : 2], ident_f32[:]
+                    )
+            tiles["tok_c", p, w] = tok_c
 
-        def regroup(b):
-            grouped = rows.tile([P, PASSES, 2 * P, PACK], BF16, name="grouped", align_bytes=64)
-            for g in range(PASSES):
-                nc.scalar.copy(
-                    out=grouped[:, g, :, :].bitcast(F32), in_=tiles["tok_c", b, g][:].rearrange("p u n -> p n u")
-                )
-            tiles["grouped", b] = grouped
+        def regroup(p, w):
+            grouped = work.tile([P, PASSES, P, PACK], BF16, name="grouped", align_bytes=64)
+            nc.scalar.copy(
+                out=grouped[:].rearrange("p g n t -> p g (n t)").bitcast(F32).rearrange("p g (n u) -> p g n u", u=2),
+                in_=tiles["tok_c", p, w][:].rearrange("p g u n -> p g n u"),
+            )
+            tiles["grouped", p, w] = grouped
 
-        def quantise(b):
-            codes = small.tile([P, PASSES * 2 * P], U32, name="codes", bufs=2, align_bytes=64)
-            scales = small.tile([P, PASSES * 2 * P], U8, name="scales", bufs=2, align_bytes=64)
+        def quantise(p, w):
+            codes = small.tile([P, PASSES * P], U32, name="codes", bufs=2, align_bytes=64)
+            scales = small.tile([P, PASSES * P], U8, name="scales", bufs=2, align_bytes=64)
             nc.vector.quantize_mx(
                 out=codes[:].bitcast(FP8X4),
                 scales=scales[:],
-                in_=tiles["grouped", b][:].rearrange("p g n t -> p (g n t)"),
+                in_=tiles["grouped", p, w][:].rearrange("p g n t -> p (g n t)"),
             )
-            tiles["codes", b] = codes
-            tiles["scales", b] = scales
+            tiles["codes", p, w] = codes
+            tiles["scales", p, w] = scales
 
-        def project(b):
-            codes = tiles["codes", b]
-            scales = tiles["scales", b]
-            product = psum_m.tile([P, 2, FEATURES], F32, name="product")
-            for w in range(2):
-                for g in range(PASSES):
-                    token_cols = slice((2 * g + w) * P, (2 * g + w + 1) * P)
-                    w_cols = slice(g * FEATURES, (g + 1) * FEATURES)
-                    nc.tensor.matmul_mx(
-                        out=product[:, w, :],
-                        lhsT=codes[:, token_cols].bitcast(FP8X4),
-                        lhsT_scale=scales[:, token_cols],
-                        rhs=w_codes[:, w_cols].bitcast(FP8X4),
-                        rhs_scale=w_scales[:, w_cols],
-                        start=(g == 0),
-                        stop=(g == PASSES - 1),
-                    )
-            tiles["product", b] = product
+        def project(p, w):
+            codes = tiles["codes", p, w]
+            scales = tiles["scales", p, w]
+            if w == 0:
+                tiles["projected", p] = psum_1.tile([P, WHOLE + 1, FEATURES], F32, name="projected")
+            for g in range(PASSES):
+                nc.tensor.matmul_mx(
+                    out=tiles["projected", p][:, w, :],
+                    lhsT=codes[:, P * g : P * (g + 1)].bitcast(FP8X4),
+                    lhsT_scale=scales[:, P * g : P * (g + 1)],
+                    rhs=w_codes[:, FEATURES * g : FEATURES * (g + 1)].bitcast(FP8X4),
+                    rhs_scale=w_scales[:, FEATURES * g : FEATURES * (g + 1)],
+                    start=(g == 0),
+                    stop=(g == PASSES - 1),
+                )
 
-        def finish(b):
-            n = b % STORE_GROUP
+        def finish(p):
+            n = WHOLE * (p % GROUP)
+            count = len(windows(p))
             if n == 0:
-                tiles["result"] = rows.tile([P, STORE_GROUP, 2, FEATURES], F32, name="result")
-            result = tiles["result"]
+                tiles["result", p // GROUP] = work.tile([P, WHOLE * GROUP + 1, FEATURES], F32, name="result")
             nc.vector.tensor_tensor(
-                out=result[:, n, :, :],
-                in0=tiles["product", b][:],
-                in1=bias[:].unsqueeze(1).to_broadcast([P, 2, FEATURES]),
+                out=tiles["result", p // GROUP][:, n : n + count, :],
+                in0=tiles["projected", p][:, 0:count, :],
+                in1=bias[:].unsqueeze(1).to_broadcast([P, count, FEATURES]),
                 op=ALU.add,
             )
-            if n == STORE_GROUP - 1:
-                flat = result[:].rearrange("p n w f -> p (n w f)")
-                nc.scalar.activation(out=flat, in_=flat, func=ACT.Gelu)
-                nc.sync.dma_start(
-                    out=out[b - n : b + 1, 0:P, :].rearrange("n t f -> t n f"), in_=result[:, :, 0, :]
-                )
-                nc.sync.dma_start(
-                    out=out[b - n : b + 1, P:TOKENS, :].rearrange("n t f -> t n f"),
-                    in_=result[P - WINDOW_START[1] : P, :, 1, :],
-                )
 
-        def when_valid(stage, b, *more):
+        def gelu(p):
+            if p % GROUP < GROUP - 1:
+                return
+            count = WHOLE * GROUP + (1 if p == PAIRS - 1 else 0)
+            result = tiles["result", p // GROUP]
+            flat = result[:, 0:count, :].rearrange("p n f -> p (n f)")
+            nc.scalar.activation(out=flat, in_=flat, func=ACT.Gelu)
+            for n in range(GROUP):
+                first = PAIR * (p - GROUP + 1 + n)
+                nc.sync.dma_start(
+                    out=flat_out[first : first + WHOLE * P, :].rearrange("(w n) f -> n w f", n=P),
+                    in_=result[:, WHOLE * n : WHOLE * (n + 1), :],
+                )
+            if p == PAIRS - 1:
+                for q in range(PAIRS):
+                    nc.sync.dma_start(
+                        out=flat_out[PAIR * q + WHOLE * P : PAIR * (q + 1), :],
+                        in_=result[REST * q : REST * (q + 1), WHOLE * GROUP, :],
+                    )
+
+        def of_image(stage, b, *more):
             if 0 <= b < IMAGES:
                 stage(b, *more)
 
-        def step(i):
-            when_valid(load, i + 3)
-            when_valid(load_again, i - 3)
-            when_valid(shifted_products, i - 3, 0)
-            when_valid(fold, i - 2)
-            when_valid(centre_square, i - 3)
-            when_valid(squares, i)
-            when_valid(project, i - 6)
-            when_valid(shifted_products, i - 3, 1)
-            when_valid(weights, i - 3)
-            when_valid(centre_term, i - 3)
-            when_valid(residual, i - 4)
-            when_valid(fold_out, i - 2)
-            when_valid(fold_sum, i - 2)
-            when_valid(shifted_terms, i - 3, 0)
-            when_valid(shifted_terms, i - 3, 1)
-            when_valid(normalise, i - 5)
-            when_valid(sum_terms, i - 3, 0)
-            when_valid(transpose_back, i - 5)
-            when_valid(mean_square, i - 1)
-            when_valid(row_scale, i - 1)
-            when_valid(window_products, i - 1)
-            when_valid(regroup, i - 5)
-            when_valid(token_norms, i - 4)
-            when_valid(scaled_norms_first, i - 2)
-            when_valid(cubes, i - 1)
-            when_valid(finish, i - 6)
-            when_valid(scaled_norms_second, i - 2)
-            when_valid(weights_ln, i - 2)
-            when_valid(length_floor, i - 4)
-            when_valid(root_ln, i - 3, 0)
-            when_valid(length_ln, i - 4)
-            when_valid(sum_terms, i - 3, 1)
-            when_valid(transpose_in, i + 1)
-            when_valid(quantise, i - 5)
-            when_valid(root_ln, i - 3, 1)
-            when_valid(weights_exp, i - 2)
-            when_valid(root_exp, i - 3)
-            when_valid(length_exp, i - 4)
+        def of_pair(stage, p, *more):
+            if 0 <= p < PAIRS:
+                stage(p, *more)
 
-        LAST_STAGE = 6
+        def of_window(stage, p, w, *more):
+            if 0 <= p < PAIRS and w in windows(p):
+                stage(p, w, *more)
+
+        def even_step(i, m):
+            of_window(load_again, m - 2, 0)
+            of_window(load_again, m - 2, 1)
+            of_image(load, i + 2)
+            of_image(shifted_products, i - 2, 0)
+            of_image(squares, i)
+            of_image(shifted_products, i - 2, 1)
+            of_image(sum_products, i - 1, 5)
+            of_image(sum_products, i - 1, 6)
+            of_window(quantise, m - 4, 2)
+            of_window(quantise, m - 4, 3)
+            of_window(root_ln, m - 2, 2, 0)
+            of_window(sum_terms, m - 2, 2, 1)
+            of_window(root_ln, m - 2, 1, 1)
+            of_image(scaled_folds, i - 1)
+            of_image(scaled_sums, i - 1)
+            of_image(mean_square, i)
+            of_image(scaled_norms_second, i - 1)
+            of_image(row_scale, i)
+            of_pair(length_floor, m - 3)
+            of_pair(length_ln, m - 3)
+            of_image(weights_ln, i - 2)
+            of_image(weights_ln, i - 1)
+            of_window(root_ln, m - 2, 2, 1)
+            of_image(cubes, i)
+            of_image(transpose_in, i + 1)
+            of_image(window_products, i, 0)
+            of_image(window_products, i, 1)
+            of_image(weights_sum, i - 2)
+            of_image(weights_sum, i - 1)
+            of_window(root_exp, m - 2, 0)
+            of_image(weights_exp, i - 2)
+            of_image(weights_exp, i - 1)
+            of_pair(length_exp, m - 3)
+            of_window(root_exp, m - 2, 1)
+            of_window(root_exp, m - 2, 2)
+            of_image(window_products, i, 2)
+            of_window(project, m - 4, 2)
+            of_window(project, m - 4, 3)
+            of_pair(finish, m - 4)
+            of_image(fold, i)
+            of_pair(gelu, m - 4)
+            of_image(centre_square, i - 2)
+            of_image(window_products, i, 3)
+            of_image(window_products, i, 4)
+            of_image(relu_terms, i - 2, 0)
+            of_image(vector_terms, i - 2, 0)
+            of_image(centre_floor, i - 2)
+            of_window(sum_terms, m - 1, 0, 0)
+            of_image(sum_products, i, 3)
+            of_image(sum_products, i, 4)
+            of_image(vector_terms, i - 2, 1)
+            of_window(residual, m - 2, 0)
+            of_window(normalise, m - 3, 0)
+            of_window(transpose_back, m - 3, 0)
+            of_window(residual, m - 2, 1)
+            of_window(normalise, m - 3, 1)
+            of_image(window_products, i, 5)
+            of_image(relu_terms, i - 2, 1)
+            of_image(fold_out, i)
+            of_window(token_norms, m - 2, 0)
+            of_window(regroup, m - 3, 0)
+            of_image(window_products, i, 6)
+            of_image(fold_sum, i)
+            of_window(sum_terms, m - 1, 0, 1)
+            of_window(token_norms, m - 2, 1)
+            of_window(quantise, m - 3, 0)
+            of_window(root_ln, m - 1, 0, 0)
+            of_window(transpose_back, m - 3, 1)
+
+        def odd_step(i, m):
+            of_window(load_again, m - 2, 2)
+            of_image(load, i + 2)
+            of_window(load_again, m - 2, 3)
+            of_window(sum_terms, m - 2, 3, 0)
+            of_window(root_ln, m - 2, 3, 0)
+            of_window(sum_terms, m - 2, 3, 1)
+            of_window(root_ln, m - 2, 3, 1)
+            of_window(root_exp, m - 2, 3)
+            of_window(residual, m - 2, 3)
+            of_window(token_norms, m - 2, 3)
+            of_image(shifted_products, i - 2, 0)
+            of_image(centre_square, i - 2)
+            of_image(squares, i)
+            of_image(shifted_products, i - 2, 1)
+            of_window(project, m - 3, 0)
+            of_image(relu_terms, i - 2, 0)
+            of_image(vector_terms, i - 2, 0)
+            of_image(centre_floor, i - 2)
+            of_window(sum_terms, m - 1, 1, 0)
+            of_image(scaled_folds, i - 1)
+            of_image(mean_square, i)
+            of_image(sum_products, i - 1, 5)
+            of_image(row_scale, i)
+            of_image(sum_products, i - 1, 6)
+            of_image(cubes, i)
+            of_image(transpose_in, i + 1)
+            of_window(root_ln, m - 1, 0, 1)
+            of_image(window_products, i, 0)
+            of_image(window_products, i, 1)
+            of_image(window_products, i, 2)
+            of_image(fold, i)
+            of_image(vector_terms, i - 2, 1)
+            of_window(regroup, m - 3, 1)
+            of_image(window_products, i, 3)
+            of_image(relu_terms, i - 2, 1)
+            of_image(scaled_sums, i - 1)
+            of_image(window_products, i, 4)
+            of_image(scaled_norms_second, i - 1)
+            of_window(sum_terms, m - 1, 2, 0)
+            of_window(residual, m - 2, 2)
+            of_window(normalise, m - 3, 2)
+            of_window(transpose_back, m - 3, 2)
+            of_image(sum_products, i, 3)
+            of_image(sum_products, i, 4)
+            of_pair(rest_first, m - 1)
+            of_pair(rest_second, m - 1)
+            of_image(window_products, i, 5)
+            of_window(quantise, m - 3, 1)
+            of_image(fold_out, i)
+            of_image(fold_sum, i)
+            of_window(project, m - 3, 1)
+            of_image(window_products, i, 6)
+            of_window(token_norms, m - 2, 2)
+            of_window(regroup, m - 3, 2)
+            of_window(root_ln, m - 1, 1, 0)
+            of_window(sum_terms, m - 1, 1, 1)
+            of_window(normalise, m - 3, 3)
+            of_window(transpose_back, m - 3, 3)
+            of_window(regroup, m - 3, 3)
+
         load(0)
         load(1)
-        load(2)
         transpose_in(0)
-        for i in range(LAST_STAGE):
-            step(i)
-        with tc.manual_schedule():
-            for i in range(LAST_STAGE, IMAGES):
-                step(i)
-        for i in range(IMAGES, IMAGES + LAST_STAGE):
-            step(i)
+        LAST = 10
+        for i in range(IMAGES + LAST):
+            with ExitStack() as pinned:
+                if LAST <= i < IMAGES:
+                    pinned.enter_context(tc.manual_schedule())
+                (odd_step if i % 2 else even_step)(i, i // 2)

@@ -25,7 +25,7 @@ PACK = 4
 PASSES = CHANNELS // (P * PACK)
 
 PITCH = 16
-LEAD = 2 * PITCH + 1
+LEAD = 2 * PITCH + 4
 PLANE = GRID * PITCH
 ROW = LEAD + PLANE + PITCH
 
@@ -34,8 +34,7 @@ SHIFTS = len(OFFSETS)
 LEFT = SHIFTS - 1
 CENTRE = SHIFTS
 WINDOW = 9
-FOLDED = 3
-RELUED = 5
+SUMMED = 2
 
 EPS_CUBED = 1e-18
 FLOOR_SQUARED = 1e-24
@@ -60,7 +59,7 @@ def tile_tokenmudule_pa_t_kernel(tc, patch_tokens, fc1_w, fc1_b, out):
         work = ctx.enter_context(tc.tile_pool(name="work", bufs=2))
         small = ctx.enter_context(tc.tile_pool(name="small", bufs=4))
         psum_io = ctx.enter_context(tc.psum_pool(name="psum_io", bufs=2))
-        psum_t = ctx.enter_context(tc.psum_pool(name="psum_t", bufs=3))
+        psum_t = ctx.enter_context(tc.psum_pool(name="psum_t", bufs=4))
         psum_1 = ctx.enter_context(tc.psum_pool(name="psum_1", bufs=1))
 
         ident_f32 = const.tile([P, P], F32, name="ident_f32")
@@ -73,14 +72,8 @@ def tile_tokenmudule_pa_t_kernel(tc, patch_tokens, fc1_w, fc1_b, out):
         nc.vector.memset(floor_minus[:], -FLOOR_SQUARED)
         eps_minus = const.tile([P, 1], F32, name="eps_minus")
         nc.vector.memset(eps_minus[:], -EPS_CUBED)
-        relued_terms = RELUED + (1 if RELUED > LEFT else 0)
         eps_in_mean = const.tile([P, 1], F32, name="eps_in_mean")
-        nc.vector.memset(eps_in_mean[:], EPS_CUBED * relued_terms / WINDOW)
-        member = const.tile([P, BLOCKS], F32, name="member")
-        nc.vector.reduce_sum(
-            out=member[:], in_=ident_f32[:].rearrange("p (k i) -> p k i", k=BLOCKS), axis=mybir.AxisListType.X
-        )
-
+        nc.vector.memset(eps_in_mean[:], EPS_CUBED * (WINDOW - 1) / WINDOW)
         bias_bf = const.tile([P, FEATURES], BF16, name="bias_bf")
         nc.sync.dma_start(out=bias_bf[:], in_=fc1_b.partition_broadcast(P))
         bias = const.tile([P, FEATURES], F32, name="bias")
@@ -99,20 +92,22 @@ def tile_tokenmudule_pa_t_kernel(tc, patch_tokens, fc1_w, fc1_b, out):
             in_=w_grouped[:].rearrange("p g n t -> p (g n t)"),
         )
 
-        square = const.tile([P, BLOCKS, ROW], F32, name="square")
+        SQUARES = 2
+        square_ring = [const.tile([P, BLOCKS, ROW], F32, name="square%d" % n) for n in range(SQUARES)]
         CUBES = 3
         cube_ring = [const.tile([P, BLOCKS, ROW], F32, name="cube%d" % n) for n in range(CUBES)]
-        for padded in [square] + cube_ring:
+        for padded in square_ring + cube_ring:
             nc.vector.memset(padded[:], 0.0)
-        term = const.tile([P, CENTRE + 1, BLOCKS, PAIR + 1], F32, name="term")
+        term = const.tile([P, CENTRE + 1, BLOCKS, PAIR + 4], F32, name="term")
         for o, (di, dj) in enumerate(OFFSETS):
             for first in (0, TOKENS):
                 if di < 0:
-                    nc.vector.memset(term[:, o, :, first : first - di * GRID], 0.0 if o < RELUED else EPS_CUBED)
-        nc.vector.memset(term[:, LEFT, :, PAIR : PAIR + 1], 0.0 if LEFT < RELUED else EPS_CUBED)
+                    nc.vector.memset(term[:, o, :, first : first - di * GRID], 0.0)
+        nc.vector.memset(term[:, LEFT, :, PAIR : PAIR + 1], 0.0)
         rest = const.tile([P, BLOCKS, P], F32, name="rest")
         JUNK = 4
         junk_row = const.tile([P, JUNK, TOKENS], BF16, name="junk_row")
+        junk_f32 = const.tile([P, JUNK, TOKENS], F32, name="junk_f32")
         junk_wide = const.tile([P, CHANNELS], BF16, name="junk_wide")
 
         tiles = {}
@@ -159,7 +154,7 @@ def tile_tokenmudule_pa_t_kernel(tc, patch_tokens, fc1_w, fc1_b, out):
             for h in range(2):
                 for k in range(HALF * h, HALF * (h + 1)):
                     nc.scalar.activation(
-                        out=line(square, k, 0, GRID, 0),
+                        out=line(square_ring[b % SQUARES], k, 0, GRID, 0),
                         in_=x_row(b, k),
                         func=ACT.Square,
                         accum_out=sum_sq[:, k : k + 1],
@@ -167,7 +162,7 @@ def tile_tokenmudule_pa_t_kernel(tc, patch_tokens, fc1_w, fc1_b, out):
                 for k in range(HALF * h, HALF * (h + 1)):
                     nc.scalar.activation(
                         out=junk_row[:, k % JUNK, :].rearrange("p (i j) -> p i j", j=GRID),
-                        in_=line(square, k, 0, GRID, 0),
+                        in_=line(square_ring[b % SQUARES], k, 0, GRID, 0),
                         func=ACT.Square,
                         accum_out=norm_sq[:, CENTRE, k : k + 1],
                     )
@@ -198,37 +193,35 @@ def tile_tokenmudule_pa_t_kernel(tc, patch_tokens, fc1_w, fc1_b, out):
                     out=line(cube_ring[b % CUBES], k, 0, GRID, 0),
                     in0=x_row(b, k),
                     scalar=c[:, k : k + 1],
-                    in1=line(square, k, 0, GRID, 0),
+                    in1=line(square_ring[b % SQUARES], k, 0, GRID, 0),
                     op0=ALU.mult,
                     op1=ALU.mult,
                 )
 
-        def window_products(b, o):
+        def columns(dj):
+            return max(0, -dj), GRID - abs(dj)
+
+        def grid_part(padded, rows, o):
             di, dj = OFFSETS[o]
-            n_lines = GRID + di
-            shift = PITCH * di + dj
-            every = slice(0, BLOCKS)
-            if o < FOLDED:
-                product = work.tile([P, GRID, BLOCKS, PITCH], F32, name="product_fold", bufs=FOLDED)
-                nc.vector.tensor_tensor(
-                    out=product[:, 0:n_lines, :, :].rearrange("p i k j -> p k i j"),
-                    in0=lines(square, every, -di, n_lines, 0, PITCH),
-                    in1=lines(square, every, -di, n_lines, shift, PITCH),
-                    op=ALU.mult,
-                )
-            else:
-                product = work.tile([P, BLOCKS, TOKENS], F32, name="product_sum")
-                nc.vector.tensor_tensor(
-                    out=product[:, :, 0 : GRID * n_lines].rearrange("p k (i j) -> p k i j", j=GRID),
-                    in0=lines(square, every, -di, n_lines, 0, GRID),
-                    in1=lines(square, every, -di, n_lines, shift, GRID),
-                    op=ALU.mult,
-                )
+            first, width = columns(dj)
+            here = lines(padded, rows, -di, GRID + di, first, width)
+            there = lines(padded, rows, -di, GRID + di, first + PITCH * di + dj, width)
+            return here, there, (GRID + di) * width
+
+        def window_products(b, o):
+            here, there, length = grid_part(square_ring[b % SQUARES], slice(0, BLOCKS), o)
+            product = work.tile([P, BLOCKS, TOKENS], F32, name="product")
+            nc.vector.tensor_tensor(
+                out=product[:, :, 0:length].rearrange("p k (i j) -> p k i j", i=GRID + OFFSETS[o][0]),
+                in0=here,
+                in1=there,
+                op=ALU.mult,
+            )
             tiles["products", b, o] = product
 
         def sum_products(b, o):
-            length = GRID * (GRID + OFFSETS[o][0])
             product = tiles["products", b, o]
+            length = grid_part(square_ring[b % SQUARES], slice(0, BLOCKS), o)[2]
             for k in range(BLOCKS):
                 nc.scalar.activation(
                     out=junk_row[:, k % JUNK, 0:length],
@@ -237,49 +230,30 @@ def tile_tokenmudule_pa_t_kernel(tc, patch_tokens, fc1_w, fc1_b, out):
                     accum_out=tiles["norm_sq", b][:, o, k : k + 1],
                 )
 
-        def fold(b):
-            folded = psum_1.tile([P, HALF, P], F32, name="folded")
-            for o in range(FOLDED):
-                n_lines = GRID + OFFSETS[o][0]
-                for i in range(n_lines):
-                    nc.tensor.matmul(
-                        out=folded[:, o, :],
-                        lhsT=tiles["products", b, o][:, i, :, :].rearrange("p k j -> p (k j)"),
-                        rhs=ident_f32[:],
-                        is_transpose=True,
-                        start=(i == 0),
-                        stop=(i == n_lines - 1),
-                    )
-            tiles["folded", b] = folded
+        def window_sums(b, o):
+            for k in range(BLOCKS):
+                here, there, length = grid_part(square_ring[b % SQUARES], slice(k, k + 1), o)
+                out_row = junk_f32[:, k % JUNK, 0:length].rearrange("p (a i j) -> p a i j", a=1, i=GRID + OFFSETS[o][0])
+                nc.vector.scalar_tensor_tensor(
+                    out=out_row,
+                    in0=here,
+                    scalar=1.0,
+                    in1=there,
+                    op0=ALU.mult,
+                    op1=ALU.mult,
+                    accum_out=tiles["norm_sq", b][:, o, k : k + 1],
+                )
 
-        def fold_out(b):
-            partial = work.tile([P, FOLDED, P], F32, name="partial", bufs=1)
-            nc.scalar.copy(out=partial[:], in_=tiles["folded", b][:, 0:FOLDED, :])
-            tiles["partial", b] = partial
-
-        def fold_sum(b):
-            partial = tiles["partial", b]
-            norms = tiles["folded", b][:, HALF - 1, 0 : FOLDED * BLOCKS].rearrange("p (o k) -> p o k", k=BLOCKS)
-            for o in range(FOLDED):
-                nc.tensor.matmul(out=norms[:, o, :], lhsT=partial[:, o, :], rhs=member[:], start=True, stop=True)
-            tiles["norms", b] = norms
-
-        def scale_norms(b, norms, first, last):
+        def scaled_norms_first(b):
             scaled = tiles["scaled", b]
             nc.vector.scalar_tensor_tensor(
-                out=scaled[:, first:last, :],
-                in0=norms,
+                out=scaled[:, 0 : CENTRE + 1, :],
+                in0=tiles["norm_sq", b][:],
                 scalar=FLOOR_SQUARED,
-                in1=scaled[:, CENTRE + 1, :].unsqueeze(1).to_broadcast([P, last - first, BLOCKS]),
+                in1=scaled[:, CENTRE + 1, :].unsqueeze(1).to_broadcast([P, CENTRE + 1, BLOCKS]),
                 op0=ALU.max,
                 op1=ALU.mult,
             )
-
-        def scaled_folds(b):
-            scale_norms(b, tiles["norms", b], 0, FOLDED)
-
-        def scaled_sums(b):
-            scale_norms(b, tiles["norm_sq", b][:, FOLDED : CENTRE + 1, :], FOLDED, CENTRE + 1)
 
         def scaled_norms_second(b):
             scaled = tiles["scaled", b]
@@ -328,18 +302,14 @@ def tile_tokenmudule_pa_t_kernel(tc, patch_tokens, fc1_w, fc1_b, out):
                     scale=tiles["centre_scale", b][:, k : k + 1],
                 )
 
-        def floor_terms(b, o, rows):
-            first_line = max(0, -OFFSETS[o][0]) if o < CENTRE else 0
-            written = terms_of(b, o, rows, first_line, GRID - first_line)
-            nc.vector.tensor_scalar(out=written, in0=written, scalar1=EPS_CUBED, scalar2=None, op0=ALU.max)
-
         def centre_floor(b):
-            floor_terms(b, CENTRE, slice(0, BLOCKS))
+            written = terms_of(b, CENTRE, slice(0, BLOCKS), 0, GRID)
+            nc.vector.tensor_scalar(out=written, in0=written, scalar1=EPS_CUBED, scalar2=None, op0=ALU.max)
 
         def shifted_products(b, h):
             rows = slice(HALF * h, HALF * (h + 1))
             cube = cube_ring[b % CUBES]
-            for o, (di, dj) in enumerate(OFFSETS[:RELUED]):
+            for o, (di, dj) in enumerate(OFFSETS):
                 n_lines = GRID + di
                 nc.vector.tensor_tensor(
                     out=terms_of(b, o, rows, -di, n_lines).rearrange("p k (i j) -> p k i j", j=GRID),
@@ -350,31 +320,12 @@ def tile_tokenmudule_pa_t_kernel(tc, patch_tokens, fc1_w, fc1_b, out):
 
         def relu_terms(b, h):
             weight = tiles["weight", b]
-            for o, (di, dj) in enumerate(OFFSETS[:RELUED]):
+            for o, (di, dj) in enumerate(OFFSETS):
                 for k in range(HALF * h, HALF * (h + 1)):
                     written = terms_of(b, o, k, -di, GRID + di)
                     nc.scalar.activation(
                         out=written, in_=written, func=ACT.Relu, scale=weight[:, o, k : k + 1], bias=eps_minus[:]
                     )
-
-        def vector_terms(b, h):
-            weight = tiles["weight", b]
-            cube = cube_ring[b % CUBES]
-            for o in range(RELUED, SHIFTS):
-                di, dj = OFFSETS[o]
-                for k in range(HALF * h, HALF * (h + 1)):
-                    nc.vector.scalar_tensor_tensor(
-                        out=terms_of(b, o, k, -di, GRID + di).rearrange("p (i j) -> p i j", j=GRID),
-                        in0=line(cube, k, -di, GRID + di, PITCH * di + dj),
-                        scalar=weight[:, o, k : k + 1],
-                        in1=line(cube, k, -di, GRID + di, 0),
-                        op0=ALU.mult,
-                        op1=ALU.mult,
-                    )
-                if o > RELUED:
-                    floor_terms(b, o - 1, slice(HALF * h, HALF * (h + 1)))
-            if RELUED < SHIFTS:
-                floor_terms(b, LEFT, slice(HALF * h, HALF * (h + 1)))
 
         def rest_first(p):
             nc.vector.reduce_sum(
@@ -569,71 +520,63 @@ def tile_tokenmudule_pa_t_kernel(tc, patch_tokens, fc1_w, fc1_b, out):
             of_window(load_again, m - 2, 0)
             of_window(load_again, m - 2, 1)
             of_image(load, i + 2)
-            of_image(shifted_products, i - 2, 0)
+            of_image(scaled_norms_first, i - 1)
             of_image(squares, i)
-            of_image(shifted_products, i - 2, 1)
-            of_image(sum_products, i - 1, 5)
-            of_image(sum_products, i - 1, 6)
-            of_window(quantise, m - 4, 2)
-            of_window(quantise, m - 4, 3)
-            of_window(root_ln, m - 2, 2, 0)
-            of_window(sum_terms, m - 2, 2, 1)
-            of_window(root_ln, m - 2, 1, 1)
-            of_image(scaled_folds, i - 1)
-            of_image(scaled_sums, i - 1)
-            of_image(mean_square, i)
+            of_image(shifted_products, i - 2, 0)
             of_image(scaled_norms_second, i - 1)
-            of_image(row_scale, i)
-            of_pair(length_floor, m - 3)
-            of_pair(length_ln, m - 3)
             of_image(weights_ln, i - 2)
             of_image(weights_ln, i - 1)
-            of_window(root_ln, m - 2, 2, 1)
+            of_image(mean_square, i)
+            of_image(weights_sum, i - 2)
+            of_image(row_scale, i)
+            of_image(weights_sum, i - 1)
+            of_window(regroup, m - 4, 2)
+            of_window(normalise, m - 4, 3)
+            of_window(transpose_back, m - 4, 3)
+            of_window(regroup, m - 4, 3)
+            of_pair(length_floor, m - 3)
             of_image(cubes, i)
             of_image(transpose_in, i + 1)
+            of_pair(length_ln, m - 3)
+            of_window(root_ln, m - 2, 2, 1)
+            of_window(quantise, m - 4, 2)
+            of_window(quantise, m - 4, 3)
+            of_window(project, m - 4, 2)
+            of_window(project, m - 4, 3)
             of_image(window_products, i, 0)
             of_image(window_products, i, 1)
-            of_image(weights_sum, i - 2)
-            of_image(weights_sum, i - 1)
             of_window(root_exp, m - 2, 0)
             of_image(weights_exp, i - 2)
             of_image(weights_exp, i - 1)
             of_pair(length_exp, m - 3)
             of_window(root_exp, m - 2, 1)
             of_window(root_exp, m - 2, 2)
-            of_image(window_products, i, 2)
-            of_window(project, m - 4, 2)
-            of_window(project, m - 4, 3)
+            of_image(shifted_products, i - 2, 1)
             of_pair(finish, m - 4)
-            of_image(fold, i)
             of_pair(gelu, m - 4)
             of_image(centre_square, i - 2)
-            of_image(window_products, i, 3)
-            of_image(window_products, i, 4)
             of_image(relu_terms, i - 2, 0)
-            of_image(vector_terms, i - 2, 0)
+            of_image(window_sums, i, 2)
             of_image(centre_floor, i - 2)
             of_window(sum_terms, m - 1, 0, 0)
-            of_image(sum_products, i, 3)
-            of_image(sum_products, i, 4)
-            of_image(vector_terms, i - 2, 1)
-            of_window(residual, m - 2, 0)
-            of_window(normalise, m - 3, 0)
-            of_window(transpose_back, m - 3, 0)
-            of_window(residual, m - 2, 1)
-            of_window(normalise, m - 3, 1)
-            of_image(window_products, i, 5)
+            of_image(window_sums, i, 3)
             of_image(relu_terms, i - 2, 1)
-            of_image(fold_out, i)
+            of_window(normalise, m - 3, 0)
+            of_window(residual, m - 2, 0)
+            of_window(transpose_back, m - 3, 0)
+            of_window(normalise, m - 3, 1)
+            of_window(residual, m - 2, 1)
+            of_window(sum_terms, m - 1, 0, 1)
+            of_image(sum_products, i, 0)
+            of_image(sum_products, i, 1)
+            of_image(window_sums, i, 4)
             of_window(token_norms, m - 2, 0)
             of_window(regroup, m - 3, 0)
-            of_image(window_products, i, 6)
-            of_image(fold_sum, i)
-            of_window(sum_terms, m - 1, 0, 1)
-            of_window(token_norms, m - 2, 1)
-            of_window(quantise, m - 3, 0)
-            of_window(root_ln, m - 1, 0, 0)
             of_window(transpose_back, m - 3, 1)
+            of_image(window_sums, i, 5)
+            of_window(token_norms, m - 2, 1)
+            of_image(window_sums, i, 6)
+            of_window(root_ln, m - 1, 0, 0)
 
         def odd_step(i, m):
             of_window(load_again, m - 2, 2)
@@ -648,53 +591,45 @@ def tile_tokenmudule_pa_t_kernel(tc, patch_tokens, fc1_w, fc1_b, out):
             of_window(token_norms, m - 2, 3)
             of_image(shifted_products, i - 2, 0)
             of_image(centre_square, i - 2)
-            of_image(squares, i)
-            of_image(shifted_products, i - 2, 1)
-            of_window(project, m - 3, 0)
             of_image(relu_terms, i - 2, 0)
-            of_image(vector_terms, i - 2, 0)
+            of_image(shifted_products, i - 2, 1)
             of_image(centre_floor, i - 2)
             of_window(sum_terms, m - 1, 1, 0)
-            of_image(scaled_folds, i - 1)
+            of_window(sum_terms, m - 1, 2, 0)
+            of_image(squares, i)
+            of_image(relu_terms, i - 2, 1)
+            of_window(quantise, m - 3, 0)
+            of_window(residual, m - 2, 2)
+            of_image(scaled_norms_first, i - 1)
+            of_window(normalise, m - 3, 2)
             of_image(mean_square, i)
-            of_image(sum_products, i - 1, 5)
+            of_image(scaled_norms_second, i - 1)
             of_image(row_scale, i)
-            of_image(sum_products, i - 1, 6)
+            of_window(regroup, m - 3, 1)
             of_image(cubes, i)
+            of_window(project, m - 3, 0)
             of_image(transpose_in, i + 1)
-            of_window(root_ln, m - 1, 0, 1)
+            of_window(sum_terms, m - 1, 1, 1)
             of_image(window_products, i, 0)
             of_image(window_products, i, 1)
-            of_image(window_products, i, 2)
-            of_image(fold, i)
-            of_image(vector_terms, i - 2, 1)
-            of_window(regroup, m - 3, 1)
-            of_image(window_products, i, 3)
-            of_image(relu_terms, i - 2, 1)
-            of_image(scaled_sums, i - 1)
-            of_image(window_products, i, 4)
-            of_image(scaled_norms_second, i - 1)
-            of_window(sum_terms, m - 1, 2, 0)
-            of_window(residual, m - 2, 2)
-            of_window(normalise, m - 3, 2)
-            of_window(transpose_back, m - 3, 2)
-            of_image(sum_products, i, 3)
-            of_image(sum_products, i, 4)
-            of_pair(rest_first, m - 1)
-            of_pair(rest_second, m - 1)
-            of_image(window_products, i, 5)
-            of_window(quantise, m - 3, 1)
-            of_image(fold_out, i)
-            of_image(fold_sum, i)
-            of_window(project, m - 3, 1)
-            of_image(window_products, i, 6)
+            of_window(root_ln, m - 1, 0, 1)
             of_window(token_norms, m - 2, 2)
-            of_window(regroup, m - 3, 2)
+            of_pair(rest_first, m - 1)
             of_window(root_ln, m - 1, 1, 0)
-            of_window(sum_terms, m - 1, 1, 1)
-            of_window(normalise, m - 3, 3)
-            of_window(transpose_back, m - 3, 3)
-            of_window(regroup, m - 3, 3)
+            of_image(window_sums, i, 2)
+            of_pair(rest_second, m - 1)
+            of_window(root_ln, m - 1, 2, 0)
+            of_window(sum_terms, m - 1, 2, 1)
+            of_image(sum_products, i, 0)
+            of_image(sum_products, i, 1)
+            of_window(quantise, m - 3, 1)
+            of_window(transpose_back, m - 3, 2)
+            of_image(window_sums, i, 3)
+            of_image(window_sums, i, 4)
+            of_window(project, m - 3, 1)
+            of_image(window_sums, i, 5)
+            of_window(root_ln, m - 1, 1, 1)
+            of_image(window_sums, i, 6)
 
         load(0)
         load(1)
@@ -702,6 +637,4 @@ def tile_tokenmudule_pa_t_kernel(tc, patch_tokens, fc1_w, fc1_b, out):
         LAST = 10
         for i in range(IMAGES + LAST):
             with ExitStack() as pinned:
-                if LAST <= i < IMAGES:
-                    pinned.enter_context(tc.manual_schedule())
                 (odd_step if i % 2 else even_step)(i, i // 2)

@@ -34,7 +34,11 @@ SHIFTS = len(OFFSETS)
 LEFT = SHIFTS - 1
 CENTRE = SHIFTS
 WINDOW = 9
-SUMMED = 2
+RELUED = 4
+LAST_RELUED = 4
+FOLDED = 1
+PRODUCTS = 2
+SUMMED = 6
 
 EPS_CUBED = 1e-18
 FLOOR_SQUARED = 1e-24
@@ -59,7 +63,7 @@ def tile_tokenmudule_pa_t_kernel(tc, patch_tokens, fc1_w, fc1_b, out):
         work = ctx.enter_context(tc.tile_pool(name="work", bufs=2))
         small = ctx.enter_context(tc.tile_pool(name="small", bufs=4))
         psum_io = ctx.enter_context(tc.psum_pool(name="psum_io", bufs=2))
-        psum_t = ctx.enter_context(tc.psum_pool(name="psum_t", bufs=4))
+        psum_t = ctx.enter_context(tc.psum_pool(name="psum_t", bufs=3))
         psum_1 = ctx.enter_context(tc.psum_pool(name="psum_1", bufs=1))
 
         ident_f32 = const.tile([P, P], F32, name="ident_f32")
@@ -74,6 +78,12 @@ def tile_tokenmudule_pa_t_kernel(tc, patch_tokens, fc1_w, fc1_b, out):
         nc.vector.memset(eps_minus[:], -EPS_CUBED)
         eps_in_mean = const.tile([P, 1], F32, name="eps_in_mean")
         nc.vector.memset(eps_in_mean[:], EPS_CUBED * (WINDOW - 1) / WINDOW)
+
+        member = const.tile([P, BLOCKS], F32, name="member")
+        nc.vector.reduce_sum(
+            out=member[:], in_=ident_f32[:].rearrange("p (k i) -> p k i", k=BLOCKS), axis=mybir.AxisListType.X
+        )
+
         bias_bf = const.tile([P, FEATURES], BF16, name="bias_bf")
         nc.sync.dma_start(out=bias_bf[:], in_=fc1_b.partition_broadcast(P))
         bias = const.tile([P, FEATURES], F32, name="bias")
@@ -210,7 +220,7 @@ def tile_tokenmudule_pa_t_kernel(tc, patch_tokens, fc1_w, fc1_b, out):
 
         def window_products(b, o):
             here, there, length = grid_part(square_ring[b % SQUARES], slice(0, BLOCKS), o)
-            product = work.tile([P, BLOCKS, TOKENS], F32, name="product")
+            product = work.tile([P, BLOCKS, TOKENS], F32, name="product", bufs=PRODUCTS)
             nc.vector.tensor_tensor(
                 out=product[:, :, 0:length].rearrange("p k (i j) -> p k i j", i=GRID + OFFSETS[o][0]),
                 in0=here,
@@ -230,6 +240,46 @@ def tile_tokenmudule_pa_t_kernel(tc, patch_tokens, fc1_w, fc1_b, out):
                     accum_out=tiles["norm_sq", b][:, o, k : k + 1],
                 )
 
+        def fold_products(b, o):
+            di, dj = OFFSETS[o]
+            n_lines = GRID + di
+            every = slice(0, BLOCKS)
+            x_sq = square_ring[b % SQUARES]
+            product = work.tile([P, GRID, BLOCKS, PITCH], F32, name="product_fold", bufs=FOLDED)
+            nc.vector.tensor_tensor(
+                out=product[:, 0:n_lines, :, :].rearrange("p i k j -> p k i j"),
+                in0=lines(x_sq, every, -di, n_lines, 0, PITCH),
+                in1=lines(x_sq, every, -di, n_lines, PITCH * di + dj, PITCH),
+                op=ALU.mult,
+            )
+            tiles["products", b, o] = product
+
+        def fold(b, o):
+            if o == 0:
+                tiles["folded", b] = psum_1.tile([P, HALF, P], F32, name="folded")
+            n_lines = GRID + OFFSETS[o][0]
+            for i in range(n_lines):
+                nc.tensor.matmul(
+                    out=tiles["folded", b][:, o, :],
+                    lhsT=tiles["products", b, o][:, i, :, :].rearrange("p k j -> p (k j)"),
+                    rhs=ident_f32[:],
+                    is_transpose=True,
+                    start=(i == 0),
+                    stop=(i == n_lines - 1),
+                )
+
+        def fold_out(b):
+            partial = work.tile([P, FOLDED, P], F32, name="partial", bufs=1)
+            nc.scalar.copy(out=partial[:], in_=tiles["folded", b][:, 0:FOLDED, :])
+            tiles["partial", b] = partial
+
+        def fold_sum(b):
+            partial = tiles["partial", b]
+            norms = tiles["folded", b][:, HALF - 1, 0 : FOLDED * BLOCKS].rearrange("p (o k) -> p o k", k=BLOCKS)
+            for o in range(FOLDED):
+                nc.tensor.matmul(out=norms[:, o, :], lhsT=partial[:, o, :], rhs=member[:], start=True, stop=True)
+            tiles["norms", b] = norms
+
         def window_sums(b, o):
             for k in range(BLOCKS):
                 here, there, length = grid_part(square_ring[b % SQUARES], slice(k, k + 1), o)
@@ -246,14 +296,18 @@ def tile_tokenmudule_pa_t_kernel(tc, patch_tokens, fc1_w, fc1_b, out):
 
         def scaled_norms_first(b):
             scaled = tiles["scaled", b]
-            nc.vector.scalar_tensor_tensor(
-                out=scaled[:, 0 : CENTRE + 1, :],
-                in0=tiles["norm_sq", b][:],
-                scalar=FLOOR_SQUARED,
-                in1=scaled[:, CENTRE + 1, :].unsqueeze(1).to_broadcast([P, CENTRE + 1, BLOCKS]),
-                op0=ALU.max,
-                op1=ALU.mult,
-            )
+            for first, last, norms in (
+                (0, FOLDED, tiles["norms", b]),
+                (FOLDED, CENTRE + 1, tiles["norm_sq", b][:, FOLDED : CENTRE + 1, :]),
+            ):
+                nc.vector.scalar_tensor_tensor(
+                    out=scaled[:, first:last, :],
+                    in0=norms,
+                    scalar=FLOOR_SQUARED,
+                    in1=scaled[:, CENTRE + 1, :].unsqueeze(1).to_broadcast([P, last - first, BLOCKS]),
+                    op0=ALU.max,
+                    op1=ALU.mult,
+                )
 
         def scaled_norms_second(b):
             scaled = tiles["scaled", b]
@@ -289,6 +343,9 @@ def tile_tokenmudule_pa_t_kernel(tc, patch_tokens, fc1_w, fc1_b, out):
             tiles["weight", b] = weight
             tiles["centre_scale", b] = centre_scale
 
+        def relued(b):
+            return LAST_RELUED if b // 2 == PAIRS - 1 else RELUED
+
         def terms_of(b, o, k, first_line, n_lines):
             first = TOKENS * (b % 2) + GRID * first_line
             return term[:, o, k, first : first + GRID * n_lines]
@@ -309,7 +366,8 @@ def tile_tokenmudule_pa_t_kernel(tc, patch_tokens, fc1_w, fc1_b, out):
         def shifted_products(b, h):
             rows = slice(HALF * h, HALF * (h + 1))
             cube = cube_ring[b % CUBES]
-            for o, (di, dj) in enumerate(OFFSETS):
+            for o in range(relued(b)):
+                di, dj = OFFSETS[o]
                 n_lines = GRID + di
                 nc.vector.tensor_tensor(
                     out=terms_of(b, o, rows, -di, n_lines).rearrange("p k (i j) -> p k i j", j=GRID),
@@ -320,12 +378,38 @@ def tile_tokenmudule_pa_t_kernel(tc, patch_tokens, fc1_w, fc1_b, out):
 
         def relu_terms(b, h):
             weight = tiles["weight", b]
-            for o, (di, dj) in enumerate(OFFSETS):
-                for k in range(HALF * h, HALF * (h + 1)):
+            for k in range(HALF * h, HALF * (h + 1)):
+                for o in range(relued(b)):
+                    di = OFFSETS[o][0]
                     written = terms_of(b, o, k, -di, GRID + di)
                     nc.scalar.activation(
                         out=written, in_=written, func=ACT.Relu, scale=weight[:, o, k : k + 1], bias=eps_minus[:]
                     )
+
+        def vector_terms(b, h):
+            weight = tiles["weight", b]
+            cube = cube_ring[b % CUBES]
+            rows = slice(HALF * h, HALF * (h + 1))
+            for o in range(relued(b), SHIFTS):
+                di, dj = OFFSETS[o]
+                for k in range(HALF * h, HALF * (h + 1)):
+                    nc.vector.scalar_tensor_tensor(
+                        out=terms_of(b, o, k, -di, GRID + di).rearrange("p (i j) -> p i j", j=GRID),
+                        in0=line(cube, k, -di, GRID + di, PITCH * di + dj),
+                        scalar=weight[:, o, k : k + 1],
+                        in1=line(cube, k, -di, GRID + di, 0),
+                        op0=ALU.mult,
+                        op1=ALU.mult,
+                    )
+                written = terms_of(b, o, rows, -di, GRID + di)
+                nc.vector.tensor_scalar(
+                    out=written,
+                    in0=written,
+                    scalar1=EPS_CUBED,
+                    scalar2=EPS_CUBED,
+                    op0=ALU.max,
+                    op1=ALU.subtract,
+                )
 
         def rest_first(p):
             nc.vector.reduce_sum(
@@ -504,6 +588,17 @@ def tile_tokenmudule_pa_t_kernel(tc, patch_tokens, fc1_w, fc1_b, out):
                         in_=result[REST * q : REST * (q + 1), WHOLE * GROUP, :],
                     )
 
+        def window_norms(b):
+            for o in range(SHIFTS):
+                if o < FOLDED:
+                    fold_products(b, o)
+                    fold(b, o)
+                elif o < FOLDED + SUMMED:
+                    window_products(b, o)
+                    sum_products(b, o)
+                else:
+                    window_sums(b, o)
+
         def of_image(stage, b, *more):
             if 0 <= b < IMAGES:
                 stage(b, *more)
@@ -520,63 +615,72 @@ def tile_tokenmudule_pa_t_kernel(tc, patch_tokens, fc1_w, fc1_b, out):
             of_window(load_again, m - 2, 0)
             of_window(load_again, m - 2, 1)
             of_image(load, i + 2)
-            of_image(scaled_norms_first, i - 1)
-            of_image(squares, i)
+            of_image(sum_products, i - 1, 5)
+            of_image(sum_products, i - 1, 6)
             of_image(shifted_products, i - 2, 0)
-            of_image(scaled_norms_second, i - 1)
-            of_image(weights_ln, i - 2)
-            of_image(weights_ln, i - 1)
-            of_image(mean_square, i)
-            of_image(weights_sum, i - 2)
-            of_image(row_scale, i)
-            of_image(weights_sum, i - 1)
+            of_image(squares, i)
+            of_image(shifted_products, i - 2, 1)
+            of_image(scaled_norms_first, i - 1)
             of_window(regroup, m - 4, 2)
+            of_image(scaled_norms_second, i - 1)
             of_window(normalise, m - 4, 3)
             of_window(transpose_back, m - 4, 3)
             of_window(regroup, m - 4, 3)
-            of_pair(length_floor, m - 3)
-            of_image(cubes, i)
-            of_image(transpose_in, i + 1)
-            of_pair(length_ln, m - 3)
-            of_window(root_ln, m - 2, 2, 1)
             of_window(quantise, m - 4, 2)
             of_window(quantise, m - 4, 3)
             of_window(project, m - 4, 2)
             of_window(project, m - 4, 3)
-            of_image(window_products, i, 0)
-            of_image(window_products, i, 1)
+            of_window(root_ln, m - 2, 1, 1)
+            of_pair(length_floor, m - 3)
+            of_image(weights_ln, i - 2)
+            of_image(weights_ln, i - 1)
+            of_image(mean_square, i)
+            of_pair(length_ln, m - 3)
+            of_image(row_scale, i)
+            of_window(root_ln, m - 2, 2, 1)
+            of_image(weights_sum, i - 2)
+            of_image(weights_sum, i - 1)
+            of_image(cubes, i)
+            of_image(transpose_in, i + 1)
             of_window(root_exp, m - 2, 0)
             of_image(weights_exp, i - 2)
             of_image(weights_exp, i - 1)
             of_pair(length_exp, m - 3)
             of_window(root_exp, m - 2, 1)
             of_window(root_exp, m - 2, 2)
-            of_image(shifted_products, i - 2, 1)
             of_pair(finish, m - 4)
+            of_image(fold_products, i, 0)
+            of_image(window_products, i, 1)
+            of_image(window_products, i, 2)
             of_pair(gelu, m - 4)
+            of_image(fold, i, 0)
             of_image(centre_square, i - 2)
             of_image(relu_terms, i - 2, 0)
-            of_image(window_sums, i, 2)
+            of_image(vector_terms, i - 2, 0)
             of_image(centre_floor, i - 2)
             of_window(sum_terms, m - 1, 0, 0)
-            of_image(window_sums, i, 3)
-            of_image(relu_terms, i - 2, 1)
-            of_window(normalise, m - 3, 0)
-            of_window(residual, m - 2, 0)
-            of_window(transpose_back, m - 3, 0)
-            of_window(normalise, m - 3, 1)
-            of_window(residual, m - 2, 1)
-            of_window(sum_terms, m - 1, 0, 1)
-            of_image(sum_products, i, 0)
+            of_image(vector_terms, i - 2, 1)
             of_image(sum_products, i, 1)
-            of_image(window_sums, i, 4)
+            of_image(sum_products, i, 2)
+            of_window(residual, m - 2, 0)
+            of_window(normalise, m - 3, 0)
+            of_window(transpose_back, m - 3, 0)
+            of_image(window_products, i, 3)
+            of_window(normalise, m - 3, 1)
+            of_image(relu_terms, i - 2, 1)
+            of_image(window_products, i, 4)
+            of_window(sum_terms, m - 1, 0, 1)
+            of_image(fold_out, i)
+            of_image(sum_products, i, 3)
+            of_window(residual, m - 2, 1)
+            of_image(fold_sum, i)
+            of_image(sum_products, i, 4)
+            of_image(window_products, i, 5)
             of_window(token_norms, m - 2, 0)
             of_window(regroup, m - 3, 0)
-            of_window(transpose_back, m - 3, 1)
-            of_image(window_sums, i, 5)
-            of_window(token_norms, m - 2, 1)
-            of_image(window_sums, i, 6)
             of_window(root_ln, m - 1, 0, 0)
+            of_window(transpose_back, m - 3, 1)
+            of_image(window_products, i, 6)
 
         def odd_step(i, m):
             of_window(load_again, m - 2, 2)
@@ -590,51 +694,60 @@ def tile_tokenmudule_pa_t_kernel(tc, patch_tokens, fc1_w, fc1_b, out):
             of_window(residual, m - 2, 3)
             of_window(token_norms, m - 2, 3)
             of_image(shifted_products, i - 2, 0)
+            of_image(sum_products, i - 1, 5)
+            of_image(sum_products, i - 1, 6)
             of_image(centre_square, i - 2)
             of_image(relu_terms, i - 2, 0)
+            of_image(vector_terms, i - 2, 0)
+            of_window(root_ln, m - 1, 0, 1)
+            of_window(quantise, m - 3, 0)
             of_image(shifted_products, i - 2, 1)
             of_image(centre_floor, i - 2)
             of_window(sum_terms, m - 1, 1, 0)
-            of_window(sum_terms, m - 1, 2, 0)
             of_image(squares, i)
-            of_image(relu_terms, i - 2, 1)
-            of_window(quantise, m - 3, 0)
-            of_window(residual, m - 2, 2)
+            of_image(vector_terms, i - 2, 1)
             of_image(scaled_norms_first, i - 1)
+            of_window(project, m - 3, 0)
+            of_window(residual, m - 2, 2)
+            of_image(relu_terms, i - 2, 1)
+            of_image(scaled_norms_second, i - 1)
             of_window(normalise, m - 3, 2)
             of_image(mean_square, i)
-            of_image(scaled_norms_second, i - 1)
+            of_window(sum_terms, m - 1, 2, 0)
+            of_pair(rest_first, m - 1)
             of_image(row_scale, i)
+            of_pair(rest_second, m - 1)
             of_window(regroup, m - 3, 1)
             of_image(cubes, i)
-            of_window(project, m - 3, 0)
+            of_window(token_norms, m - 2, 1)
             of_image(transpose_in, i + 1)
+            of_window(transpose_back, m - 3, 2)
             of_window(sum_terms, m - 1, 1, 1)
-            of_image(window_products, i, 0)
+            of_image(fold_products, i, 0)
             of_image(window_products, i, 1)
-            of_window(root_ln, m - 1, 0, 1)
+            of_image(window_products, i, 2)
+            of_window(quantise, m - 3, 1)
             of_window(token_norms, m - 2, 2)
-            of_pair(rest_first, m - 1)
+            of_image(sum_products, i, 1)
+            of_image(window_products, i, 3)
+            of_image(sum_products, i, 2)
+            of_image(window_products, i, 4)
             of_window(root_ln, m - 1, 1, 0)
-            of_image(window_sums, i, 2)
-            of_pair(rest_second, m - 1)
+            of_image(fold, i, 0)
+            of_window(project, m - 3, 1)
             of_window(root_ln, m - 1, 2, 0)
             of_window(sum_terms, m - 1, 2, 1)
-            of_image(sum_products, i, 0)
-            of_image(sum_products, i, 1)
-            of_window(quantise, m - 3, 1)
-            of_window(transpose_back, m - 3, 2)
-            of_image(window_sums, i, 3)
-            of_image(window_sums, i, 4)
-            of_window(project, m - 3, 1)
-            of_image(window_sums, i, 5)
-            of_window(root_ln, m - 1, 1, 1)
-            of_image(window_sums, i, 6)
+            of_image(sum_products, i, 3)
+            of_image(window_products, i, 5)
+            of_image(fold_out, i)
+            of_image(fold_sum, i)
+            of_image(sum_products, i, 4)
+            of_image(window_products, i, 6)
 
         load(0)
         load(1)
         transpose_in(0)
         LAST = 10
-        for i in range(IMAGES + LAST):
-            with ExitStack() as pinned:
+        with tc.manual_schedule(engines={mybir.EngineType.Activation}):
+            for i in range(IMAGES + LAST):
                 (odd_step if i % 2 else even_step)(i, i // 2)

@@ -34,11 +34,11 @@ SHIFTS = len(OFFSETS)
 LEFT = SHIFTS - 1
 CENTRE = SHIFTS
 WINDOW = 9
-RELUED = 4
-LAST_RELUED = 4
-FOLDED = 1
+RELUED = (5, 5)
+FOLDED = 2
+FOLD_BUFS = 2
 PRODUCTS = 2
-SUMMED = 6
+JUNK = 4
 
 EPS_CUBED = 1e-18
 FLOOR_SQUARED = 1e-24
@@ -102,7 +102,7 @@ def tile_tokenmudule_pa_t_kernel(tc, patch_tokens, fc1_w, fc1_b, out):
             in_=w_grouped[:].rearrange("p g n t -> p (g n t)"),
         )
 
-        SQUARES = 2
+        SQUARES = 1
         square_ring = [const.tile([P, BLOCKS, ROW], F32, name="square%d" % n) for n in range(SQUARES)]
         CUBES = 3
         cube_ring = [const.tile([P, BLOCKS, ROW], F32, name="cube%d" % n) for n in range(CUBES)]
@@ -115,7 +115,6 @@ def tile_tokenmudule_pa_t_kernel(tc, patch_tokens, fc1_w, fc1_b, out):
                     nc.vector.memset(term[:, o, :, first : first - di * GRID], 0.0)
         nc.vector.memset(term[:, LEFT, :, PAIR : PAIR + 1], 0.0)
         rest = const.tile([P, BLOCKS, P], F32, name="rest")
-        JUNK = 4
         junk_row = const.tile([P, JUNK, TOKENS], BF16, name="junk_row")
         junk_f32 = const.tile([P, JUNK, TOKENS], F32, name="junk_f32")
         junk_wide = const.tile([P, CHANNELS], BF16, name="junk_wide")
@@ -245,7 +244,7 @@ def tile_tokenmudule_pa_t_kernel(tc, patch_tokens, fc1_w, fc1_b, out):
             n_lines = GRID + di
             every = slice(0, BLOCKS)
             x_sq = square_ring[b % SQUARES]
-            product = work.tile([P, GRID, BLOCKS, PITCH], F32, name="product_fold", bufs=FOLDED)
+            product = work.tile([P, GRID, BLOCKS, PITCH], F32, name="product_fold", bufs=FOLD_BUFS)
             nc.vector.tensor_tensor(
                 out=product[:, 0:n_lines, :, :].rearrange("p i k j -> p k i j"),
                 in0=lines(x_sq, every, -di, n_lines, 0, PITCH),
@@ -283,9 +282,8 @@ def tile_tokenmudule_pa_t_kernel(tc, patch_tokens, fc1_w, fc1_b, out):
         def window_sums(b, o):
             for k in range(BLOCKS):
                 here, there, length = grid_part(square_ring[b % SQUARES], slice(k, k + 1), o)
-                out_row = junk_f32[:, k % JUNK, 0:length].rearrange("p (a i j) -> p a i j", a=1, i=GRID + OFFSETS[o][0])
                 nc.vector.scalar_tensor_tensor(
-                    out=out_row,
+                    out=junk_f32[:, k % JUNK, 0:length].rearrange("p (a i j) -> p a i j", a=1, i=GRID + OFFSETS[o][0]),
                     in0=here,
                     scalar=1.0,
                     in1=there,
@@ -343,8 +341,8 @@ def tile_tokenmudule_pa_t_kernel(tc, patch_tokens, fc1_w, fc1_b, out):
             tiles["weight", b] = weight
             tiles["centre_scale", b] = centre_scale
 
-        def relued(b):
-            return LAST_RELUED if b // 2 == PAIRS - 1 else RELUED
+        def relued(b, h):
+            return RELUED[h]
 
         def terms_of(b, o, k, first_line, n_lines):
             first = TOKENS * (b % 2) + GRID * first_line
@@ -366,7 +364,7 @@ def tile_tokenmudule_pa_t_kernel(tc, patch_tokens, fc1_w, fc1_b, out):
         def shifted_products(b, h):
             rows = slice(HALF * h, HALF * (h + 1))
             cube = cube_ring[b % CUBES]
-            for o in range(relued(b)):
+            for o in range(relued(b, h)):
                 di, dj = OFFSETS[o]
                 n_lines = GRID + di
                 nc.vector.tensor_tensor(
@@ -379,18 +377,24 @@ def tile_tokenmudule_pa_t_kernel(tc, patch_tokens, fc1_w, fc1_b, out):
         def relu_terms(b, h):
             weight = tiles["weight", b]
             for k in range(HALF * h, HALF * (h + 1)):
-                for o in range(relued(b)):
+                for o in range(relued(b, h)):
                     di = OFFSETS[o][0]
                     written = terms_of(b, o, k, -di, GRID + di)
                     nc.scalar.activation(
                         out=written, in_=written, func=ACT.Relu, scale=weight[:, o, k : k + 1], bias=eps_minus[:]
                     )
 
+        def vector_floor(b, h, o):
+            di = OFFSETS[o][0]
+            written = terms_of(b, o, slice(HALF * h, HALF * (h + 1)), -di, GRID + di)
+            nc.vector.tensor_scalar(
+                out=written, in0=written, scalar1=EPS_CUBED, scalar2=EPS_CUBED, op0=ALU.max, op1=ALU.subtract
+            )
+
         def vector_terms(b, h):
             weight = tiles["weight", b]
             cube = cube_ring[b % CUBES]
-            rows = slice(HALF * h, HALF * (h + 1))
-            for o in range(relued(b), SHIFTS):
+            for o in range(relued(b, h), SHIFTS):
                 di, dj = OFFSETS[o]
                 for k in range(HALF * h, HALF * (h + 1)):
                     nc.vector.scalar_tensor_tensor(
@@ -401,15 +405,10 @@ def tile_tokenmudule_pa_t_kernel(tc, patch_tokens, fc1_w, fc1_b, out):
                         op0=ALU.mult,
                         op1=ALU.mult,
                     )
-                written = terms_of(b, o, rows, -di, GRID + di)
-                nc.vector.tensor_scalar(
-                    out=written,
-                    in0=written,
-                    scalar1=EPS_CUBED,
-                    scalar2=EPS_CUBED,
-                    op0=ALU.max,
-                    op1=ALU.subtract,
-                )
+                if o > relued(b, h):
+                    vector_floor(b, h, o - 1)
+            if relued(b, h) < SHIFTS:
+                vector_floor(b, h, SHIFTS - 1)
 
         def rest_first(p):
             nc.vector.reduce_sum(
@@ -447,7 +446,7 @@ def tile_tokenmudule_pa_t_kernel(tc, patch_tokens, fc1_w, fc1_b, out):
 
         def root_ln(p, w, h):
             if h == 0:
-                tiles["r_t", p, w] = work.tile([P, CHANNELS], F32, name="r_t", bufs=6)
+                tiles["r_t", p, w] = work.tile([P, CHANNELS], F32, name="r_t", bufs=7)
             nc.scalar.activation(
                 out=tiles["r_t", p, w][:, BANK * h : BANK * (h + 1)].rearrange("p (u c e) -> p u c e", u=2, e=2),
                 in_=tiles["total_t", p, w, h][:].rearrange("p (u e) c -> p u c e", e=2),
@@ -513,7 +512,8 @@ def tile_tokenmudule_pa_t_kernel(tc, patch_tokens, fc1_w, fc1_b, out):
 
         def transpose_back(p, w):
             words = tiles["tok_t", p, w][:].bitcast(F32)
-            tok_c = psum_1.tile([P, PASSES, 2, P], F32, name="tok_c")
+            pool, tag = (psum_t, "total_t") if p == PAIRS - 1 else (psum_1, "tok_c")
+            tok_c = pool.tile([P, PASSES, 2, P], F32, name="tok_c", tag=tag)
             for g in range(PASSES):
                 for u in range(2):
                     nc.tensor.transpose(
@@ -560,7 +560,7 @@ def tile_tokenmudule_pa_t_kernel(tc, patch_tokens, fc1_w, fc1_b, out):
             n = WHOLE * (p % GROUP)
             count = len(windows(p))
             if n == 0:
-                tiles["result", p // GROUP] = work.tile([P, WHOLE * GROUP + 1, FEATURES], F32, name="result")
+                tiles["result", p // GROUP] = work.tile([P, WHOLE * GROUP + 1, FEATURES], F32, name="result", bufs=1)
             nc.vector.tensor_tensor(
                 out=tiles["result", p // GROUP][:, n : n + count, :],
                 in0=tiles["projected", p][:, 0:count, :],
@@ -588,17 +588,6 @@ def tile_tokenmudule_pa_t_kernel(tc, patch_tokens, fc1_w, fc1_b, out):
                         in_=result[REST * q : REST * (q + 1), WHOLE * GROUP, :],
                     )
 
-        def window_norms(b):
-            for o in range(SHIFTS):
-                if o < FOLDED:
-                    fold_products(b, o)
-                    fold(b, o)
-                elif o < FOLDED + SUMMED:
-                    window_products(b, o)
-                    sum_products(b, o)
-                else:
-                    window_sums(b, o)
-
         def of_image(stage, b, *more):
             if 0 <= b < IMAGES:
                 stage(b, *more)
@@ -616,7 +605,6 @@ def tile_tokenmudule_pa_t_kernel(tc, patch_tokens, fc1_w, fc1_b, out):
             of_window(load_again, m - 2, 1)
             of_image(load, i + 2)
             of_image(sum_products, i - 1, 5)
-            of_image(sum_products, i - 1, 6)
             of_image(shifted_products, i - 2, 0)
             of_image(squares, i)
             of_image(shifted_products, i - 2, 1)
@@ -638,6 +626,10 @@ def tile_tokenmudule_pa_t_kernel(tc, patch_tokens, fc1_w, fc1_b, out):
             of_pair(length_ln, m - 3)
             of_image(row_scale, i)
             of_window(root_ln, m - 2, 2, 1)
+            of_window(sum_terms, m - 2, 3, 0)
+            of_window(root_ln, m - 2, 3, 0)
+            of_window(sum_terms, m - 2, 3, 1)
+            of_window(root_ln, m - 2, 3, 1)
             of_image(weights_sum, i - 2)
             of_image(weights_sum, i - 1)
             of_image(cubes, i)
@@ -648,19 +640,20 @@ def tile_tokenmudule_pa_t_kernel(tc, patch_tokens, fc1_w, fc1_b, out):
             of_pair(length_exp, m - 3)
             of_window(root_exp, m - 2, 1)
             of_window(root_exp, m - 2, 2)
+            of_window(root_exp, m - 2, 3)
             of_pair(finish, m - 4)
             of_image(fold_products, i, 0)
-            of_image(window_products, i, 1)
+            of_image(fold, i, 0)
+            of_image(fold_products, i, 1)
+            of_image(fold, i, 1)
             of_image(window_products, i, 2)
             of_pair(gelu, m - 4)
-            of_image(fold, i, 0)
             of_image(centre_square, i - 2)
             of_image(relu_terms, i - 2, 0)
             of_image(vector_terms, i - 2, 0)
             of_image(centre_floor, i - 2)
             of_window(sum_terms, m - 1, 0, 0)
             of_image(vector_terms, i - 2, 1)
-            of_image(sum_products, i, 1)
             of_image(sum_products, i, 2)
             of_window(residual, m - 2, 0)
             of_window(normalise, m - 3, 0)
@@ -680,22 +673,16 @@ def tile_tokenmudule_pa_t_kernel(tc, patch_tokens, fc1_w, fc1_b, out):
             of_window(regroup, m - 3, 0)
             of_window(root_ln, m - 1, 0, 0)
             of_window(transpose_back, m - 3, 1)
-            of_image(window_products, i, 6)
+            of_image(window_sums, i, 6)
 
         def odd_step(i, m):
             of_window(load_again, m - 2, 2)
-            of_image(load, i + 2)
             of_window(load_again, m - 2, 3)
-            of_window(sum_terms, m - 2, 3, 0)
-            of_window(root_ln, m - 2, 3, 0)
-            of_window(sum_terms, m - 2, 3, 1)
-            of_window(root_ln, m - 2, 3, 1)
-            of_window(root_exp, m - 2, 3)
+            of_image(load, i + 2)
             of_window(residual, m - 2, 3)
             of_window(token_norms, m - 2, 3)
             of_image(shifted_products, i - 2, 0)
             of_image(sum_products, i - 1, 5)
-            of_image(sum_products, i - 1, 6)
             of_image(centre_square, i - 2)
             of_image(relu_terms, i - 2, 0)
             of_image(vector_terms, i - 2, 0)
@@ -724,16 +711,16 @@ def tile_tokenmudule_pa_t_kernel(tc, patch_tokens, fc1_w, fc1_b, out):
             of_window(transpose_back, m - 3, 2)
             of_window(sum_terms, m - 1, 1, 1)
             of_image(fold_products, i, 0)
-            of_image(window_products, i, 1)
+            of_image(fold, i, 0)
+            of_image(fold_products, i, 1)
+            of_image(fold, i, 1)
             of_image(window_products, i, 2)
             of_window(quantise, m - 3, 1)
             of_window(token_norms, m - 2, 2)
-            of_image(sum_products, i, 1)
             of_image(window_products, i, 3)
             of_image(sum_products, i, 2)
             of_image(window_products, i, 4)
             of_window(root_ln, m - 1, 1, 0)
-            of_image(fold, i, 0)
             of_window(project, m - 3, 1)
             of_window(root_ln, m - 1, 2, 0)
             of_window(sum_terms, m - 1, 2, 1)
@@ -742,7 +729,7 @@ def tile_tokenmudule_pa_t_kernel(tc, patch_tokens, fc1_w, fc1_b, out):
             of_image(fold_out, i)
             of_image(fold_sum, i)
             of_image(sum_products, i, 4)
-            of_image(window_products, i, 6)
+            of_image(window_sums, i, 6)
 
         load(0)
         load(1)

@@ -160,21 +160,20 @@ def tile_tokenmudule_pa_t_kernel(tc, patch_tokens, fc1_w, fc1_b, out):
         def squares(b):
             sum_sq = small.tile([P, BLOCKS], F32, name="sum_sq")
             norm_sq = small.tile([P, CENTRE + 1, BLOCKS], F32, name="norm_sq")
-            for h in range(2):
-                for k in range(HALF * h, HALF * (h + 1)):
-                    nc.scalar.activation(
-                        out=line(square_ring[b % SQUARES], k, 0, GRID, 0),
-                        in_=x_row(b, k),
-                        func=ACT.Square,
-                        accum_out=sum_sq[:, k : k + 1],
-                    )
-                for k in range(HALF * h, HALF * (h + 1)):
-                    nc.scalar.activation(
-                        out=junk_row[:, k % JUNK, :].rearrange("p (i j) -> p i j", j=GRID),
-                        in_=line(square_ring[b % SQUARES], k, 0, GRID, 0),
-                        func=ACT.Square,
-                        accum_out=norm_sq[:, CENTRE, k : k + 1],
-                    )
+            for k in range(BLOCKS):
+                nc.scalar.activation(
+                    out=line(square_ring[b % SQUARES], k, 0, GRID, 0),
+                    in_=x_row(b, k),
+                    func=ACT.Square,
+                    accum_out=sum_sq[:, k : k + 1],
+                )
+            for k in range(BLOCKS):
+                nc.scalar.activation(
+                    out=junk_row[:, k % JUNK, :].rearrange("p (i j) -> p i j", j=GRID),
+                    in_=line(square_ring[b % SQUARES], k, 0, GRID, 0),
+                    func=ACT.Square,
+                    accum_out=norm_sq[:, CENTRE, k : k + 1],
+                )
             tiles["sum_sq", b] = sum_sq
             tiles["norm_sq", b] = norm_sq
 
@@ -423,6 +422,15 @@ def tile_tokenmudule_pa_t_kernel(tc, patch_tokens, fc1_w, fc1_b, out):
                 out=total, in0=total, in1=term[:, LEFT, :, WHOLE * P + 1 : PAIR + 1], op=ALU.add
             )
 
+        def presum(p):
+            if p < PAIRS - 1:
+                return
+            for k in range(HALF, BLOCKS):
+                total = term[:, 0, k, P : WHOLE * P]
+                for o in range(1, CENTRE + 1):
+                    nc.vector.tensor_tensor(out=total, in0=total, in1=term[:, o, k, P : WHOLE * P], op=ALU.add)
+                nc.vector.tensor_tensor(out=total, in0=total, in1=term[:, LEFT, k, P + 1 : WHOLE * P + 1], op=ALU.add)
+
         def sum_terms(p, w, h):
             total_t = psum_t.tile([P, HALF, P], F32, name="total_t")
             first = P * w
@@ -430,6 +438,8 @@ def tile_tokenmudule_pa_t_kernel(tc, patch_tokens, fc1_w, fc1_b, out):
                 k = HALF * h + kk
                 if w == WHOLE:
                     addends = [rest[:, k, :]]
+                elif p == PAIRS - 1 and w > 0 and h == 1:
+                    addends = [term[:, 0, k, first : first + P]]
                 else:
                     addends = [term[:, o, k, first : first + P] for o in range(CENTRE + 1)]
                     addends.append(term[:, LEFT, k, first + 1 : first + 1 + P])
@@ -447,13 +457,16 @@ def tile_tokenmudule_pa_t_kernel(tc, patch_tokens, fc1_w, fc1_b, out):
         def root_ln(p, w, h):
             if h == 0:
                 tiles["r_t", p, w] = work.tile([P, CHANNELS], F32, name="r_t", bufs=7)
-            nc.scalar.activation(
-                out=tiles["r_t", p, w][:, BANK * h : BANK * (h + 1)].rearrange("p (u c e) -> p u c e", u=2, e=2),
-                in_=tiles["total_t", p, w, h][:].rearrange("p (u e) c -> p u c e", e=2),
-                func=ACT.Ln,
-                scale=1.0 / WINDOW,
-                bias=eps_in_mean[:],
-            )
+            r_t = tiles["r_t", p, w][:, BANK * h : BANK * (h + 1)].rearrange("p (u a c e) -> p u a c e", u=2, a=2, e=2)
+            total = tiles["total_t", p, w, h][:].rearrange("p (a e) (c u) -> p u a c e", e=2, u=2)
+            for u in range(2):
+                nc.scalar.activation(
+                    out=r_t[:, u, :, :, :],
+                    in_=total[:, u, :, :, :],
+                    func=ACT.Ln,
+                    scale=1.0 / WINDOW,
+                    bias=eps_in_mean[:],
+                )
 
         def load_again(p, w):
             x_again = loads.tile([P, CHANNELS], BF16, name="x_again", bufs=3)
@@ -472,8 +485,11 @@ def tile_tokenmudule_pa_t_kernel(tc, patch_tokens, fc1_w, fc1_b, out):
             nc.scalar.activation(out=r_t[:], in_=r_t[:], func=ACT.Exp, scale=1.0 / 3.0)
 
         def residual(p, w):
-            r_t = tiles["r_t", p, w]
-            nc.vector.tensor_tensor(out=r_t[:], in0=r_t[:], in1=tiles["x_again", p, w][:], op=ALU.add)
+            for g in range(PASSES):
+                channels = slice(BANK * g, BANK * (g + 1))
+                r_t = tiles["r_t", p, w][:, channels].rearrange("p (u c e) -> p u c e", u=2, e=2)
+                x_again = tiles["x_again", p, w][:, channels].rearrange("p (c u e) -> p u c e", u=2, e=2)
+                nc.vector.tensor_tensor(out=r_t, in0=r_t, in1=x_again, op=ALU.add)
 
         def token_norms(p, w):
             if w == 0:
@@ -517,7 +533,7 @@ def tile_tokenmudule_pa_t_kernel(tc, patch_tokens, fc1_w, fc1_b, out):
             for g in range(PASSES):
                 for u in range(2):
                     nc.tensor.transpose(
-                        tok_c[:, g, u, :], words[:, 2 * P * g + u : 2 * P * (g + 1) : 2], ident_f32[:]
+                        tok_c[:, g, u, :], words[:, P * (2 * g + u) : P * (2 * g + u + 1)], ident_f32[:]
                     )
             tiles["tok_c", p, w] = tok_c
 
@@ -604,6 +620,8 @@ def tile_tokenmudule_pa_t_kernel(tc, patch_tokens, fc1_w, fc1_b, out):
             of_window(load_again, m - 2, 0)
             of_window(load_again, m - 2, 1)
             of_image(load, i + 2)
+            of_image(fold_out, i - 1)
+            of_image(fold_sum, i - 1)
             of_image(sum_products, i - 1, 5)
             of_image(shifted_products, i - 2, 0)
             of_image(squares, i)
@@ -643,9 +661,7 @@ def tile_tokenmudule_pa_t_kernel(tc, patch_tokens, fc1_w, fc1_b, out):
             of_window(root_exp, m - 2, 3)
             of_pair(finish, m - 4)
             of_image(fold_products, i, 0)
-            of_image(fold, i, 0)
             of_image(fold_products, i, 1)
-            of_image(fold, i, 1)
             of_image(window_products, i, 2)
             of_pair(gelu, m - 4)
             of_image(centre_square, i - 2)
@@ -663,10 +679,8 @@ def tile_tokenmudule_pa_t_kernel(tc, patch_tokens, fc1_w, fc1_b, out):
             of_image(relu_terms, i - 2, 1)
             of_image(window_products, i, 4)
             of_window(sum_terms, m - 1, 0, 1)
-            of_image(fold_out, i)
             of_image(sum_products, i, 3)
             of_window(residual, m - 2, 1)
-            of_image(fold_sum, i)
             of_image(sum_products, i, 4)
             of_image(window_products, i, 5)
             of_window(token_norms, m - 2, 0)
@@ -674,6 +688,8 @@ def tile_tokenmudule_pa_t_kernel(tc, patch_tokens, fc1_w, fc1_b, out):
             of_window(root_ln, m - 1, 0, 0)
             of_window(transpose_back, m - 3, 1)
             of_image(window_sums, i, 6)
+            of_image(fold, i, 0)
+            of_image(fold, i, 1)
 
         def odd_step(i, m):
             of_window(load_again, m - 2, 2)
@@ -682,6 +698,8 @@ def tile_tokenmudule_pa_t_kernel(tc, patch_tokens, fc1_w, fc1_b, out):
             of_window(residual, m - 2, 3)
             of_window(token_norms, m - 2, 3)
             of_image(shifted_products, i - 2, 0)
+            of_image(fold_out, i - 1)
+            of_image(fold_sum, i - 1)
             of_image(sum_products, i - 1, 5)
             of_image(centre_square, i - 2)
             of_image(relu_terms, i - 2, 0)
@@ -704,6 +722,7 @@ def tile_tokenmudule_pa_t_kernel(tc, patch_tokens, fc1_w, fc1_b, out):
             of_pair(rest_first, m - 1)
             of_image(row_scale, i)
             of_pair(rest_second, m - 1)
+            of_pair(presum, m - 1)
             of_window(regroup, m - 3, 1)
             of_image(cubes, i)
             of_window(token_norms, m - 2, 1)
@@ -711,9 +730,7 @@ def tile_tokenmudule_pa_t_kernel(tc, patch_tokens, fc1_w, fc1_b, out):
             of_window(transpose_back, m - 3, 2)
             of_window(sum_terms, m - 1, 1, 1)
             of_image(fold_products, i, 0)
-            of_image(fold, i, 0)
             of_image(fold_products, i, 1)
-            of_image(fold, i, 1)
             of_image(window_products, i, 2)
             of_window(quantise, m - 3, 1)
             of_window(token_norms, m - 2, 2)
@@ -726,10 +743,10 @@ def tile_tokenmudule_pa_t_kernel(tc, patch_tokens, fc1_w, fc1_b, out):
             of_window(sum_terms, m - 1, 2, 1)
             of_image(sum_products, i, 3)
             of_image(window_products, i, 5)
-            of_image(fold_out, i)
-            of_image(fold_sum, i)
             of_image(sum_products, i, 4)
             of_image(window_sums, i, 6)
+            of_image(fold, i, 0)
+            of_image(fold, i, 1)
 
         load(0)
         load(1)

@@ -620,8 +620,6 @@ def tile_tokenmudule_pa_t_kernel(tc, patch_tokens, fc1_w, fc1_b, out):
             of_window(load_again, m - 2, 0)
             of_window(load_again, m - 2, 1)
             of_image(load, i + 2)
-            of_image(fold_out, i - 1)
-            of_image(fold_sum, i - 1)
             of_image(sum_products, i - 1, 5)
             of_image(shifted_products, i - 2, 0)
             of_image(squares, i)
@@ -661,7 +659,9 @@ def tile_tokenmudule_pa_t_kernel(tc, patch_tokens, fc1_w, fc1_b, out):
             of_window(root_exp, m - 2, 3)
             of_pair(finish, m - 4)
             of_image(fold_products, i, 0)
+            of_image(fold, i, 0)
             of_image(fold_products, i, 1)
+            of_image(fold, i, 1)
             of_image(window_products, i, 2)
             of_pair(gelu, m - 4)
             of_image(centre_square, i - 2)
@@ -679,8 +679,10 @@ def tile_tokenmudule_pa_t_kernel(tc, patch_tokens, fc1_w, fc1_b, out):
             of_image(relu_terms, i - 2, 1)
             of_image(window_products, i, 4)
             of_window(sum_terms, m - 1, 0, 1)
+            of_image(fold_out, i)
             of_image(sum_products, i, 3)
             of_window(residual, m - 2, 1)
+            of_image(fold_sum, i)
             of_image(sum_products, i, 4)
             of_image(window_products, i, 5)
             of_window(token_norms, m - 2, 0)
@@ -688,8 +690,6 @@ def tile_tokenmudule_pa_t_kernel(tc, patch_tokens, fc1_w, fc1_b, out):
             of_window(root_ln, m - 1, 0, 0)
             of_window(transpose_back, m - 3, 1)
             of_image(window_sums, i, 6)
-            of_image(fold, i, 0)
-            of_image(fold, i, 1)
 
         def odd_step(i, m):
             of_window(load_again, m - 2, 2)
@@ -698,8 +698,6 @@ def tile_tokenmudule_pa_t_kernel(tc, patch_tokens, fc1_w, fc1_b, out):
             of_window(residual, m - 2, 3)
             of_window(token_norms, m - 2, 3)
             of_image(shifted_products, i - 2, 0)
-            of_image(fold_out, i - 1)
-            of_image(fold_sum, i - 1)
             of_image(sum_products, i - 1, 5)
             of_image(centre_square, i - 2)
             of_image(relu_terms, i - 2, 0)
@@ -730,7 +728,9 @@ def tile_tokenmudule_pa_t_kernel(tc, patch_tokens, fc1_w, fc1_b, out):
             of_window(transpose_back, m - 3, 2)
             of_window(sum_terms, m - 1, 1, 1)
             of_image(fold_products, i, 0)
+            of_image(fold, i, 0)
             of_image(fold_products, i, 1)
+            of_image(fold, i, 1)
             of_image(window_products, i, 2)
             of_window(quantise, m - 3, 1)
             of_window(token_norms, m - 2, 2)
@@ -743,10 +743,10 @@ def tile_tokenmudule_pa_t_kernel(tc, patch_tokens, fc1_w, fc1_b, out):
             of_window(sum_terms, m - 1, 2, 1)
             of_image(sum_products, i, 3)
             of_image(window_products, i, 5)
+            of_image(fold_out, i)
+            of_image(fold_sum, i)
             of_image(sum_products, i, 4)
             of_image(window_sums, i, 6)
-            of_image(fold, i, 0)
-            of_image(fold, i, 1)
 
         load(0)
         load(1)

@@ -28,8 +28,10 @@ PITCH = 16
 LEAD = 2 * PITCH + 4
 PLANE = GRID * PITCH
 ROW = LEAD + PLANE + PITCH
+FOLD = P // BLOCKS
+FLAT = -(-TOKENS // FOLD) * FOLD
 
-OFFSETS = [(di, dj) for di in (-2, -1) for dj in (-1, 0, 1)] + [(0, -1)]
+OFFSETS = [(-2, 0), (-1, 0), (-2, -1), (-2, 1), (-1, -1), (-1, 1), (0, -1)]
 SHIFTS = len(OFFSETS)
 LEFT = SHIFTS - 1
 CENTRE = SHIFTS
@@ -103,11 +105,13 @@ def tile_tokenmudule_pa_t_kernel(tc, patch_tokens, fc1_w, fc1_b, out):
         )
 
         SQUARES = 1
-        square_ring = [const.tile([P, BLOCKS, ROW], F32, name="square%d" % n) for n in range(SQUARES)]
+        square_ring = [const.tile([P, BLOCKS, FLAT], F32, name="square%d" % n) for n in range(SQUARES)]
         CUBES = 3
         cube_ring = [const.tile([P, BLOCKS, ROW], F32, name="cube%d" % n) for n in range(CUBES)]
-        for padded in square_ring + cube_ring:
+        for padded in square_ring:
             nc.vector.memset(padded[:], 0.0)
+        for padded in cube_ring:
+            nc.gpsimd.memset(padded[:], 0.0)
         term = const.tile([P, CENTRE + 1, BLOCKS, PAIR + 4], F32, name="term")
         for o, (di, dj) in enumerate(OFFSETS):
             for first in (0, TOKENS):
@@ -130,6 +134,9 @@ def tile_tokenmudule_pa_t_kernel(tc, patch_tokens, fc1_w, fc1_b, out):
             start = LEAD + PITCH * first_line + shift
             view = padded[:, k, start : start + PITCH * n_lines]
             return view.rearrange("p (i j) -> p i j", j=PITCH)[:, :, 0:GRID]
+
+        def flat_row(b, k):
+            return square_ring[b % SQUARES][:, k, 0:TOKENS].rearrange("p (i j) -> p i j", j=GRID)
 
         def windows(p):
             return range(WHOLE + (1 if p == PAIRS - 1 else 0))
@@ -162,7 +169,7 @@ def tile_tokenmudule_pa_t_kernel(tc, patch_tokens, fc1_w, fc1_b, out):
             norm_sq = small.tile([P, CENTRE + 1, BLOCKS], F32, name="norm_sq")
             for k in range(BLOCKS):
                 nc.scalar.activation(
-                    out=line(square_ring[b % SQUARES], k, 0, GRID, 0),
+                    out=flat_row(b, k),
                     in_=x_row(b, k),
                     func=ACT.Square,
                     accum_out=sum_sq[:, k : k + 1],
@@ -170,7 +177,7 @@ def tile_tokenmudule_pa_t_kernel(tc, patch_tokens, fc1_w, fc1_b, out):
             for k in range(BLOCKS):
                 nc.scalar.activation(
                     out=junk_row[:, k % JUNK, :].rearrange("p (i j) -> p i j", j=GRID),
-                    in_=line(square_ring[b % SQUARES], k, 0, GRID, 0),
+                    in_=flat_row(b, k),
                     func=ACT.Square,
                     accum_out=norm_sq[:, CENTRE, k : k + 1],
                 )
@@ -201,7 +208,7 @@ def tile_tokenmudule_pa_t_kernel(tc, patch_tokens, fc1_w, fc1_b, out):
                     out=line(cube_ring[b % CUBES], k, 0, GRID, 0),
                     in0=x_row(b, k),
                     scalar=c[:, k : k + 1],
-                    in1=line(square_ring[b % SQUARES], k, 0, GRID, 0),
+                    in1=flat_row(b, k),
                     op0=ALU.mult,
                     op1=ALU.mult,
                 )
@@ -212,8 +219,9 @@ def tile_tokenmudule_pa_t_kernel(tc, patch_tokens, fc1_w, fc1_b, out):
         def grid_part(padded, rows, o):
             di, dj = OFFSETS[o]
             first, width = columns(dj)
-            here = lines(padded, rows, -di, GRID + di, first, width)
-            there = lines(padded, rows, -di, GRID + di, first + PITCH * di + dj, width)
+            grid = padded[:, rows, 0:TOKENS].rearrange("p k (i j) -> p k i j", j=GRID)
+            here = grid[:, :, -di:GRID, first : first + width]
+            there = grid[:, :, 0 : GRID + di, first + dj : first + dj + width]
             return here, there, (GRID + di) * width
 
         def window_products(b, o):
@@ -238,16 +246,18 @@ def tile_tokenmudule_pa_t_kernel(tc, patch_tokens, fc1_w, fc1_b, out):
                     accum_out=tiles["norm_sq", b][:, o, k : k + 1],
                 )
 
+        def fold_steps(o):
+            return -(-GRID * (GRID + OFFSETS[o][0]) // FOLD)
+
         def fold_products(b, o):
-            di, dj = OFFSETS[o]
-            n_lines = GRID + di
-            every = slice(0, BLOCKS)
+            start = -GRID * OFFSETS[o][0]
+            steps = fold_steps(o)
             x_sq = square_ring[b % SQUARES]
-            product = work.tile([P, GRID, BLOCKS, PITCH], F32, name="product_fold", bufs=FOLD_BUFS)
+            product = work.tile([P, FLAT // FOLD, BLOCKS, FOLD], F32, name="product_fold", bufs=FOLD_BUFS)
             nc.vector.tensor_tensor(
-                out=product[:, 0:n_lines, :, :].rearrange("p i k j -> p k i j"),
-                in0=lines(x_sq, every, -di, n_lines, 0, PITCH),
-                in1=lines(x_sq, every, -di, n_lines, PITCH * di + dj, PITCH),
+                out=product[:, 0:steps, :, :].rearrange("p r k i -> p k r i"),
+                in0=x_sq[:, :, start : start + FOLD * steps].rearrange("p k (r i) -> p k r i", i=FOLD),
+                in1=x_sq[:, :, 0 : FOLD * steps].rearrange("p k (r i) -> p k r i", i=FOLD),
                 op=ALU.mult,
             )
             tiles["products", b, o] = product
@@ -255,15 +265,15 @@ def tile_tokenmudule_pa_t_kernel(tc, patch_tokens, fc1_w, fc1_b, out):
         def fold(b, o):
             if o == 0:
                 tiles["folded", b] = psum_1.tile([P, HALF, P], F32, name="folded")
-            n_lines = GRID + OFFSETS[o][0]
-            for i in range(n_lines):
+            steps = fold_steps(o)
+            for r in range(steps):
                 nc.tensor.matmul(
                     out=tiles["folded", b][:, o, :],
-                    lhsT=tiles["products", b, o][:, i, :, :].rearrange("p k j -> p (k j)"),
+                    lhsT=tiles["products", b, o][:, r, :, :].rearrange("p k i -> p (k i)"),
                     rhs=ident_f32[:],
                     is_transpose=True,
-                    start=(i == 0),
-                    stop=(i == n_lines - 1),
+                    start=(r == 0),
+                    stop=(r == steps - 1),
                 )
 
         def fold_out(b):

@@ -104,7 +104,7 @@ def tile_tokenmudule_pa_t_kernel(tc, patch_tokens, fc1_w, fc1_b, out):
             in_=w_grouped[:].rearrange("p g n t -> p (g n t)"),
         )
 
-        SQUARES = 1
+        SQUARES = 2
         square_ring = [const.tile([P, BLOCKS, FLAT], F32, name="square%d" % n) for n in range(SQUARES)]
         CUBES = 3
         cube_ring = [const.tile([P, BLOCKS, ROW], F32, name="cube%d" % n) for n in range(CUBES)]
@@ -699,7 +699,6 @@ def tile_tokenmudule_pa_t_kernel(tc, patch_tokens, fc1_w, fc1_b, out):
             of_window(regroup, m - 3, 0)
             of_window(root_ln, m - 1, 0, 0)
             of_window(transpose_back, m - 3, 1)
-            of_image(window_sums, i, 6)
 
         def odd_step(i, m):
             of_window(load_again, m - 2, 2)
@@ -708,9 +707,9 @@ def tile_tokenmudule_pa_t_kernel(tc, patch_tokens, fc1_w, fc1_b, out):
             of_window(residual, m - 2, 3)
             of_window(token_norms, m - 2, 3)
             of_image(shifted_products, i - 2, 0)
-            of_image(sum_products, i - 1, 5)
             of_image(centre_square, i - 2)
             of_image(relu_terms, i - 2, 0)
+            of_image(sum_products, i - 1, 5)
             of_image(vector_terms, i - 2, 0)
             of_window(root_ln, m - 1, 0, 1)
             of_window(quantise, m - 3, 0)
@@ -719,10 +718,11 @@ def tile_tokenmudule_pa_t_kernel(tc, patch_tokens, fc1_w, fc1_b, out):
             of_window(sum_terms, m - 1, 1, 0)
             of_image(squares, i)
             of_image(vector_terms, i - 2, 1)
-            of_image(scaled_norms_first, i - 1)
             of_window(project, m - 3, 0)
             of_window(residual, m - 2, 2)
             of_image(relu_terms, i - 2, 1)
+            of_image(window_sums, i - 1, 6)
+            of_image(scaled_norms_first, i - 1)
             of_image(scaled_norms_second, i - 1)
             of_window(normalise, m - 3, 2)
             of_image(mean_square, i)

from contextlib import ExitStack

import concourse.mybir as mybir
from concourse.masks import make_identity

F32 = mybir.dt.float32
BF16 = mybir.dt.bfloat16
U32 = mybir.dt.uint32
U8 = mybir.dt.uint8
FP8X4 = mybir.dt.float8_e4m3fn_x4
ACT = mybir.ActivationFunctionType
ALU = mybir.AluOpType

P = 128
IMAGES = 32
PAIRS = IMAGES // 2
GRID = 14
TOKENS = GRID * GRID
CHANNELS = 1024
FEATURES = 128
BLOCKS = CHANNELS // P
HALF = BLOCKS // 2
BANK = HALF * P
PACK = 4
PASSES = CHANNELS // (P * PACK)

PITCH = 16
LEAD = 2 * PITCH + 4
PLANE = GRID * PITCH
ROW = LEAD + PLANE + PITCH
FOLD = P // BLOCKS
FLAT = -(-TOKENS // FOLD) * FOLD

OFFSETS = [(-2, 0), (-1, 0), (-2, -1), (-2, 1), (-1, -1), (-1, 1), (0, -1)]
SHIFTS = len(OFFSETS)
LEFT = SHIFTS - 1
CENTRE = SHIFTS
WINDOW = 9
RELUED = (5, 5)
FOLDED = 2
FOLD_BUFS = 2
PRODUCTS = 2
JUNK = 4

EPS_CUBED = 1e-18
FLOOR_SQUARED = 1e-24
LN_SMALLEST = 1e-18

WINDOW_START = (0, TOKENS - P)
PAIR = 2 * TOKENS
WHOLE = PAIR // P
REST = PAIR - WHOLE * P
GROUP = 2

FLOPS = 2 * IMAGES * TOKENS * CHANNELS * FEATURES


def tile_tokenmudule_pa_t_kernel(tc, patch_tokens, fc1_w, fc1_b, out):
    nc = tc.nc
    flat_x = patch_tokens.rearrange("b t c -> (b t) c")
    flat_out = out.rearrange("b t f -> (b t) f")
    with ExitStack() as ctx:
        const = ctx.enter_context(tc.tile_pool(name="const", bufs=1))
        loads = ctx.enter_context(tc.tile_pool(name="loads", bufs=2))
        work = ctx.enter_context(tc.tile_pool(name="work", bufs=2))
        small = ctx.enter_context(tc.tile_pool(name="small", bufs=4))
        psum_io = ctx.enter_context(tc.psum_pool(name="psum_io", bufs=2))
        psum_t = ctx.enter_context(tc.psum_pool(name="psum_t", bufs=3))
        psum_1 = ctx.enter_context(tc.psum_pool(name="psum_1", bufs=1))

        ident_f32 = const.tile([P, P], F32, name="ident_f32")
        make_identity(nc, ident_f32[:])
        ln_smallest = const.tile([P, 1], F32, name="ln_smallest")
        nc.vector.memset(ln_smallest[:], LN_SMALLEST)
        floor_plus = const.tile([P, 1], F32, name="floor_plus")
        nc.vector.memset(floor_plus[:], FLOOR_SQUARED)
        floor_minus = const.tile([P, 1], F32, name="floor_minus")
        nc.vector.memset(floor_minus[:], -FLOOR_SQUARED)
        eps_minus = const.tile([P, 1], F32, name="eps_minus")
        nc.vector.memset(eps_minus[:], -EPS_CUBED)
        eps_in_mean = const.tile([P, 1], F32, name="eps_in_mean")
        nc.vector.memset(eps_in_mean[:], EPS_CUBED * (WINDOW - 1) / WINDOW)

        member = const.tile([P, BLOCKS], F32, name="member")
        nc.vector.reduce_sum(
            out=member[:], in_=ident_f32[:].rearrange("p (k i) -> p k i", k=BLOCKS), axis=mybir.AxisListType.X
        )

        bias_bf = const.tile([P, FEATURES], BF16, name="bias_bf")
        nc.sync.dma_start(out=bias_bf[:], in_=fc1_b.partition_broadcast(P))
        bias = const.tile([P, FEATURES], F32, name="bias")
        nc.vector.tensor_copy(out=bias[:], in_=bias_bf[:])

        w_raw = work.tile([P, PASSES, PACK, FEATURES], BF16, name="w_raw", tag="tok")
        nc.sync.dma_start(out=w_raw[:], in_=fc1_w.rearrange("(g p t) n -> p g t n", p=P, t=PACK))
        w_grouped = work.tile([P, PASSES, FEATURES, PACK], BF16, name="w_grouped", tag="grouped", align_bytes=64)
        for g in range(PASSES):
            nc.vector.tensor_copy(out=w_grouped[:, g, :, :], in_=w_raw[:, g, :, :].rearrange("p t n -> p n t"))
        w_codes = const.tile([P, PASSES * FEATURES], U32, name="w_codes", align_bytes=64)
        w_scales = const.tile([P, PASSES * FEATURES], U8, name="w_scales", align_bytes=64)
        nc.vector.quantize_mx(
            out=w_codes[:].bitcast(FP8X4),
            scales=w_scales[:],
            in_=w_grouped[:].rearrange("p g n t -> p (g n t)"),
        )

        SQUARES = 2
        square_ring = [const.tile([P, BLOCKS, FLAT], F32, name="square%d" % n) for n in range(SQUARES)]
        CUBES = 3
        cube_ring = [const.tile([P, BLOCKS, ROW], F32, name="cube%d" % n) for n in range(CUBES)]
        for padded in square_ring:
            nc.vector.memset(padded[:], 0.0)
        for padded in cube_ring:
            nc.gpsimd.memset(padded[:], 0.0)
        term = const.tile([P, CENTRE + 1, BLOCKS, PAIR + 4], F32, name="term")
        for o, (di, dj) in enumerate(OFFSETS):
            for first in (0, TOKENS):
                if di < 0:
                    nc.vector.memset(term[:, o, :, first : first - di * GRID], 0.0)
        nc.vector.memset(term[:, LEFT, :, PAIR : PAIR + 1], 0.0)
        rest = const.tile([P, BLOCKS, P], F32, name="rest")
        junk_row = const.tile([P, JUNK, TOKENS], BF16, name="junk_row")
        junk_f32 = const.tile([P, JUNK, TOKENS], F32, name="junk_f32")
        junk_wide = const.tile([P, CHANNELS], BF16, name="junk_wide")

        tiles = {}

        def lines(padded, rows, first_line, n_lines, shift, width):
            start = LEAD + PITCH * first_line + shift
            view = padded[:, rows, start : start + PITCH * n_lines]
            return view.rearrange("p k (i j) -> p k i j", j=PITCH)[:, :, :, 0:width]

        def line(padded, k, first_line, n_lines, shift):
            start = LEAD + PITCH * first_line + shift
            view = padded[:, k, start : start + PITCH * n_lines]
            return view.rearrange("p (i j) -> p i j", j=PITCH)[:, :, 0:GRID]

        def flat_row(b, k):
            return square_ring[b % SQUARES][:, k, 0:TOKENS].rearrange("p (i j) -> p i j", j=GRID)

        def windows(p):
            return range(WHOLE + (1 if p == PAIRS - 1 else 0))

        def load(b):
            x_in = loads.tile([P, 2, CHANNELS], BF16, name="x_in")
            for w in range(2):
                nc.sync.dma_start(out=x_in[:, w, :], in_=patch_tokens[b, WINDOW_START[w] : WINDOW_START[w] + P, :])
            tiles["x_in", b] = x_in

        def transpose_in(b):
            words = tiles["x_in", b][:].bitcast(F32)
            for h in range(2):
                x_t = psum_io.tile([P, 2, TOKENS], F32, name="x_t")
                for uu in range(2):
                    cols = slice((2 * h + uu) * P, (2 * h + uu + 1) * P)
                    for w in range(2):
                        nc.tensor.transpose(
                            x_t[:, uu, WINDOW_START[w] : WINDOW_START[w] + P], words[:, w, cols], ident_f32[:]
                        )
                tiles["x_t", b, h] = x_t[:].rearrange("p u n -> p (u n)").bitcast(BF16).rearrange(
                    "p (u i j e) -> p u e i j", u=2, e=2, j=GRID
                )

        def x_row(b, k):
            return tiles["x_t", b, k // HALF][:, (k % HALF) // 2, k % 2, :, :]

        def squares(b):
            sum_sq = small.tile([P, BLOCKS], F32, name="sum_sq")
            norm_sq = small.tile([P, CENTRE + 1, BLOCKS], F32, name="norm_sq")
            for k in range(BLOCKS):
                nc.scalar.activation(
                    out=flat_row(b, k),
                    in_=x_row(b, k),
                    func=ACT.Square,
                    accum_out=sum_sq[:, k : k + 1],
                )
            for k in range(BLOCKS):
                nc.scalar.activation(
                    out=junk_row[:, k % JUNK, :].rearrange("p (i j) -> p i j", j=GRID),
                    in_=flat_row(b, k),
                    func=ACT.Square,
                    accum_out=norm_sq[:, CENTRE, k : k + 1],
                )
            tiles["sum_sq", b] = sum_sq
            tiles["norm_sq", b] = norm_sq

        def mean_square(b):
            mean_sq = small.tile([P, BLOCKS], F32, name="mean_sq")
            nc.vector.tensor_scalar(
                out=mean_sq[:],
                in0=tiles["sum_sq", b][:],
                scalar1=1.0 / TOKENS,
                scalar2=1e-19,
                op0=ALU.mult,
                op1=ALU.max,
            )
            tiles["mean_sq", b] = mean_sq

        def row_scale(b):
            scaled = small.tile([P, CENTRE + 2, BLOCKS], F32, name="scaled")
            nc.vector.reciprocal(out=scaled[:, CENTRE + 1, :], in_=tiles["mean_sq", b][:])
            tiles["scaled", b] = scaled

        def cubes(b):
            c = tiles["scaled", b][:, CENTRE + 1, :]
            for k in range(BLOCKS):
                nc.vector.scalar_tensor_tensor(
                    out=line(cube_ring[b % CUBES], k, 0, GRID, 0),
                    in0=x_row(b, k),
                    scalar=c[:, k : k + 1],
                    in1=flat_row(b, k),
                    op0=ALU.mult,
                    op1=ALU.mult,
                )

        def columns(dj):
            return max(0, -dj), GRID - abs(dj)

        def grid_part(padded, rows, o):
            di, dj = OFFSETS[o]
            first, width = columns(dj)
            grid = padded[:, rows, 0:TOKENS].rearrange("p k (i j) -> p k i j", j=GRID)
            here = grid[:, :, -di:GRID, first : first + width]
            there = grid[:, :, 0 : GRID + di, first + dj : first + dj + width]
            return here, there, (GRID + di) * width

        def window_products(b, o):
            here, there, length = grid_part(square_ring[b % SQUARES], slice(0, BLOCKS), o)
            product = work.tile([P, BLOCKS, TOKENS], F32, name="product", bufs=PRODUCTS)
            nc.vector.tensor_tensor(
                out=product[:, :, 0:length].rearrange("p k (i j) -> p k i j", i=GRID + OFFSETS[o][0]),
                in0=here,
                in1=there,
                op=ALU.mult,
            )
            tiles["products", b, o] = product

        def sum_products(b, o):
            product = tiles["products", b, o]
            length = grid_part(square_ring[b % SQUARES], slice(0, BLOCKS), o)[2]
            for k in range(BLOCKS):
                nc.scalar.activation(
                    out=junk_row[:, k % JUNK, 0:length],
                    in_=product[:, k, 0:length],
                    func=ACT.Copy,
                    accum_out=tiles["norm_sq", b][:, o, k : k + 1],
                )

        def fold_steps(o):
            return -(-GRID * (GRID + OFFSETS[o][0]) // FOLD)

        def fold_products(b, o):
            start = -GRID * OFFSETS[o][0]
            steps = fold_steps(o)
            x_sq = square_ring[b % SQUARES]
            product = work.tile([P, FLAT // FOLD, BLOCKS, FOLD], F32, name="product_fold", bufs=FOLD_BUFS)
            nc.vector.tensor_tensor(
                out=product[:, 0:steps, :, :].rearrange("p r k i -> p k r i"),
                in0=x_sq[:, :, start : start + FOLD * steps].rearrange("p k (r i) -> p k r i", i=FOLD),
                in1=x_sq[:, :, 0 : FOLD * steps].rearrange("p k (r i) -> p k r i", i=FOLD),
                op=ALU.mult,
            )
            tiles["products", b, o] = product

        def fold(b, o):
            if o == 0:
                tiles["folded", b] = psum_1.tile([P, HALF, P], F32, name="folded")
            steps = fold_steps(o)
            for r in range(steps):
                nc.tensor.matmul(
                    out=tiles["folded", b][:, o, :],
                    lhsT=tiles["products", b, o][:, r, :, :].rearrange("p k i -> p (k i)"),
                    rhs=ident_f32[:],
                    is_transpose=True,
                    start=(r == 0),
                    stop=(r == steps - 1),
                )

        def fold_out(b):
            partial = work.tile([P, FOLDED, P], F32, name="partial", bufs=1)
            nc.scalar.copy(out=partial[:], in_=tiles["folded", b][:, 0:FOLDED, :])
            tiles["partial", b] = partial

        def fold_sum(b):
            partial = tiles["partial", b]
            norms = tiles["folded", b][:, HALF - 1, 0 : FOLDED * BLOCKS].rearrange("p (o k) -> p o k", k=BLOCKS)
            for o in range(FOLDED):
                nc.tensor.matmul(out=norms[:, o, :], lhsT=partial[:, o, :], rhs=member[:], start=True, stop=True)
            tiles["norms", b] = norms

        def window_sums(b, o):
            for k in range(BLOCKS):
                here, there, length = grid_part(square_ring[b % SQUARES], slice(k, k + 1), o)
                nc.vector.scalar_tensor_tensor(
                    out=junk_f32[:, k % JUNK, 0:length].rearrange("p (a i j) -> p a i j", a=1, i=GRID + OFFSETS[o][0]),
                    in0=here,
                    scalar=1.0,
                    in1=there,
                    op0=ALU.mult,
                    op1=ALU.mult,
                    accum_out=tiles["norm_sq", b][:, o, k : k + 1],
                )

        def scaled_norms_first(b):
            scaled = tiles["scaled", b]
            for first, last, norms in (
                (0, FOLDED, tiles["norms", b]),
                (FOLDED, CENTRE + 1, tiles["norm_sq", b][:, FOLDED : CENTRE + 1, :]),
            ):
                nc.vector.scalar_tensor_tensor(
                    out=scaled[:, first:last, :],
                    in0=norms,
                    scalar=FLOOR_SQUARED,
                    in1=scaled[:, CENTRE + 1, :].unsqueeze(1).to_broadcast([P, last - first, BLOCKS]),
                    op0=ALU.max,
                    op1=ALU.mult,
                )

        def scaled_norms_second(b):
            scaled = tiles["scaled", b]
            norms = scaled[:, 0 : CENTRE + 1, :]
            c = scaled[:, CENTRE + 1, :]
            nc.vector.tensor_tensor(
                out=norms, in0=norms, in1=c.unsqueeze(1).to_broadcast([P, CENTRE + 1, BLOCKS]), op=ALU.mult
            )

        def weights_ln(b):
            scaled = tiles["scaled", b]
            nc.scalar.activation(out=scaled[:], in_=scaled[:], func=ACT.Ln, bias=ln_smallest[:])

        def weights_sum(b):
            scaled = tiles["scaled", b]
            ln_weight = small.tile([P, CENTRE + 1, BLOCKS], F32, name="ln_weight")
            nc.vector.scalar_tensor_tensor(
                out=ln_weight[:],
                in0=scaled[:, 0 : CENTRE + 1, :],
                scalar=-1.5,
                in1=scaled[:, CENTRE + 1, :].unsqueeze(1).to_broadcast([P, CENTRE + 1, BLOCKS]),
                op0=ALU.mult,
                op1=ALU.add,
            )
            tiles["ln_weight", b] = ln_weight

        def weights_exp(b):
            ln_weight = tiles["ln_weight", b]
            weight = small.tile([P, CENTRE, BLOCKS], F32, name="weight")
            nc.scalar.activation(out=weight[:], in_=ln_weight[:, 0:CENTRE, :], func=ACT.Exp)
            centre_scale = small.tile([P, BLOCKS], F32, name="centre_scale")
            nc.scalar.activation(out=centre_scale[:], in_=ln_weight[:, CENTRE, :], func=ACT.Exp, scale=0.5)
            tiles["weight", b] = weight
            tiles["centre_scale", b] = centre_scale

        def relued(b, h):
            return RELUED[h]

        def terms_of(b, o, k, first_line, n_lines):
            first = TOKENS * (b % 2) + GRID * first_line
            return term[:, o, k, first : first + GRID * n_lines]

        def centre_square(b):
            for k in range(BLOCKS):
                nc.scalar.activation(
                    out=terms_of(b, CENTRE, k, 0, GRID).rearrange("p (i j) -> p i j", j=GRID),
                    in_=line(cube_ring[b % CUBES], k, 0, GRID, 0),
                    func=ACT.Square,
                    scale=tiles["centre_scale", b][:, k : k + 1],
                )

        def centre_floor(b):
            written = terms_of(b, CENTRE, slice(0, BLOCKS), 0, GRID)
            nc.vector.tensor_scalar(out=written, in0=written, scalar1=EPS_CUBED, scalar2=None, op0=ALU.max)

        def shifted_products(b, h):
            rows = slice(HALF * h, HALF * (h + 1))
            cube = cube_ring[b % CUBES]
            for o in range(relued(b, h)):
                di, dj = OFFSETS[o]
                n_lines = GRID + di
                nc.vector.tensor_tensor(
                    out=terms_of(b, o, rows, -di, n_lines).rearrange("p k (i j) -> p k i j", j=GRID),
                    in0=lines(cube, rows, -di, n_lines, PITCH * di + dj, GRID),
                    in1=lines(cube, rows, -di, n_lines, 0, GRID),
                    op=ALU.mult,
                )

        def relu_terms(b, h):
            weight = tiles["weight", b]
            for k in range(HALF * h, HALF * (h + 1)):
                for o in range(relued(b, h)):
                    di = OFFSETS[o][0]
                    written = terms_of(b, o, k, -di, GRID + di)
                    nc.scalar.activation(
                        out=written, in_=written, func=ACT.Relu, scale=weight[:, o, k : k + 1], bias=eps_minus[:]
                    )

        def vector_floor(b, h, o):
            di = OFFSETS[o][0]
            written = terms_of(b, o, slice(HALF * h, HALF * (h + 1)), -di, GRID + di)
            nc.vector.tensor_scalar(
                out=written, in0=written, scalar1=EPS_CUBED, scalar2=EPS_CUBED, op0=ALU.max, op1=ALU.subtract
            )

        def vector_terms(b, h):
            weight = tiles["weight", b]
            cube = cube_ring[b % CUBES]
            for o in range(relued(b, h), SHIFTS):
                di, dj = OFFSETS[o]
                for k in range(HALF * h, HALF * (h + 1)):
                    nc.vector.scalar_tensor_tensor(
                        out=terms_of(b, o, k, -di, GRID + di).rearrange("p (i j) -> p i j", j=GRID),
                        in0=line(cube, k, -di, GRID + di, PITCH * di + dj),
                        scalar=weight[:, o, k : k + 1],
                        in1=line(cube, k, -di, GRID + di, 0),
                        op0=ALU.mult,
                        op1=ALU.mult,
                    )
                if o > relued(b, h):
                    vector_floor(b, h, o - 1)
            if relued(b, h) < SHIFTS:
                vector_floor(b, h, SHIFTS - 1)

        def rest_first(p):
            nc.vector.reduce_sum(
                out=rest[:, :, REST * p : REST * (p + 1)],
                in_=term[:, :, :, WHOLE * P : PAIR].rearrange("p o k n -> p k n o"),
                axis=mybir.AxisListType.X,
            )

        def rest_second(p):
            total = rest[:, :, REST * p : REST * (p + 1)]
            nc.vector.tensor_tensor(
                out=total, in0=total, in1=term[:, LEFT, :, WHOLE * P + 1 : PAIR + 1], op=ALU.add
            )

        def presum(p):
            if p < PAIRS - 1:
                return
            for k in range(HALF, BLOCKS):
                total = term[:, 0, k, P : WHOLE * P]
                for o in range(1, CENTRE + 1):
                    nc.vector.tensor_tensor(out=total, in0=total, in1=term[:, o, k, P : WHOLE * P], op=ALU.add)
                nc.vector.tensor_tensor(out=total, in0=total, in1=term[:, LEFT, k, P + 1 : WHOLE * P + 1], op=ALU.add)

        def sum_terms(p, w, h):
            total_t = psum_t.tile([P, HALF, P], F32, name="total_t")
            first = P * w
            for kk in range(HALF):
                k = HALF * h + kk
                if w == WHOLE:
                    addends = [rest[:, k, :]]
                elif p == PAIRS - 1 and w > 0 and h == 1:
                    addends = [term[:, 0, k, first : first + P]]
                else:
                    addends = [term[:, o, k, first : first + P] for o in range(CENTRE + 1)]
                    addends.append(term[:, LEFT, k, first + 1 : first + 1 + P])
                for n, one in enumerate(addends):
                    nc.tensor.matmul(
                        out=total_t[:, kk, :],
                        lhsT=one,
                        rhs=ident_f32[:],
                        is_transpose=True,
                        start=(n == 0),
                        stop=(n == len(addends) - 1),
                    )
            tiles["total_t", p, w, h] = total_t

        def root_ln(p, w, h):
            if h == 0:
                tiles["r_t", p, w] = work.tile([P, CHANNELS], F32, name="r_t", bufs=7)
            r_t = tiles["r_t", p, w][:, BANK * h : BANK * (h + 1)].rearrange("p (u a c e) -> p u a c e", u=2, a=2, e=2)
            total = tiles["total_t", p, w, h][:].rearrange("p (a e) (c u) -> p u a c e", e=2, u=2)
            for u in range(2):
                nc.scalar.activation(
                    out=r_t[:, u, :, :, :],
                    in_=total[:, u, :, :, :],
                    func=ACT.Ln,
                    scale=1.0 / WINDOW,
                    bias=eps_in_mean[:],
                )

        def load_again(p, w):
            x_again = loads.tile([P, CHANNELS], BF16, name="x_again", bufs=3)
            if w < WHOLE:
                nc.sync.dma_start(out=x_again[:], in_=flat_x[PAIR * p + P * w : PAIR * p + P * (w + 1), :])
            else:
                for q in range(PAIRS):
                    nc.sync.dma_start(
                        out=x_again[REST * q : REST * (q + 1), :],
                        in_=flat_x[PAIR * q + WHOLE * P : PAIR * (q + 1), :],
                    )
            tiles["x_again", p, w] = x_again

        def root_exp(p, w):
            r_t = tiles["r_t", p, w]
            nc.scalar.activation(out=r_t[:], in_=r_t[:], func=ACT.Exp, scale=1.0 / 3.0)

        def residual(p, w):
            for g in range(PASSES):
                channels = slice(BANK * g, BANK * (g + 1))
                r_t = tiles["r_t", p, w][:, channels].rearrange("p (u c e) -> p u c e", u=2, e=2)
                x_again = tiles["x_again", p, w][:, channels].rearrange("p (c u e) -> p u c e", u=2, e=2)
                nc.vector.tensor_tensor(out=r_t, in0=r_t, in1=x_again, op=ALU.add)

        def token_norms(p, w):
            if w == 0:
                tiles["length_sq", p] = small.tile([P, WHOLE + 1], F32, name="length_sq")
            nc.scalar.activation(
                out=junk_wide[:],
                in_=tiles["r_t", p, w][:],
                func=ACT.Square,
                accum_out=tiles["length_sq", p][:, w : w + 1],
            )

        def lengths(p):
            return tiles["length_sq", p][:, 0 : len(windows(p))]

        def length_floor(p):
            nc.scalar.activation(out=lengths(p), in_=lengths(p), func=ACT.Relu, bias=floor_minus[:])

        def length_ln(p):
            nc.scalar.activation(out=lengths(p), in_=lengths(p), func=ACT.Ln, bias=floor_plus[:])

        def length_exp(p):
            inverse = small.tile([P, WHOLE + 1], F32, name="inverse")
            nc.scalar.activation(out=inverse[:, 0 : len(windows(p))], in_=lengths(p), func=ACT.Exp, scale=-0.5)
            tiles["inverse", p] = inverse

        def normalise(p, w):
            tok_t = work.tile([P, CHANNELS], BF16, name="tok_t", tag="tok")
            nc.vector.tensor_scalar(
                out=tok_t[:],
                in0=tiles["r_t", p, w][:],
                scalar1=tiles["inverse", p][:, w : w + 1],
                scalar2=None,
                op0=ALU.mult,
            )
            tiles["tok_t", p, w] = tok_t

        def transpose_back(p, w):
            words = tiles["tok_t", p, w][:].bitcast(F32)
            pool, tag = (psum_t, "total_t") if p == PAIRS - 1 else (psum_1, "tok_c")
            tok_c = pool.tile([P, PASSES, 2, P], F32, name="tok_c", tag=tag)
            for g in range(PASSES):
                for u in range(2):
                    nc.tensor.transpose(
                        tok_c[:, g, u, :], words[:, P * (2 * g + u) : P * (2 * g + u + 1)], ident_f32[:]
                    )
            tiles["tok_c", p, w] = tok_c

        def regroup(p, w):
            grouped = work.tile([P, PASSES, P, PACK], BF16, name="grouped", align_bytes=64)
            nc.scalar.copy(
                out=grouped[:].rearrange("p g n t -> p g (n t)").bitcast(F32).rearrange("p g (n u) -> p g n u", u=2),
                in_=tiles["tok_c", p, w][:].rearrange("p g u n -> p g n u"),
            )
            tiles["grouped", p, w] = grouped

        def quantise(p, w):
            codes = small.tile([P, PASSES * P], U32, name="codes", bufs=2, align_bytes=64)
            scales = small.tile([P, PASSES * P], U8, name="scales", bufs=2, align_bytes=64)
            nc.vector.quantize_mx(
                out=codes[:].bitcast(FP8X4),
                scales=scales[:],
                in_=tiles["grouped", p, w][:].rearrange("p g n t -> p (g n t)"),
            )
            tiles["codes", p, w] = codes
            tiles["scales", p, w] = scales

        def project(p, w):
            codes = tiles["codes", p, w]
            scales = tiles["scales", p, w]
            if w == 0:
                tiles["projected", p] = psum_1.tile([P, WHOLE + 1, FEATURES], F32, name="projected")
            for g in range(PASSES):
                nc.tensor.matmul_mx(
                    out=tiles["projected", p][:, w, :],
                    lhsT=codes[:, P * g : P * (g + 1)].bitcast(FP8X4),
                    lhsT_scale=scales[:, P * g : P * (g + 1)],
                    rhs=w_codes[:, FEATURES * g : FEATURES * (g + 1)].bitcast(FP8X4),
                    rhs_scale=w_scales[:, FEATURES * g : FEATURES * (g + 1)],
                    start=(g == 0),
                    stop=(g == PASSES - 1),
                )

        def finish(p):
            n = WHOLE * (p % GROUP)
            count = len(windows(p))
            if n == 0:
                tiles["result", p // GROUP] = work.tile([P, WHOLE * GROUP + 1, FEATURES], F32, name="result", bufs=1)
            nc.vector.tensor_tensor(
                out=tiles["result", p // GROUP][:, n : n + count, :],
                in0=tiles["projected", p][:, 0:count, :],
                in1=bias[:].unsqueeze(1).to_broadcast([P, count, FEATURES]),
                op=ALU.add,
            )

        def gelu(p):
            if p % GROUP < GROUP - 1:
                return
            count = WHOLE * GROUP + (1 if p == PAIRS - 1 else 0)
            result = tiles["result", p // GROUP]
            flat = result[:, 0:count, :].rearrange("p n f -> p (n f)")
            nc.scalar.activation(out=flat, in_=flat, func=ACT.Gelu)
            for n in range(GROUP):
                first = PAIR * (p - GROUP + 1 + n)
                nc.sync.dma_start(
                    out=flat_out[first : first + WHOLE * P, :].rearrange("(w n) f -> n w f", n=P),
                    in_=result[:, WHOLE * n : WHOLE * (n + 1), :],
                )
            if p == PAIRS - 1:
                for q in range(PAIRS):
                    nc.sync.dma_start(
                        out=flat_out[PAIR * q + WHOLE * P : PAIR * (q + 1), :],
                        in_=result[REST * q : REST * (q + 1), WHOLE * GROUP, :],
                    )

        def of_image(stage, b, *more):
            if 0 <= b < IMAGES:
                stage(b, *more)

        def of_pair(stage, p, *more):
            if 0 <= p < PAIRS:
                stage(p, *more)

        def of_window(stage, p, w, *more):
            if 0 <= p < PAIRS and w in windows(p):
                stage(p, w, *more)

        def even_step(i, m):
            of_window(load_again, m - 2, 0)
            of_window(load_again, m - 2, 1)
            of_image(load, i + 2)
            of_image(sum_products, i - 1, 5)
            of_image(shifted_products, i - 2, 0)
            of_image(squares, i)
            of_image(shifted_products, i - 2, 1)
            of_image(scaled_norms_first, i - 1)
            of_window(regroup, m - 4, 2)
            of_image(scaled_norms_second, i - 1)
            of_window(normalise, m - 4, 3)
            of_window(transpose_back, m - 4, 3)
            of_window(regroup, m - 4, 3)
            of_window(quantise, m - 4, 2)
            of_window(quantise, m - 4, 3)
            of_window(project, m - 4, 2)
            of_window(project, m - 4, 3)
            of_window(root_ln, m - 2, 1, 1)
            of_pair(length_floor, m - 3)
            of_image(weights_ln, i - 2)
            of_image(weights_ln, i - 1)
            of_image(mean_square, i)
            of_pair(length_ln, m - 3)
            of_image(row_scale, i)
            of_window(root_ln, m - 2, 2, 1)
            of_window(sum_terms, m - 2, 3, 0)
            of_window(root_ln, m - 2, 3, 0)
            of_window(sum_terms, m - 2, 3, 1)
            of_window(root_ln, m - 2, 3, 1)
            of_image(weights_sum, i - 2)
            of_image(weights_sum, i - 1)
            of_image(cubes, i)
            of_image(transpose_in, i + 1)
            of_window(root_exp, m - 2, 0)
            of_image(weights_exp, i - 2)
            of_image(weights_exp, i - 1)
            of_pair(length_exp, m - 3)
            of_window(root_exp, m - 2, 1)
            of_window(root_exp, m - 2, 2)
            of_window(root_exp, m - 2, 3)
            of_pair(finish, m - 4)
            of_image(fold_products, i, 0)
            of_image(fold, i, 0)
            of_image(fold_products, i, 1)
            of_image(fold, i, 1)
            of_image(window_products, i, 2)
            of_pair(gelu, m - 4)
            of_image(centre_square, i - 2)
            of_image(relu_terms, i - 2, 0)
            of_image(vector_terms, i - 2, 0)
            of_image(centre_floor, i - 2)
            of_window(sum_terms, m - 1, 0, 0)
            of_image(vector_terms, i - 2, 1)
            of_image(sum_products, i, 2)
            of_window(residual, m - 2, 0)
            of_window(normalise, m - 3, 0)
            of_window(transpose_back, m - 3, 0)
            of_image(window_products, i, 3)
            of_window(normalise, m - 3, 1)
            of_image(relu_terms, i - 2, 1)
            of_image(window_products, i, 4)
            of_window(sum_terms, m - 1, 0, 1)
            of_image(fold_out, i)
            of_image(sum_products, i, 3)
            of_window(residual, m - 2, 1)
            of_image(fold_sum, i)
            of_image(sum_products, i, 4)
            of_image(window_products, i, 5)
            of_window(token_norms, m - 2, 0)
            of_window(regroup, m - 3, 0)
            of_window(root_ln, m - 1, 0, 0)
            of_window(transpose_back, m - 3, 1)

        def odd_step(i, m):
            of_window(load_again, m - 2, 2)
            of_window(load_again, m - 2, 3)
            of_image(load, i + 2)
            of_window(residual, m - 2, 3)
            of_window(token_norms, m - 2, 3)
            of_image(shifted_products, i - 2, 0)
            of_image(centre_square, i - 2)
            of_image(relu_terms, i - 2, 0)
            of_image(sum_products, i - 1, 5)
            of_image(vector_terms, i - 2, 0)
            of_window(root_ln, m - 1, 0, 1)
            of_window(quantise, m - 3, 0)
            of_image(shifted_products, i - 2, 1)
            of_image(centre_floor, i - 2)
            of_window(sum_terms, m - 1, 1, 0)
            of_image(squares, i)
            of_image(vector_terms, i - 2, 1)
            of_window(project, m - 3, 0)
            of_window(residual, m - 2, 2)
            of_image(relu_terms, i - 2, 1)
            of_image(window_sums, i - 1, 6)
            of_image(scaled_norms_first, i - 1)
            of_image(scaled_norms_second, i - 1)
            of_window(normalise, m - 3, 2)
            of_image(mean_square, i)
            of_window(sum_terms, m - 1, 2, 0)
            of_pair(rest_first, m - 1)
            of_image(row_scale, i)
            of_pair(rest_second, m - 1)
            of_pair(presum, m - 1)
            of_window(regroup, m - 3, 1)
            of_image(cubes, i)
            of_window(token_norms, m - 2, 1)
            of_image(transpose_in, i + 1)
            of_window(transpose_back, m - 3, 2)
            of_window(sum_terms, m - 1, 1, 1)
            of_image(fold_products, i, 0)
            of_image(fold, i, 0)
            of_image(fold_products, i, 1)
            of_image(fold, i, 1)
            of_image(window_products, i, 2)
            of_window(quantise, m - 3, 1)
            of_window(token_norms, m - 2, 2)
            of_image(window_products, i, 3)
            of_image(sum_products, i, 2)
            of_image(window_products, i, 4)
            of_window(root_ln, m - 1, 1, 0)
            of_window(project, m - 3, 1)
            of_window(root_ln, m - 1, 2, 0)
            of_window(sum_terms, m - 1, 2, 1)
            of_image(sum_products, i, 3)
            of_image(window_products, i, 5)
            of_image(fold_out, i)
            of_image(fold_sum, i)
            of_image(sum_products, i, 4)
            of_image(window_sums, i, 6)

        load(0)
        load(1)
        transpose_in(0)
        LAST = 10
        with tc.manual_schedule(engines={mybir.EngineType.Activation}):
            for i in range(IMAGES + LAST):
                (odd_step if i % 2 else even_step)(i, i // 2)
